import numpy as np
import ml_dtypes


def mxq(x, axis, fmt="e4m3"):
    dtype, down = {"e4m3": (ml_dtypes.float8_e4m3fn, 7), "e5m2": (ml_dtypes.float8_e5m2, 14)}[fmt]
    v = np.moveaxis(np.asarray(x, np.float32).astype(ml_dtypes.bfloat16).astype(np.float64), axis, -1)
    blocks = v.reshape(v.shape[:-1] + (-1, 32))
    amax = np.abs(blocks).max(-1, keepdims=True)
    byte = np.maximum(np.where(amax > 0, np.frexp(amax)[1] - 1 + 127, 0) - down, 1)
    scale = np.exp2(byte - 127.0)
    codes = (blocks / scale).astype(np.float32).astype(dtype).astype(np.float64)
    return np.moveaxis((codes * scale).reshape(v.shape), -1, axis)


WIDE = False


def mx_kscale(k):
    if not WIDE:
        return np.ones(k)
    levels = np.array([10, -10, 5, -5, 0])
    a = np.random.permutation(np.resize(levels, k // 512 * 4)).reshape(k // 512, 4)
    idx = np.arange(k)
    return np.exp2(a[idx // 512, idx % 128 // 32])


BF16 = ml_dtypes.bfloat16


def bf(x):
    return np.asarray(x, np.float32).astype(BF16)


def f64(x):
    return np.asarray(x).astype(np.float64)


B, T, U, De, Dd, V = 2, 128, 64, 512, 512, 256
F = De + Dd


def log_sigmoid(v):
    return -np.logaddexp(0.0, -v)


def log_softmax(v):
    z = v - v.max(-1, keepdims=True)
    return z - np.log(np.exp(z).sum(-1, keepdims=True))


def setup_inputs():
    s, r = mx_kscale(De), mx_kscale(Dd)
    return {"encoder_output": bf(np.random.standard_normal((B, T, De)) * s),
            "decoder_output": bf(np.random.standard_normal((B, U, Dd)) * r),
            "W_enc": bf(np.random.standard_normal((F, De)) * 0.7 / np.sqrt(De) / s[None, :]),
            "b_enc": bf(np.random.standard_normal(F) * 0.3),
            "W_dec": bf(np.random.standard_normal((F, Dd)) * 0.7 / np.sqrt(Dd) / r[None, :]),
            "b_dec": bf(np.random.standard_normal(F) * 0.3),
            "W_fc": bf(np.random.standard_normal((V, F)) * 1.5 / np.sqrt(F)),
            "b_fc": bf(np.random.standard_normal(V) * 0.3)}


def reference(encoder_output, decoder_output, W_enc, b_enc, W_dec, b_dec, W_fc, b_fc):
    enc = (mxq(f64(encoder_output), 2, "e4m3") @ mxq(f64(W_enc), 1, "e4m3").T) + f64(b_enc)
    dec = (mxq(f64(decoder_output), 2, "e4m3") @ mxq(f64(W_dec), 1, "e4m3").T) + f64(b_dec)
    combined = enc[:, :, None, :] + dec[:, None, :, :]
    h = np.tanh(combined)
    vocab_logits = (mxq(h, 3, "e4m3") @ mxq(f64(W_fc), 1, "e4m3").T) + f64(b_fc)
    blk_logit = vocab_logits[..., :1]
    log_blk = log_sigmoid(blk_logit)
    log_not_blk = log_sigmoid(-blk_logit)
    vocab_log_probs = log_not_blk + log_softmax(vocab_logits[..., 1:])
    return np.concatenate([log_blk, vocab_log_probs], axis=-1)

@@ -1,0 +1,296 @@
+from contextlib import ExitStack
+
+import concourse.mybir as mybir
+from concourse.masks import make_identity
+
+F32 = mybir.dt.float32
+BF16 = mybir.dt.bfloat16
+U32 = mybir.dt.uint32
+U8 = mybir.dt.uint8
+FP8X4 = mybir.dt.float8_e4m3fn_x4
+ACT = mybir.ActivationFunctionType
+ALU = mybir.AluOpType
+AX = mybir.AxisListType
+
+P = 128
+B, T, U, K1, F, V = 2, 128, 64, 512, 1024, 256
+NCH = 8
+UPU = 4
+NUNITS = B * U // UPU
+BATCH_UNITS = [11, 11, 8, 2]
+PIN = False
+
+FLOPS = 2 * (B * T * K1 * F + B * U * K1 * F + B * T * U * F * V)
+
+
+def tile_jointnet_t_kernel(
+    tc, encoder_output, decoder_output, W_enc, b_enc, W_dec, b_dec, W_fc, b_fc, out
+):
+    nc = tc.nc
+    with ExitStack() as ctx:
+        if PIN:
+            ctx.enter_context(tc.manual_schedule())
+        const = ctx.enter_context(tc.tile_pool(name="const", bufs=1))
+        ps_tr = ctx.enter_context(tc.psum_pool(name="ps_tr", bufs=2))
+        ps_s1 = ctx.enter_context(tc.psum_pool(name="ps_s1", bufs=2))
+        ps_lg = ctx.enter_context(tc.psum_pool(name="ps_lg", bufs=4))
+        hp_pool = ctx.enter_context(tc.tile_pool(name="hp", bufs=3))
+        gr_pool = ctx.enter_context(tc.tile_pool(name="gr", bufs=2))
+        cd_pool = ctx.enter_context(tc.tile_pool(name="cd", bufs=3))
+        l_pool = ctx.enter_context(tc.tile_pool(name="lp", bufs=2))
+        small = ctx.enter_context(tc.tile_pool(name="small", bufs=2))
+        junk_pool = ctx.enter_context(tc.tile_pool(name="junk", bufs=2))
+
+        benc_bf = const.tile([P, NCH], BF16, name="benc_bf")
+        bdec_bf = const.tile([P, NCH], BF16, name="bdec_bf")
+        bfc_bf = const.tile([P, V], BF16, name="bfc_bf")
+        with nc.allow_non_contiguous_dma(reason="bias vectors, 8-byte runs"):
+            nc.scalar.dma_start(
+                out=benc_bf[:].rearrange("p (g j) -> p g j", g=2),
+                in_=b_enc.rearrange("(g p j) -> p g j", g=2, j=4),
+            )
+            nc.scalar.dma_start(
+                out=bdec_bf[:].rearrange("p (g j) -> p g j", g=2),
+                in_=b_dec.rearrange("(g p j) -> p g j", g=2, j=4),
+            )
+        enc_sb = const.tile([P, B, K1], BF16, name="enc_sb")
+        nc.sync.dma_start(out=enc_sb[:], in_=encoder_output.rearrange("b t k -> t b k"))
+        dec_sb = const.tile([P, K1], BF16, name="dec_sb")
+        nc.sync.dma_start(out=dec_sb[:], in_=decoder_output.rearrange("b u k -> (b u) k"))
+        wenc_sb = const.tile([P, NCH, K1], BF16, name="wenc_sb")
+        wdec_sb = const.tile([P, NCH, K1], BF16, name="wdec_sb")
+        for g in range(2):
+            for w_sb, w in ((wenc_sb, W_enc), (wdec_sb, W_dec)):
+                nc.sync.dma_start(
+                    out=w_sb[:, 4 * g : 4 * g + 4, :],
+                    in_=w[512 * g : 512 * g + 512, :].rearrange("(p j) k -> p j k", j=4),
+                )
+        wfc_sb = const.tile([P, 2, F], BF16, name="wfc_sb")
+        nc.sync.dma_start(out=wfc_sb[:], in_=W_fc.rearrange("(h v) k -> v h k", h=2))
+        nc.scalar.dma_start(out=bfc_bf[:], in_=b_fc.partition_broadcast(P))
+
+        ident = const.tile([P, P], F32, name="ident")
+        make_identity(nc, ident[:])
+
+        benc = const.tile([P, NCH], F32, name="benc")
+        bdec = const.tile([P, NCH], F32, name="bdec")
+        bfc = const.tile([P, V], F32, name="bfc")
+        nc.vector.tensor_copy(out=benc[:], in_=benc_bf[:])
+        nc.vector.tensor_copy(out=bdec[:], in_=bdec_bf[:])
+
+        xg = const.tile([P, 3 * 512], BF16, name="xg", align_bytes=64)
+        xc = const.tile([P, 3 * P], U32, name="xc", align_bytes=64)
+        xs = const.tile([P, 3 * P], U8, name="xs", align_bytes=64)
+        weg = const.tile([P, NCH * 512], BF16, name="weg", align_bytes=64)
+        wec = const.tile([P, NCH * P], U32, name="wec", align_bytes=64)
+        wes = const.tile([P, NCH * P], U8, name="wes", align_bytes=64)
+        wdg = const.tile([P, NCH * 512], BF16, name="wdg", align_bytes=64)
+        wdc = const.tile([P, NCH * P], U32, name="wdc", align_bytes=64)
+        wds = const.tile([P, NCH * P], U8, name="wds", align_bytes=64)
+        wfg = const.tile([P, 4 * 512], BF16, name="wfg", align_bytes=64)
+        wfc = const.tile([P, 4 * P], U32, name="wfc", align_bytes=64)
+        wfs = const.tile([P, 4 * P], U8, name="wfs", align_bytes=64)
+
+        def halves(rows):
+            w32 = rows.bitcast(F32)
+            return [w32[:, 0:P], w32[:, P : 2 * P]]
+
+        def transpose_tiles(views, dst, on_scalar):
+            n = len(views)
+            tr = ps_tr.tile([P, 2, 2, P], F32, name="tr")
+            for s in range(n):
+                for u in range(2):
+                    nc.tensor.transpose(tr[:, s, u, :], views[s][u], ident[:])
+            o = dst.bitcast(F32).rearrange("p (s r u) -> p s r u", s=n, u=2)
+            i = tr[:, 0:n, :, :].rearrange("p s u r -> p s r u")
+            if on_scalar:
+                nc.scalar.copy(out=o, in_=i)
+            else:
+                nc.vector.tensor_copy(out=o, in_=i)
+
+        def quantise(grouped, codes, scales, first, count):
+            nc.vector.quantize_mx(
+                out=codes[:, first * P : (first + count) * P].bitcast(FP8X4),
+                scales=scales[:, first * P : (first + count) * P],
+                in_=grouped[:, first * 512 : (first + count) * 512],
+            )
+
+        transpose_tiles([halves(enc_sb[:, 0, :]), halves(enc_sb[:, 1, :])], xg[:, 0:1024], True)
+        transpose_tiles([halves(dec_sb[:, :])], xg[:, 1024:1536], False)
+        quantise(xg, xc, xs, 0, 2)
+        quantise(xg, xc, xs, 2, 1)
+
+        encB = const.tile([P, NCH, B * T], F32, name="encB")
+        decB = const.tile([P, NCH, B * U], F32, name="decB")
+        for g in range(2):
+            for w_sb, grouped, on_scalar in ((wenc_sb, weg, True), (wdec_sb, wdg, False)):
+                for c in (4 * g, 4 * g + 2):
+                    transpose_tiles(
+                        [halves(w_sb[:, c, :]), halves(w_sb[:, c + 1, :])],
+                        grouped[:, c * 512 : (c + 2) * 512],
+                        on_scalar,
+                    )
+            quantise(weg, wec, wes, 4 * g, 4)
+            quantise(wdg, wdc, wds, 4 * g, 4)
+            for c in range(4 * g, 4 * g + 4):
+                cols = slice(c * P, (c + 1) * P)
+                s1 = ps_s1.tile([P, 384], F32, name="s1")
+                nc.tensor.matmul_mx(
+                    out=s1[:, 0:256],
+                    lhsT=wec[:, cols].bitcast(FP8X4),
+                    lhsT_scale=wes[:, cols],
+                    rhs=xc[:, 0:256].bitcast(FP8X4),
+                    rhs_scale=xs[:, 0:256],
+                    start=True,
+                    stop=True,
+                )
+                nc.tensor.matmul_mx(
+                    out=s1[:, 256:384],
+                    lhsT=wdc[:, cols].bitcast(FP8X4),
+                    lhsT_scale=wds[:, cols],
+                    rhs=xc[:, 256:384].bitcast(FP8X4),
+                    rhs_scale=xs[:, 256:384],
+                    start=True,
+                    stop=True,
+                )
+                if c % 2 == 0:
+                    nc.vector.tensor_scalar(
+                        out=encB[:, c, :], in0=s1[:, 0:256], scalar1=benc[:, c : c + 1],
+                        scalar2=None, op0=ALU.add,
+                    )
+                    nc.vector.tensor_scalar(
+                        out=decB[:, c, :], in0=s1[:, 256:384], scalar1=bdec[:, c : c + 1],
+                        scalar2=None, op0=ALU.add,
+                    )
+                else:
+                    nc.scalar.activation(
+                        out=encB[:, c, :], in_=s1[:, 0:256], func=ACT.Identity,
+                        bias=benc[:, c : c + 1], scale=1.0,
+                    )
+                    nc.scalar.activation(
+                        out=decB[:, c, :], in_=s1[:, 256:384], func=ACT.Identity,
+                        bias=bdec[:, c : c + 1], scale=1.0,
+                    )
+
+        for g in range(2):
+            views = []
+            for h in range(2):
+                w32 = wfc_sb[:, h, :].bitcast(F32).rearrange("p (g w u) -> p g w u", g=2, u=2)
+                views.append([w32[:, g, :, 0], w32[:, g, :, 1]])
+            transpose_tiles(views, wfg[:, g * 1024 : (g + 1) * 1024], False)
+        quantise(wfg, wfc, wfs, 0, 4)
+        nc.vector.tensor_copy(out=bfc[:], in_=bfc_bf[:])
+
+        unit = 0
+        for n_units in BATCH_UNITS:
+            n = n_units * UPU
+            L = l_pool.tile([P, n, V], F32, name="L")
+            negm = small.tile([P, n], F32, name="negm")
+            ssum = small.tile([P, n], F32, name="ssum")
+            first_unit = unit
+            for iu in range(n_units):
+                b = unit // (U // UPU)
+                u0 = (unit % (U // UPU)) * UPU
+                k0 = iu * UPU
+                hP = hp_pool.tile([P, 4, 2 * UPU * P], BF16, name="hP")
+                grouped = gr_pool.tile([P, 8 * UPU * P], BF16, name="grouped", align_bytes=64)
+                words = cd_pool.tile([P, 2 * UPU * P], U32, name="words", align_bytes=64)
+                planes = cd_pool.tile([P, 2 * UPU * P], U8, name="planes", align_bytes=64)
+                for h in range(2):
+                    for g in range(2):
+                        for j in range(4):
+                            for uu in (2 * h, 2 * h + 1):
+                                x = uu * 2 + g
+                                nc.scalar.activation(
+                                    out=hP[:, j, x * P : (x + 1) * P],
+                                    in_=encB[:, 4 * g + j, b * T : (b + 1) * T],
+                                    func=ACT.Tanh,
+                                    bias=decB[:, 4 * g + j, b * U + u0 + uu : b * U + u0 + uu + 1],
+                                    scale=1.0,
+                                )
+                    nc.vector.tensor_copy(
+                        out=grouped[:, 2048 * h : 2048 * h + 2048].rearrange(
+                            "p (c i j) -> p c j i", i=4, j=4
+                        ),
+                        in_=hP[:, :, 512 * h : 512 * h + 512].rearrange("p j (c i) -> p c j i", i=4),
+                    )
+                for h in range(2):
+                    nc.vector.quantize_mx(
+                        out=words[:, 512 * h : 512 * h + 512].bitcast(FP8X4),
+                        scales=planes[:, 512 * h : 512 * h + 512],
+                        in_=grouped[:, 2048 * h : 2048 * h + 2048],
+                    )
+                for h in range(2):
+                    lg = ps_lg.tile([P, 2, V], F32, name="lg")
+                    for q in range(2):
+                        for g in range(2):
+                            x = (2 * h + q) * 2 + g
+                            nc.tensor.matmul_mx(
+                                out=lg[:, q, :],
+                                lhsT=words[:, x * P : (x + 1) * P].bitcast(FP8X4),
+                                lhsT_scale=planes[:, x * P : (x + 1) * P],
+                                rhs=wfc[:, g * V : (g + 1) * V].bitcast(FP8X4),
+                                rhs_scale=wfs[:, g * V : (g + 1) * V],
+                                start=(g == 0),
+                                stop=(g == 1),
+                            )
+                    nc.vector.tensor_tensor(
+                        out=L[:, k0 + 2 * h : k0 + 2 * h + 2, :],
+                        in0=lg[:],
+                        in1=bfc[:].unsqueeze(1).to_broadcast([P, 2, V]),
+                        op=ALU.add,
+                    )
+                nc.vector.tensor_reduce(
+                    out=negm[:, k0 : k0 + UPU],
+                    in_=L[:, k0 : k0 + UPU, 1:V],
+                    axis=AX.X,
+                    op=ALU.max,
+                    negate=True,
+                )
+                for q in range(UPU):
+                    junk = junk_pool.tile([P, V], BF16, name="junk")
+                    nc.scalar.activation(
+                        out=junk[:, 1:V],
+                        in_=L[:, k0 + q, 1:V],
+                        func=ACT.Exp,
+                        bias=negm[:, k0 + q : k0 + q + 1],
+                        scale=1.0,
+                        accum_out=ssum[:, k0 + q : k0 + q + 1],
+                    )
+                unit += 1
+
+            l0 = L[:, :, 0]
+            nab = small.tile([P, n], F32, name="nab")
+            nc.vector.scalar_tensor_tensor(
+                out=nab[:], in0=l0, scalar=-1.0, in1=l0, op0=ALU.mult, op1=ALU.min
+            )
+            ex = small.tile([P, n], F32, name="ex")
+            nc.scalar.activation(out=ex[:], in_=nab[:], func=ACT.Exp)
+            sq = small.tile([P, 2, n], F32, name="sq")
+            nc.vector.tensor_scalar_add(out=sq[:, 0, :], in0=ex[:], scalar1=1.0)
+            nc.vector.tensor_tensor(out=sq[:, 1, :], in0=sq[:, 0, :], in1=ssum[:], op=ALU.mult)
+            lns = small.tile([P, 2, n], F32, name="lns")
+            nc.scalar.activation(out=lns[:], in_=sq[:], func=ACT.Ln)
+            t1 = small.tile([P, n], F32, name="t1")
+            nc.vector.scalar_tensor_tensor(
+                out=t1[:], in0=l0, scalar=0.0, in1=negm[:], op0=ALU.max, op1=ALU.subtract
+            )
+            cc = small.tile([P, n], F32, name="cc")
+            nc.vector.tensor_tensor(out=cc[:], in0=t1[:], in1=lns[:, 1, :], op=ALU.add)
+            nc.vector.scalar_tensor_tensor(
+                out=l0, in0=l0, scalar=0.0, in1=lns[:, 0, :], op0=ALU.min, op1=ALU.subtract
+            )
+            for iu in range(n_units):
+                un = first_unit + iu
+                b = un // (U // UPU)
+                u0 = (un % (U // UPU)) * UPU
+                k0 = iu * UPU
+                for q in range(UPU):
+                    nc.vector.tensor_scalar(
+                        out=L[:, k0 + q, 1:V],
+                        in0=L[:, k0 + q, 1:V],
+                        scalar1=cc[:, k0 + q : k0 + q + 1],
+                        scalar2=None,
+                        op0=ALU.subtract,
+                    )
+                nc.sync.dma_start(out=out[b, :, u0 : u0 + UPU, :], in_=L[:, k0 : k0 + UPU, :])

@@ -15,10 +15,11 @@ AX = mybir.AxisListType
 P = 128
 B, T, U, K1, F, V = 2, 128, 64, 512, 1024, 256
 NCH = 8
-UPU = 4
-NUNITS = B * U // UPU
-BATCH_UNITS = [11, 11, 8, 2]
-PIN = False
+HU = B * U // 2
+BATCH_HU = [38, 20, 6]
+LEAD = 3
+PIN = True
+V3_TAIL = "VAVG"
 
 FLOPS = 2 * (B * T * K1 * F + B * U * K1 * F + B * T * U * F * V)
 
@@ -31,108 +32,104 @@ def tile_jointnet_t_kernel(
         if PIN:
             ctx.enter_context(tc.manual_schedule())
         const = ctx.enter_context(tc.tile_pool(name="const", bufs=1))
-        ps_tr = ctx.enter_context(tc.psum_pool(name="ps_tr", bufs=2))
+        ps_tr = ctx.enter_context(tc.psum_pool(name="ps_tr", bufs=3))
         ps_s1 = ctx.enter_context(tc.psum_pool(name="ps_s1", bufs=2))
-        ps_lg = ctx.enter_context(tc.psum_pool(name="ps_lg", bufs=4))
-        hp_pool = ctx.enter_context(tc.tile_pool(name="hp", bufs=3))
-        gr_pool = ctx.enter_context(tc.tile_pool(name="gr", bufs=2))
+        ps_lg = ctx.enter_context(tc.psum_pool(name="ps_lg", bufs=3))
+        hp_pool = ctx.enter_context(tc.tile_pool(name="hp", bufs=LEAD + 1))
+        gr_pool = ctx.enter_context(tc.tile_pool(name="gr", bufs=3))
         cd_pool = ctx.enter_context(tc.tile_pool(name="cd", bufs=3))
-        l_pool = ctx.enter_context(tc.tile_pool(name="lp", bufs=2))
         small = ctx.enter_context(tc.tile_pool(name="small", bufs=2))
         junk_pool = ctx.enter_context(tc.tile_pool(name="junk", bufs=2))
+        l_first = ctx.enter_context(tc.tile_pool(name="l_first", bufs=1))
 
-        benc_bf = const.tile([P, NCH], BF16, name="benc_bf")
-        bdec_bf = const.tile([P, NCH], BF16, name="bdec_bf")
-        bfc_bf = const.tile([P, V], BF16, name="bfc_bf")
-        with nc.allow_non_contiguous_dma(reason="bias vectors, 8-byte runs"):
-            nc.scalar.dma_start(
-                out=benc_bf[:].rearrange("p (g j) -> p g j", g=2),
-                in_=b_enc.rearrange("(g p j) -> p g j", g=2, j=4),
-            )
-            nc.scalar.dma_start(
-                out=bdec_bf[:].rearrange("p (g j) -> p g j", g=2),
-                in_=b_dec.rearrange("(g p j) -> p g j", g=2, j=4),
-            )
-        enc_sb = const.tile([P, B, K1], BF16, name="enc_sb")
-        nc.sync.dma_start(out=enc_sb[:], in_=encoder_output.rearrange("b t k -> t b k"))
-        dec_sb = const.tile([P, K1], BF16, name="dec_sb")
-        nc.sync.dma_start(out=dec_sb[:], in_=decoder_output.rearrange("b u k -> (b u) k"))
-        wenc_sb = const.tile([P, NCH, K1], BF16, name="wenc_sb")
-        wdec_sb = const.tile([P, NCH, K1], BF16, name="wdec_sb")
-        for g in range(2):
-            for w_sb, w in ((wenc_sb, W_enc), (wdec_sb, W_dec)):
-                nc.sync.dma_start(
-                    out=w_sb[:, 4 * g : 4 * g + 4, :],
-                    in_=w[512 * g : 512 * g + 512, :].rearrange("(p j) k -> p j k", j=4),
-                )
-        wfc_sb = const.tile([P, 2, F], BF16, name="wfc_sb")
-        nc.sync.dma_start(out=wfc_sb[:], in_=W_fc.rearrange("(h v) k -> v h k", h=2))
-        nc.scalar.dma_start(out=bfc_bf[:], in_=b_fc.partition_broadcast(P))
-
-        ident = const.tile([P, P], F32, name="ident")
-        make_identity(nc, ident[:])
-
+        xc = const.tile([P, 3 * P], U32, name="xc", align_bytes=64)
+        xs = const.tile([P, 3 * P], U8, name="xs", align_bytes=64)
+        wec = const.tile([P, NCH * P], U32, name="wec", align_bytes=64)
+        wes = const.tile([P, NCH * P], U8, name="wes", align_bytes=64)
+        wdc = const.tile([P, NCH * P], U32, name="wdc", align_bytes=64)
+        wds = const.tile([P, NCH * P], U8, name="wds", align_bytes=64)
+        wfc = const.tile([P, 4 * P], U32, name="wfc", align_bytes=64)
+        wfs = const.tile([P, 4 * P], U8, name="wfs", align_bytes=64)
+        encB = const.tile([P, NCH, B * T], F32, name="encB")
+        decB = const.tile([P, NCH, B * U], F32, name="decB")
         benc = const.tile([P, NCH], F32, name="benc")
         bdec = const.tile([P, NCH], F32, name="bdec")
         bfc = const.tile([P, V], F32, name="bfc")
-        nc.vector.tensor_copy(out=benc[:], in_=benc_bf[:])
-        nc.vector.tensor_copy(out=bdec[:], in_=bdec_bf[:])
+        ident = const.tile([P, P], F32, name="ident")
+        warm_in = const.tile([P, 1], F32, name="warm_in")
+        warm_out = const.tile([P, 1], F32, name="warm_out")
 
-        xg = const.tile([P, 3 * 512], BF16, name="xg", align_bytes=64)
-        xc = const.tile([P, 3 * P], U32, name="xc", align_bytes=64)
-        xs = const.tile([P, 3 * P], U8, name="xs", align_bytes=64)
-        weg = const.tile([P, NCH * 512], BF16, name="weg", align_bytes=64)
-        wec = const.tile([P, NCH * P], U32, name="wec", align_bytes=64)
-        wes = const.tile([P, NCH * P], U8, name="wes", align_bytes=64)
-        wdg = const.tile([P, NCH * 512], BF16, name="wdg", align_bytes=64)
-        wdc = const.tile([P, NCH * P], U32, name="wdc", align_bytes=64)
-        wds = const.tile([P, NCH * P], U8, name="wds", align_bytes=64)
-        wfg = const.tile([P, 4 * 512], BF16, name="wfg", align_bytes=64)
-        wfc = const.tile([P, 4 * P], U32, name="wfc", align_bytes=64)
-        wfs = const.tile([P, 4 * P], U8, name="wfs", align_bytes=64)
+        with tc.tile_pool(name="stage", bufs=1) as stage:
+            benc_bf = stage.tile([P, NCH], BF16, name="benc_bf")
+            bdec_bf = stage.tile([P, NCH], BF16, name="bdec_bf")
+            bfc_bf = stage.tile([P, V], BF16, name="bfc_bf")
+            with nc.allow_non_contiguous_dma(reason="bias vectors, 8-byte runs"):
+                nc.scalar.dma_start(
+                    out=benc_bf[:].rearrange("p (g j) -> p g j", g=2),
+                    in_=b_enc.rearrange("(g p j) -> p g j", g=2, j=4),
+                )
+                nc.scalar.dma_start(
+                    out=bdec_bf[:].rearrange("p (g j) -> p g j", g=2),
+                    in_=b_dec.rearrange("(g p j) -> p g j", g=2, j=4),
+                )
+            enc_sb = stage.tile([P, B, K1], BF16, name="enc_sb")
+            nc.sync.dma_start(out=enc_sb[:], in_=encoder_output.rearrange("b t k -> t b k"))
+            dec_sb = stage.tile([P, K1], BF16, name="dec_sb")
+            nc.sync.dma_start(out=dec_sb[:], in_=decoder_output.rearrange("b u k -> (b u) k"))
+            wenc_sb = stage.tile([P, NCH, K1], BF16, name="wenc_sb")
+            wdec_sb = stage.tile([P, NCH, K1], BF16, name="wdec_sb")
+            for g in range(2):
+                for w_sb, w in ((wenc_sb, W_enc), (wdec_sb, W_dec)):
+                    nc.sync.dma_start(
+                        out=w_sb[:, 4 * g : 4 * g + 4, :],
+                        in_=w[512 * g : 512 * g + 512, :].rearrange("(p j) k -> p j k", j=4),
+                    )
+            wfc_sb = stage.tile([P, 2, F], BF16, name="wfc_sb")
+            nc.sync.dma_start(out=wfc_sb[:], in_=W_fc.rearrange("(h v) k -> v h k", h=2))
+            nc.sync.dma_start(out=bfc_bf[:], in_=b_fc.partition_broadcast(P))
 
-        def halves(rows):
-            w32 = rows.bitcast(F32)
-            return [w32[:, 0:P], w32[:, P : 2 * P]]
+            make_identity(nc, ident[:])
+            nc.vector.memset(warm_in[:], 0.0)
+            nc.scalar.activation(out=warm_out[:], in_=warm_in[:], func=ACT.Tanh)
 
-        def transpose_tiles(views, dst, on_scalar):
-            n = len(views)
-            tr = ps_tr.tile([P, 2, 2, P], F32, name="tr")
-            for s in range(n):
-                for u in range(2):
-                    nc.tensor.transpose(tr[:, s, u, :], views[s][u], ident[:])
-            o = dst.bitcast(F32).rearrange("p (s r u) -> p s r u", s=n, u=2)
-            i = tr[:, 0:n, :, :].rearrange("p s u r -> p s r u")
-            if on_scalar:
-                nc.scalar.copy(out=o, in_=i)
-            else:
-                nc.vector.tensor_copy(out=o, in_=i)
+            xg = stage.tile([P, 3 * 512], BF16, name="xg", align_bytes=64)
+            weg = stage.tile([P, NCH * 512], BF16, name="weg", align_bytes=64)
+            wdg = stage.tile([P, NCH * 512], BF16, name="wdg", align_bytes=64)
+            wfg = stage.tile([P, 4 * 512], BF16, name="wfg", align_bytes=64)
 
-        def quantise(grouped, codes, scales, first, count):
-            nc.vector.quantize_mx(
-                out=codes[:, first * P : (first + count) * P].bitcast(FP8X4),
-                scales=scales[:, first * P : (first + count) * P],
-                in_=grouped[:, first * 512 : (first + count) * 512],
-            )
+            def halves(rows):
+                w32 = rows.bitcast(F32)
+                return [w32[:, 0:P], w32[:, P : 2 * P]]
 
-        transpose_tiles([halves(enc_sb[:, 0, :]), halves(enc_sb[:, 1, :])], xg[:, 0:1024], True)
-        transpose_tiles([halves(dec_sb[:, :])], xg[:, 1024:1536], False)
-        quantise(xg, xc, xs, 0, 2)
-        quantise(xg, xc, xs, 2, 1)
+            def transpose_tiles(views, dst, on_scalar):
+                n = len(views)
+                tr = ps_tr.tile([P, 2, 2, P], F32, name="tr")
+                for s in range(n):
+                    for u in range(2):
+                        nc.tensor.transpose(tr[:, s, u, :], views[s][u], ident[:])
+                o = dst.bitcast(F32).rearrange("p (s r u) -> p s r u", s=n, u=2)
+                i = tr[:, 0:n, :, :].rearrange("p s u r -> p s r u")
+                if on_scalar:
+                    nc.scalar.copy(out=o, in_=i)
+                else:
+                    nc.vector.tensor_copy(out=o, in_=i)
 
-        encB = const.tile([P, NCH, B * T], F32, name="encB")
-        decB = const.tile([P, NCH, B * U], F32, name="decB")
-        for g in range(2):
-            for w_sb, grouped, on_scalar in ((wenc_sb, weg, True), (wdec_sb, wdg, False)):
+            def transpose_weights(w_sb, grouped, g, on_scalar):
                 for c in (4 * g, 4 * g + 2):
                     transpose_tiles(
                         [halves(w_sb[:, c, :]), halves(w_sb[:, c + 1, :])],
                         grouped[:, c * 512 : (c + 2) * 512],
                         on_scalar,
                     )
-            quantise(weg, wec, wes, 4 * g, 4)
-            quantise(wdg, wdc, wds, 4 * g, 4)
-            for c in range(4 * g, 4 * g + 4):
+
+            def quantise(grouped, codes, scales, first, count):
+                nc.vector.quantize_mx(
+                    out=codes[:, first * P : (first + count) * P].bitcast(FP8X4),
+                    scales=scales[:, first * P : (first + count) * P],
+                    in_=grouped[:, first * 512 : (first + count) * 512],
+                )
+
+            def input_matmuls(c, on_scalar):
                 cols = slice(c * P, (c + 1) * P)
                 s1 = ps_s1.tile([P, 384], F32, name="s1")
                 nc.tensor.matmul_mx(
@@ -153,144 +150,247 @@ def tile_jointnet_t_kernel(
                     start=True,
                     stop=True,
                 )
-                if c % 2 == 0:
-                    nc.vector.tensor_scalar(
-                        out=encB[:, c, :], in0=s1[:, 0:256], scalar1=benc[:, c : c + 1],
-                        scalar2=None, op0=ALU.add,
-                    )
-                    nc.vector.tensor_scalar(
-                        out=decB[:, c, :], in0=s1[:, 256:384], scalar1=bdec[:, c : c + 1],
-                        scalar2=None, op0=ALU.add,
-                    )
-                else:
-                    nc.scalar.activation(
-                        out=encB[:, c, :], in_=s1[:, 0:256], func=ACT.Identity,
-                        bias=benc[:, c : c + 1], scale=1.0,
-                    )
-                    nc.scalar.activation(
-                        out=decB[:, c, :], in_=s1[:, 256:384], func=ACT.Identity,
-                        bias=bdec[:, c : c + 1], scale=1.0,
-                    )
+                for dst, src, bias in (
+                    (decB[:, c, :], s1[:, 256:384], bdec[:, c : c + 1]),
+                    (encB[:, c, :], s1[:, 0:256], benc[:, c : c + 1]),
+                ):
+                    if on_scalar:
+                        nc.scalar.activation(out=dst, in_=src, func=ACT.Identity, bias=bias, scale=1.0)
+                    else:
+                        nc.vector.tensor_scalar(
+                            out=dst, in0=src, scalar1=bias, scalar2=None, op0=ALU.add
+                        )
 
-        for g in range(2):
-            views = []
-            for h in range(2):
-                w32 = wfc_sb[:, h, :].bitcast(F32).rearrange("p (g w u) -> p g w u", g=2, u=2)
-                views.append([w32[:, g, :, 0], w32[:, g, :, 1]])
-            transpose_tiles(views, wfg[:, g * 1024 : (g + 1) * 1024], False)
-        quantise(wfg, wfc, wfs, 0, 4)
-        nc.vector.tensor_copy(out=bfc[:], in_=bfc_bf[:])
+            transpose_tiles(
+                [halves(enc_sb[:, 0, :]), halves(enc_sb[:, 1, :])], xg[:, 0:1024], True
+            )
+            transpose_tiles([halves(dec_sb[:, :])], xg[:, 1024:1536], False)
+            nc.vector.tensor_copy(out=benc[:], in_=benc_bf[:])
+            nc.vector.tensor_copy(out=bdec[:], in_=bdec_bf[:])
+            quantise(xg, xc, xs, 0, 2)
+            quantise(xg, xc, xs, 2, 1)
+            transpose_weights(wenc_sb, weg, 0, True)
+            transpose_weights(wdec_sb, wdg, 0, False)
+            quantise(weg, wec, wes, 0, 4)
+            quantise(wdg, wdc, wds, 0, 4)
+            transpose_weights(wenc_sb, weg, 1, True)
+            for c in range(4):
+                input_matmuls(c, c % 2 == 1)
+            transpose_weights(wdec_sb, wdg, 1, False)
+            quantise(weg, wec, wes, 4, 4)
+            quantise(wdg, wdc, wds, 4, 4)
+            for c in range(4, 8):
+                input_matmuls(c, False)
+            for g in range(2):
+                views = []
+                for h in range(2):
+                    w32 = wfc_sb[:, h, :].bitcast(F32).rearrange("p (g w u) -> p g w u", g=2, u=2)
+                    views.append([w32[:, g, :, 0], w32[:, g, :, 1]])
+                transpose_tiles(views, wfg[:, g * 1024 : (g + 1) * 1024], False)
+            quantise(wfg, wfc, wfs, 0, 4)
+            nc.vector.tensor_copy(out=bfc[:], in_=bfc_bf[:])
 
-        unit = 0
-        for n_units in BATCH_UNITS:
-            n = n_units * UPU
-            L = l_pool.tile([P, n, V], F32, name="L")
-            negm = small.tile([P, n], F32, name="negm")
-            ssum = small.tile([P, n], F32, name="ssum")
-            first_unit = unit
-            for iu in range(n_units):
-                b = unit // (U // UPU)
-                u0 = (unit % (U // UPU)) * UPU
-                k0 = iu * UPU
-                hP = hp_pool.tile([P, 4, 2 * UPU * P], BF16, name="hP")
-                grouped = gr_pool.tile([P, 8 * UPU * P], BF16, name="grouped", align_bytes=64)
-                words = cd_pool.tile([P, 2 * UPU * P], U32, name="words", align_bytes=64)
-                planes = cd_pool.tile([P, 2 * UPU * P], U8, name="planes", align_bytes=64)
-                for h in range(2):
-                    for g in range(2):
-                        for j in range(4):
-                            for uu in (2 * h, 2 * h + 1):
-                                x = uu * 2 + g
-                                nc.scalar.activation(
-                                    out=hP[:, j, x * P : (x + 1) * P],
-                                    in_=encB[:, 4 * g + j, b * T : (b + 1) * T],
-                                    func=ACT.Tanh,
-                                    bias=decB[:, 4 * g + j, b * U + u0 + uu : b * U + u0 + uu + 1],
-                                    scale=1.0,
-                                )
-                    nc.vector.tensor_copy(
-                        out=grouped[:, 2048 * h : 2048 * h + 2048].rearrange(
-                            "p (c i j) -> p c j i", i=4, j=4
-                        ),
-                        in_=hP[:, :, 512 * h : 512 * h + 512].rearrange("p j (c i) -> p c j i", i=4),
-                    )
-                for h in range(2):
-                    nc.vector.quantize_mx(
-                        out=words[:, 512 * h : 512 * h + 512].bitcast(FP8X4),
-                        scales=planes[:, 512 * h : 512 * h + 512],
-                        in_=grouped[:, 2048 * h : 2048 * h + 2048],
-                    )
-                for h in range(2):
-                    lg = ps_lg.tile([P, 2, V], F32, name="lg")
-                    for q in range(2):
-                        for g in range(2):
-                            x = (2 * h + q) * 2 + g
-                            nc.tensor.matmul_mx(
-                                out=lg[:, q, :],
-                                lhsT=words[:, x * P : (x + 1) * P].bitcast(FP8X4),
-                                lhsT_scale=planes[:, x * P : (x + 1) * P],
-                                rhs=wfc[:, g * V : (g + 1) * V].bitcast(FP8X4),
-                                rhs_scale=wfs[:, g * V : (g + 1) * V],
-                                start=(g == 0),
-                                stop=(g == 1),
-                            )
-                    nc.vector.tensor_tensor(
-                        out=L[:, k0 + 2 * h : k0 + 2 * h + 2, :],
-                        in0=lg[:],
-                        in1=bfc[:].unsqueeze(1).to_broadcast([P, 2, V]),
-                        op=ALU.add,
-                    )
-                nc.vector.tensor_reduce(
-                    out=negm[:, k0 : k0 + UPU],
-                    in_=L[:, k0 : k0 + UPU, 1:V],
-                    axis=AX.X,
-                    op=ALU.max,
-                    negate=True,
-                )
-                for q in range(UPU):
-                    junk = junk_pool.tile([P, V], BF16, name="junk")
+        l_rest = ctx.enter_context(tc.tile_pool(name="l_rest", bufs=1))
+
+        batch_of = []
+        first_of = []
+        for bi, n_hu in enumerate(BATCH_HU):
+            first_of.append(len(batch_of))
+            batch_of.extend([bi] * n_hu)
+        last_of = [first_of[bi] + BATCH_HU[bi] - 1 for bi in range(len(BATCH_HU))]
+        hPs, groupeds, codes, lgs = {}, {}, {}, {}
+        Ls, negms, ssums, misc = {}, {}, {}, {}
+
+        def tanh_part(s, g):
+            b = s // (HU // B)
+            u0 = (s % (HU // B)) * 2
+            if g == 0:
+                hPs[s] = hp_pool.tile([P, 4, 4 * P], BF16, name="hP")
+            for j in range(4):
+                for q in range(2):
+                    x = q * 2 + g
                     nc.scalar.activation(
-                        out=junk[:, 1:V],
-                        in_=L[:, k0 + q, 1:V],
-                        func=ACT.Exp,
-                        bias=negm[:, k0 + q : k0 + q + 1],
+                        out=hPs[s][:, j, x * P : (x + 1) * P],
+                        in_=encB[:, 4 * g + j, b * T : (b + 1) * T],
+                        func=ACT.Tanh,
+                        bias=decB[:, 4 * g + j, b * U + u0 + q : b * U + u0 + q + 1],
                         scale=1.0,
-                        accum_out=ssum[:, k0 + q : k0 + q + 1],
                     )
-                unit += 1
 
-            l0 = L[:, :, 0]
+        def regroup(s):
+            groupeds[s] = gr_pool.tile([P, 16 * P], BF16, name="grouped", align_bytes=64)
+            nc.vector.tensor_copy(
+                out=groupeds[s][:].rearrange("p (c i j) -> p c j i", i=4, j=4),
+                in_=hPs[s][:].rearrange("p j (c i) -> p c j i", i=4),
+            )
+
+        def quantise_h(s):
+            words = cd_pool.tile([P, 4 * P], U32, name="words", align_bytes=64)
+            planes = cd_pool.tile([P, 4 * P], U8, name="planes", align_bytes=64)
+            codes[s] = (words, planes)
+            nc.vector.quantize_mx(
+                out=words[:].bitcast(FP8X4), scales=planes[:], in_=groupeds[s][:]
+            )
+
+        def logits(s):
+            words, planes = codes[s]
+            lgs[s] = ps_lg.tile([P, 2, V], F32, name="lg")
+            for q in range(2):
+                for g in range(2):
+                    x = q * 2 + g
+                    nc.tensor.matmul_mx(
+                        out=lgs[s][:, q, :],
+                        lhsT=words[:, x * P : (x + 1) * P].bitcast(FP8X4),
+                        lhsT_scale=planes[:, x * P : (x + 1) * P],
+                        rhs=wfc[:, g * V : (g + 1) * V].bitcast(FP8X4),
+                        rhs_scale=wfs[:, g * V : (g + 1) * V],
+                        start=(g == 0),
+                        stop=(g == 1),
+                    )
+
+        def bias_and_max(s):
+            bi = batch_of[s]
+            n = 2 * BATCH_HU[bi]
+            if s == first_of[bi]:
+                pool = l_first if bi == 0 else l_rest
+                Ls[bi] = pool.tile([P, n, V], F32, name="L%d" % bi)
+                negms[bi] = small.tile([P, n], F32, name="negm")
+                ssums[bi] = small.tile([P, n], F32, name="ssum")
+            k = 2 * (s - first_of[bi])
+            nc.vector.tensor_tensor(
+                out=Ls[bi][:, k : k + 2, :],
+                in0=lgs[s][:],
+                in1=bfc[:].unsqueeze(1).to_broadcast([P, 2, V]),
+                op=ALU.add,
+            )
+            nc.vector.tensor_reduce(
+                out=negms[bi][:, k : k + 2],
+                in_=Ls[bi][:, k : k + 2, 1:V],
+                axis=AX.X,
+                op=ALU.max,
+                negate=True,
+            )
+
+        def exps(s):
+            bi = batch_of[s]
+            k = 2 * (s - first_of[bi])
+            for q in range(2):
+                junk = junk_pool.tile([P, V], BF16, name="junk")
+                nc.scalar.activation(
+                    out=junk[:, 1:V],
+                    in_=Ls[bi][:, k + q, 1:V],
+                    func=ACT.Exp,
+                    bias=negms[bi][:, k + q : k + q + 1],
+                    scale=1.0,
+                    accum_out=ssums[bi][:, k + q : k + q + 1],
+                )
+
+        def row_a(bi):
+            n = 2 * BATCH_HU[bi]
+            l0 = Ls[bi][:, :, 0]
             nab = small.tile([P, n], F32, name="nab")
+            t1 = small.tile([P, n], F32, name="t1")
+            mn = small.tile([P, n], F32, name="mn")
             nc.vector.scalar_tensor_tensor(
                 out=nab[:], in0=l0, scalar=-1.0, in1=l0, op0=ALU.mult, op1=ALU.min
             )
+            nc.vector.scalar_tensor_tensor(
+                out=t1[:], in0=l0, scalar=0.0, in1=negms[bi][:], op0=ALU.max, op1=ALU.subtract
+            )
+            nc.vector.tensor_scalar_min(out=mn[:], in0=l0, scalar1=0.0)
+            misc[bi] = {"nab": nab, "t1": t1, "mn": mn}
+
+        def row_b(bi):
+            n = 2 * BATCH_HU[bi]
             ex = small.tile([P, n], F32, name="ex")
-            nc.scalar.activation(out=ex[:], in_=nab[:], func=ACT.Exp)
+            nc.scalar.activation(out=ex[:], in_=misc[bi]["nab"][:], func=ACT.Exp)
+            misc[bi]["ex"] = ex
+
+        def row_c(bi):
+            n = 2 * BATCH_HU[bi]
             sq = small.tile([P, 2, n], F32, name="sq")
-            nc.vector.tensor_scalar_add(out=sq[:, 0, :], in0=ex[:], scalar1=1.0)
-            nc.vector.tensor_tensor(out=sq[:, 1, :], in0=sq[:, 0, :], in1=ssum[:], op=ALU.mult)
+            nc.vector.tensor_scalar_add(out=sq[:, 0, :], in0=misc[bi]["ex"][:], scalar1=1.0)
+            nc.vector.tensor_tensor(
+                out=sq[:, 1, :], in0=sq[:, 0, :], in1=ssums[bi][:], op=ALU.mult
+            )
+            misc[bi]["sq"] = sq
+
+        def row_d(bi):
+            n = 2 * BATCH_HU[bi]
             lns = small.tile([P, 2, n], F32, name="lns")
-            nc.scalar.activation(out=lns[:], in_=sq[:], func=ACT.Ln)
-            t1 = small.tile([P, n], F32, name="t1")
+            nc.scalar.activation(out=lns[:], in_=misc[bi]["sq"][:], func=ACT.Ln)
+            misc[bi]["lns"] = lns
+
+        def row_e(bi):
+            n = 2 * BATCH_HU[bi]
+            lns = misc[bi]["lns"]
+            negc = small.tile([P, n], F32, name="negc")
+            o0 = small.tile([P, n], F32, name="o0")
             nc.vector.scalar_tensor_tensor(
-                out=t1[:], in0=l0, scalar=0.0, in1=negm[:], op0=ALU.max, op1=ALU.subtract
+                out=negc[:], in0=misc[bi]["t1"][:], scalar=-1.0, in1=lns[:, 1, :],
+                op0=ALU.mult, op1=ALU.subtract,
             )
-            cc = small.tile([P, n], F32, name="cc")
-            nc.vector.tensor_tensor(out=cc[:], in0=t1[:], in1=lns[:, 1, :], op=ALU.add)
-            nc.vector.scalar_tensor_tensor(
-                out=l0, in0=l0, scalar=0.0, in1=lns[:, 0, :], op0=ALU.min, op1=ALU.subtract
+            nc.vector.tensor_tensor(
+                out=o0[:], in0=misc[bi]["mn"][:], in1=lns[:, 0, :], op=ALU.subtract
             )
-            for iu in range(n_units):
-                un = first_unit + iu
-                b = un // (U // UPU)
-                u0 = (un % (U // UPU)) * UPU
-                k0 = iu * UPU
-                for q in range(UPU):
-                    nc.vector.tensor_scalar(
-                        out=L[:, k0 + q, 1:V],
-                        in0=L[:, k0 + q, 1:V],
-                        scalar1=cc[:, k0 + q : k0 + q + 1],
-                        scalar2=None,
-                        op0=ALU.subtract,
-                    )
-                nc.sync.dma_start(out=out[b, :, u0 : u0 + UPU, :], in_=L[:, k0 : k0 + UPU, :])
+            nc.vector.tensor_tensor(
+                out=Ls[bi][:, :, 0], in0=o0[:], in1=negc[:], op=ALU.subtract
+            )
+            misc[bi]["negc"] = negc
+
+        def finish(bi, engines):
+            negc = misc[bi]["negc"]
+            for k0 in range(0, 2 * BATCH_HU[bi], 4):
+                s = first_of[bi] + k0 // 2
+                b = s // (HU // B)
+                u0 = (s % (HU // B)) * 2
+                for q in range(4):
+                    k = k0 + q
+                    row = Ls[bi][:, k, :]
+                    e = engines[q % len(engines)]
+                    if e == "G":
+                        nc.gpsimd.tensor_scalar(
+                            out=row, in0=row, scalar1=1.0, scalar2=negc[:, k : k + 1],
+                            op0=ALU.mult, op1=ALU.add,
+                        )
+                    elif e == "A":
+                        nc.scalar.activation(
+                            out=row, in_=row, func=ACT.Identity, bias=negc[:, k : k + 1], scale=1.0
+                        )
+                    else:
+                        nc.vector.tensor_scalar(
+                            out=row, in0=row, scalar1=negc[:, k : k + 1], scalar2=None, op0=ALU.add
+                        )
+                nc.sync.dma_start(out=out[b, :, u0 : u0 + 4, :], in_=Ls[bi][:, k0 : k0 + 4, :])
+
+        for s in range(LEAD):
+            tanh_part(s, 0)
+        for s in range(LEAD):
+            tanh_part(s, 1)
+        n_batches = len(BATCH_HU)
+        for w in range(HU + 7):
+            if LEAD <= w < HU:
+                tanh_part(w, 0)
+                tanh_part(w, 1)
+            if 0 <= w - 4 < HU:
+                exps(w - 4)
+            for bi in range(n_batches):
+                if w - 4 == last_of[bi]:
+                    row_b(bi)
+            if 0 <= w - 2 < HU:
+                quantise_h(w - 2)
+                logits(w - 2)
+            for bi in range(n_batches):
+                if w - 5 == last_of[bi]:
+                    row_c(bi)
+                    row_d(bi)
+                if w - 6 == last_of[bi]:
+                    row_e(bi)
+                    finish(bi, V3_TAIL if bi == n_batches - 1 else "G")
+            if 0 <= w - 1 < HU:
+                regroup(w - 1)
+            if 0 <= w - 3 < HU:
+                bias_and_max(w - 3)
+            for bi in range(n_batches):
+                if w - 3 == last_of[bi]:
+                    row_a(bi)

@@ -15,11 +15,11 @@ AX = mybir.AxisListType
 P = 128
 B, T, U, K1, F, V = 2, 128, 64, 512, 1024, 256
 NCH = 8
-HU = B * U // 2
-BATCH_HU = [38, 20, 6]
-LEAD = 3
-PIN = True
-V3_TAIL = "VAVG"
+ROWS = B * U
+BATCH_ROWS = [80, 36, 12]
+TAPER = 4
+V3_ENGINES = ["G", "GGV", "VAVG"]
+PIN = False
 
 FLOPS = 2 * (B * T * K1 * F + B * U * K1 * F + B * T * U * F * V)
 
@@ -35,7 +35,7 @@ def tile_jointnet_t_kernel(
         ps_tr = ctx.enter_context(tc.psum_pool(name="ps_tr", bufs=3))
         ps_s1 = ctx.enter_context(tc.psum_pool(name="ps_s1", bufs=2))
         ps_lg = ctx.enter_context(tc.psum_pool(name="ps_lg", bufs=3))
-        hp_pool = ctx.enter_context(tc.tile_pool(name="hp", bufs=LEAD + 1))
+        hp_pool = ctx.enter_context(tc.tile_pool(name="hp", bufs=6))
         gr_pool = ctx.enter_context(tc.tile_pool(name="gr", bufs=3))
         cd_pool = ctx.enter_context(tc.tile_pool(name="cd", bufs=3))
         small = ctx.enter_context(tc.tile_pool(name="small", bufs=2))
@@ -78,11 +78,14 @@ def tile_jointnet_t_kernel(
             nc.sync.dma_start(out=dec_sb[:], in_=decoder_output.rearrange("b u k -> (b u) k"))
             wenc_sb = stage.tile([P, NCH, K1], BF16, name="wenc_sb")
             wdec_sb = stage.tile([P, NCH, K1], BF16, name="wdec_sb")
-            for g in range(2):
+            for c in range(0, NCH, 2):
+                g, j0 = c // 4, c % 4
                 for w_sb, w in ((wenc_sb, W_enc), (wdec_sb, W_dec)):
                     nc.sync.dma_start(
-                        out=w_sb[:, 4 * g : 4 * g + 4, :],
-                        in_=w[512 * g : 512 * g + 512, :].rearrange("(p j) k -> p j k", j=4),
+                        out=w_sb[:, c : c + 2, :],
+                        in_=w[512 * g : 512 * g + 512, :].rearrange("(p j) k -> p j k", j=4)[
+                            :, j0 : j0 + 2, :
+                        ],
                     )
             wfc_sb = stage.tile([P, 2, F], BF16, name="wfc_sb")
             nc.sync.dma_start(out=wfc_sb[:], in_=W_fc.rearrange("(h v) k -> v h k", h=2))
@@ -113,14 +116,6 @@ def tile_jointnet_t_kernel(
                     nc.scalar.copy(out=o, in_=i)
                 else:
                     nc.vector.tensor_copy(out=o, in_=i)
-
-            def transpose_weights(w_sb, grouped, g, on_scalar):
-                for c in (4 * g, 4 * g + 2):
-                    transpose_tiles(
-                        [halves(w_sb[:, c, :]), halves(w_sb[:, c + 1, :])],
-                        grouped[:, c * 512 : (c + 2) * 512],
-                        on_scalar,
-                    )
 
             def quantise(grouped, codes, scales, first, count):
                 nc.vector.quantize_mx(
@@ -169,18 +164,17 @@ def tile_jointnet_t_kernel(
             nc.vector.tensor_copy(out=bdec[:], in_=bdec_bf[:])
             quantise(xg, xc, xs, 0, 2)
             quantise(xg, xc, xs, 2, 1)
-            transpose_weights(wenc_sb, weg, 0, True)
-            transpose_weights(wdec_sb, wdg, 0, False)
-            quantise(weg, wec, wes, 0, 4)
-            quantise(wdg, wdc, wds, 0, 4)
-            transpose_weights(wenc_sb, weg, 1, True)
-            for c in range(4):
-                input_matmuls(c, c % 2 == 1)
-            transpose_weights(wdec_sb, wdg, 1, False)
-            quantise(weg, wec, wes, 4, 4)
-            quantise(wdg, wdc, wds, 4, 4)
-            for c in range(4, 8):
-                input_matmuls(c, False)
+            for c in range(0, NCH, 2):
+                for w_sb, grouped, on_scalar in ((wenc_sb, weg, c == 0), (wdec_sb, wdg, False)):
+                    transpose_tiles(
+                        [halves(w_sb[:, c, :]), halves(w_sb[:, c + 1, :])],
+                        grouped[:, c * 512 : (c + 2) * 512],
+                        on_scalar,
+                    )
+                quantise(weg, wec, wes, c, 2)
+                quantise(wdg, wdc, wds, c, 2)
+                input_matmuls(c, c == 0)
+                input_matmuls(c + 1, False)
             for g in range(2):
                 views = []
                 for h in range(2):
@@ -192,102 +186,80 @@ def tile_jointnet_t_kernel(
 
         l_rest = ctx.enter_context(tc.tile_pool(name="l_rest", bufs=1))
 
-        batch_of = []
-        first_of = []
-        for bi, n_hu in enumerate(BATCH_HU):
-            first_of.append(len(batch_of))
-            batch_of.extend([bi] * n_hu)
-        last_of = [first_of[bi] + BATCH_HU[bi] - 1 for bi in range(len(BATCH_HU))]
-        hPs, groupeds, codes, lgs = {}, {}, {}, {}
-        Ls, negms, ssums, misc = {}, {}, {}, {}
-
-        def tanh_part(s, g):
-            b = s // (HU // B)
-            u0 = (s % (HU // B)) * 2
-            if g == 0:
-                hPs[s] = hp_pool.tile([P, 4, 4 * P], BF16, name="hP")
-            for j in range(4):
-                for q in range(2):
-                    x = q * 2 + g
-                    nc.scalar.activation(
-                        out=hPs[s][:, j, x * P : (x + 1) * P],
-                        in_=encB[:, 4 * g + j, b * T : (b + 1) * T],
-                        func=ACT.Tanh,
-                        bias=decB[:, 4 * g + j, b * U + u0 + q : b * U + u0 + q + 1],
-                        scale=1.0,
-                    )
-
-        def regroup(s):
-            groupeds[s] = gr_pool.tile([P, 16 * P], BF16, name="grouped", align_bytes=64)
-            nc.vector.tensor_copy(
-                out=groupeds[s][:].rearrange("p (c i j) -> p c j i", i=4, j=4),
-                in_=hPs[s][:].rearrange("p j (c i) -> p c j i", i=4),
-            )
-
-        def quantise_h(s):
-            words = cd_pool.tile([P, 4 * P], U32, name="words", align_bytes=64)
-            planes = cd_pool.tile([P, 4 * P], U8, name="planes", align_bytes=64)
-            codes[s] = (words, planes)
-            nc.vector.quantize_mx(
-                out=words[:].bitcast(FP8X4), scales=planes[:], in_=groupeds[s][:]
-            )
-
-        def logits(s):
-            words, planes = codes[s]
-            lgs[s] = ps_lg.tile([P, 2, V], F32, name="lg")
-            for q in range(2):
+        steps = [(r, 2) for r in range(0, ROWS - TAPER, 2)] + [
+            (r, 1) for r in range(ROWS - TAPER, ROWS)
+        ]
+        row0 = 0
+        for bi, n in enumerate(BATCH_ROWS):
+            pool = l_first if bi == 0 else l_rest
+            L = pool.tile([P, n, V], F32, name="L%d" % bi)
+            negm = small.tile([P, n], F32, name="negm")
+            ssum = small.tile([P, n], F32, name="ssum")
+            for r, nu in steps:
+                if not row0 <= r < row0 + n:
+                    continue
+                b = r // U
+                k = r - row0
+                hP = hp_pool.tile([P, 4, 2 * nu * P], BF16, name="hP")
                 for g in range(2):
-                    x = q * 2 + g
-                    nc.tensor.matmul_mx(
-                        out=lgs[s][:, q, :],
-                        lhsT=words[:, x * P : (x + 1) * P].bitcast(FP8X4),
-                        lhsT_scale=planes[:, x * P : (x + 1) * P],
-                        rhs=wfc[:, g * V : (g + 1) * V].bitcast(FP8X4),
-                        rhs_scale=wfs[:, g * V : (g + 1) * V],
-                        start=(g == 0),
-                        stop=(g == 1),
+                    for j in range(4):
+                        for q in range(nu):
+                            x = q * 2 + g
+                            nc.scalar.activation(
+                                out=hP[:, j, x * P : (x + 1) * P],
+                                in_=encB[:, 4 * g + j, b * T : (b + 1) * T],
+                                func=ACT.Tanh,
+                                bias=decB[:, 4 * g + j, r + q : r + q + 1],
+                                scale=1.0,
+                            )
+                grouped = gr_pool.tile([P, 8 * nu * P], BF16, name="grouped", align_bytes=64)
+                nc.vector.tensor_copy(
+                    out=grouped[:].rearrange("p (c i j) -> p c j i", i=4, j=4),
+                    in_=hP[:].rearrange("p j (c i) -> p c j i", i=4),
+                )
+                words = cd_pool.tile([P, 2 * nu * P], U32, name="words", align_bytes=64)
+                planes = cd_pool.tile([P, 2 * nu * P], U8, name="planes", align_bytes=64)
+                nc.vector.quantize_mx(
+                    out=words[:].bitcast(FP8X4), scales=planes[:], in_=grouped[:]
+                )
+                lg = ps_lg.tile([P, nu, V], F32, name="lg")
+                for q in range(nu):
+                    for g in range(2):
+                        x = q * 2 + g
+                        nc.tensor.matmul_mx(
+                            out=lg[:, q, :],
+                            lhsT=words[:, x * P : (x + 1) * P].bitcast(FP8X4),
+                            lhsT_scale=planes[:, x * P : (x + 1) * P],
+                            rhs=wfc[:, g * V : (g + 1) * V].bitcast(FP8X4),
+                            rhs_scale=wfs[:, g * V : (g + 1) * V],
+                            start=(g == 0),
+                            stop=(g == 1),
+                        )
+                nc.vector.tensor_tensor(
+                    out=L[:, k : k + nu, :],
+                    in0=lg[:],
+                    in1=bfc[:].unsqueeze(1).to_broadcast([P, nu, V]),
+                    op=ALU.add,
+                )
+                nc.vector.tensor_reduce(
+                    out=negm[:, k : k + nu],
+                    in_=L[:, k : k + nu, 1:V],
+                    axis=AX.X,
+                    op=ALU.max,
+                    negate=True,
+                )
+                for q in range(nu):
+                    junk = junk_pool.tile([P, V], BF16, name="junk")
+                    nc.scalar.activation(
+                        out=junk[:, 1:V],
+                        in_=L[:, k + q, 1:V],
+                        func=ACT.Exp,
+                        bias=negm[:, k + q : k + q + 1],
+                        scale=1.0,
+                        accum_out=ssum[:, k + q : k + q + 1],
                     )
 
-        def bias_and_max(s):
-            bi = batch_of[s]
-            n = 2 * BATCH_HU[bi]
-            if s == first_of[bi]:
-                pool = l_first if bi == 0 else l_rest
-                Ls[bi] = pool.tile([P, n, V], F32, name="L%d" % bi)
-                negms[bi] = small.tile([P, n], F32, name="negm")
-                ssums[bi] = small.tile([P, n], F32, name="ssum")
-            k = 2 * (s - first_of[bi])
-            nc.vector.tensor_tensor(
-                out=Ls[bi][:, k : k + 2, :],
-                in0=lgs[s][:],
-                in1=bfc[:].unsqueeze(1).to_broadcast([P, 2, V]),
-                op=ALU.add,
-            )
-            nc.vector.tensor_reduce(
-                out=negms[bi][:, k : k + 2],
-                in_=Ls[bi][:, k : k + 2, 1:V],
-                axis=AX.X,
-                op=ALU.max,
-                negate=True,
-            )
-
-        def exps(s):
-            bi = batch_of[s]
-            k = 2 * (s - first_of[bi])
-            for q in range(2):
-                junk = junk_pool.tile([P, V], BF16, name="junk")
-                nc.scalar.activation(
-                    out=junk[:, 1:V],
-                    in_=Ls[bi][:, k + q, 1:V],
-                    func=ACT.Exp,
-                    bias=negms[bi][:, k + q : k + q + 1],
-                    scale=1.0,
-                    accum_out=ssums[bi][:, k + q : k + q + 1],
-                )
-
-        def row_a(bi):
-            n = 2 * BATCH_HU[bi]
-            l0 = Ls[bi][:, :, 0]
+            l0 = L[:, :, 0]
             nab = small.tile([P, n], F32, name="nab")
             t1 = small.tile([P, n], F32, name="t1")
             mn = small.tile([P, n], F32, name="mn")
@@ -295,59 +267,31 @@ def tile_jointnet_t_kernel(
                 out=nab[:], in0=l0, scalar=-1.0, in1=l0, op0=ALU.mult, op1=ALU.min
             )
             nc.vector.scalar_tensor_tensor(
-                out=t1[:], in0=l0, scalar=0.0, in1=negms[bi][:], op0=ALU.max, op1=ALU.subtract
+                out=t1[:], in0=l0, scalar=0.0, in1=negm[:], op0=ALU.max, op1=ALU.subtract
             )
             nc.vector.tensor_scalar_min(out=mn[:], in0=l0, scalar1=0.0)
-            misc[bi] = {"nab": nab, "t1": t1, "mn": mn}
-
-        def row_b(bi):
-            n = 2 * BATCH_HU[bi]
             ex = small.tile([P, n], F32, name="ex")
-            nc.scalar.activation(out=ex[:], in_=misc[bi]["nab"][:], func=ACT.Exp)
-            misc[bi]["ex"] = ex
-
-        def row_c(bi):
-            n = 2 * BATCH_HU[bi]
+            nc.scalar.activation(out=ex[:], in_=nab[:], func=ACT.Exp)
             sq = small.tile([P, 2, n], F32, name="sq")
-            nc.vector.tensor_scalar_add(out=sq[:, 0, :], in0=misc[bi]["ex"][:], scalar1=1.0)
-            nc.vector.tensor_tensor(
-                out=sq[:, 1, :], in0=sq[:, 0, :], in1=ssums[bi][:], op=ALU.mult
-            )
-            misc[bi]["sq"] = sq
-
-        def row_d(bi):
-            n = 2 * BATCH_HU[bi]
+            nc.vector.tensor_scalar_add(out=sq[:, 0, :], in0=ex[:], scalar1=1.0)
+            nc.vector.tensor_tensor(out=sq[:, 1, :], in0=sq[:, 0, :], in1=ssum[:], op=ALU.mult)
             lns = small.tile([P, 2, n], F32, name="lns")
-            nc.scalar.activation(out=lns[:], in_=misc[bi]["sq"][:], func=ACT.Ln)
-            misc[bi]["lns"] = lns
-
-        def row_e(bi):
-            n = 2 * BATCH_HU[bi]
-            lns = misc[bi]["lns"]
+            nc.scalar.activation(out=lns[:], in_=sq[:], func=ACT.Ln)
             negc = small.tile([P, n], F32, name="negc")
             o0 = small.tile([P, n], F32, name="o0")
             nc.vector.scalar_tensor_tensor(
-                out=negc[:], in0=misc[bi]["t1"][:], scalar=-1.0, in1=lns[:, 1, :],
+                out=negc[:], in0=t1[:], scalar=-1.0, in1=lns[:, 1, :],
                 op0=ALU.mult, op1=ALU.subtract,
             )
-            nc.vector.tensor_tensor(
-                out=o0[:], in0=misc[bi]["mn"][:], in1=lns[:, 0, :], op=ALU.subtract
-            )
-            nc.vector.tensor_tensor(
-                out=Ls[bi][:, :, 0], in0=o0[:], in1=negc[:], op=ALU.subtract
-            )
-            misc[bi]["negc"] = negc
-
-        def finish(bi, engines):
-            negc = misc[bi]["negc"]
-            for k0 in range(0, 2 * BATCH_HU[bi], 4):
-                s = first_of[bi] + k0 // 2
-                b = s // (HU // B)
-                u0 = (s % (HU // B)) * 2
+            nc.vector.tensor_tensor(out=o0[:], in0=mn[:], in1=lns[:, 0, :], op=ALU.subtract)
+            nc.vector.tensor_tensor(out=l0, in0=o0[:], in1=negc[:], op=ALU.subtract)
+            engines = V3_ENGINES[bi]
+            for k0 in range(0, n, 4):
+                r = row0 + k0
                 for q in range(4):
                     k = k0 + q
-                    row = Ls[bi][:, k, :]
-                    e = engines[q % len(engines)]
+                    row = L[:, k, :]
+                    e = engines[k % len(engines)]
                     if e == "G":
                         nc.gpsimd.tensor_scalar(
                             out=row, in0=row, scalar1=1.0, scalar2=negc[:, k : k + 1],
@@ -361,36 +305,7 @@ def tile_jointnet_t_kernel(
                         nc.vector.tensor_scalar(
                             out=row, in0=row, scalar1=negc[:, k : k + 1], scalar2=None, op0=ALU.add
                         )
-                nc.sync.dma_start(out=out[b, :, u0 : u0 + 4, :], in_=Ls[bi][:, k0 : k0 + 4, :])
-
-        for s in range(LEAD):
-            tanh_part(s, 0)
-        for s in range(LEAD):
-            tanh_part(s, 1)
-        n_batches = len(BATCH_HU)
-        for w in range(HU + 7):
-            if LEAD <= w < HU:
-                tanh_part(w, 0)
-                tanh_part(w, 1)
-            if 0 <= w - 4 < HU:
-                exps(w - 4)
-            for bi in range(n_batches):
-                if w - 4 == last_of[bi]:
-                    row_b(bi)
-            if 0 <= w - 2 < HU:
-                quantise_h(w - 2)
-                logits(w - 2)
-            for bi in range(n_batches):
-                if w - 5 == last_of[bi]:
-                    row_c(bi)
-                    row_d(bi)
-                if w - 6 == last_of[bi]:
-                    row_e(bi)
-                    finish(bi, V3_TAIL if bi == n_batches - 1 else "G")
-            if 0 <= w - 1 < HU:
-                regroup(w - 1)
-            if 0 <= w - 3 < HU:
-                bias_and_max(w - 3)
-            for bi in range(n_batches):
-                if w - 3 == last_of[bi]:
-                    row_a(bi)
+                nc.sync.dma_start(
+                    out=out[r // U, :, r % U : r % U + 4, :], in_=L[:, k0 : k0 + 4, :]
+                )
+            row0 += n

@@ -18,7 +18,7 @@ NCH = 8
 ROWS = B * U
 BATCH_ROWS = [80, 36, 12]
 TAPER = 4
-V3_ENGINES = ["G", "GGV", "VAVG"]
+V3_ENGINES = ["V", "V", "VAVA"]
 PIN = False
 
 FLOPS = 2 * (B * T * K1 * F + B * U * K1 * F + B * T * U * F * V)

@@ -18,7 +18,7 @@ NCH = 8
 ROWS = B * U
 BATCH_ROWS = [80, 36, 12]
 TAPER = 4
-V3_ENGINES = ["V", "V", "VAVA"]
+V3_ENGINES = ["VVVA", "VA", "VA"]
 PIN = False
 
 FLOPS = 2 * (B * T * K1 * F + B * U * K1 * F + B * T * U * F * V)

@@ -16,10 +16,13 @@ P = 128
 B, T, U, K1, F, V = 2, 128, 64, 512, 1024, 256
 NCH = 8
 ROWS = B * U
-BATCH_ROWS = [80, 36, 12]
+BATCH_ROWS = [72, 44, 12]
 TAPER = 4
-V3_ENGINES = ["VVVA", "VA", "VA"]
-PIN = False
+LEAD = 3
+PIN = True
+QUOTA = (2, 1, 0)
+QUOTA_LATE = (1, 3, 2)
+LATE_FROM = 63
 
 FLOPS = 2 * (B * T * K1 * F + B * U * K1 * F + B * T * U * F * V)
 
@@ -35,7 +38,7 @@ def tile_jointnet_t_kernel(
         ps_tr = ctx.enter_context(tc.psum_pool(name="ps_tr", bufs=3))
         ps_s1 = ctx.enter_context(tc.psum_pool(name="ps_s1", bufs=2))
         ps_lg = ctx.enter_context(tc.psum_pool(name="ps_lg", bufs=3))
-        hp_pool = ctx.enter_context(tc.tile_pool(name="hp", bufs=6))
+        hp_pool = ctx.enter_context(tc.tile_pool(name="hp", bufs=LEAD + 2))
         gr_pool = ctx.enter_context(tc.tile_pool(name="gr", bufs=3))
         cd_pool = ctx.enter_context(tc.tile_pool(name="cd", bufs=3))
         small = ctx.enter_context(tc.tile_pool(name="small", bufs=2))
@@ -78,14 +81,11 @@ def tile_jointnet_t_kernel(
             nc.sync.dma_start(out=dec_sb[:], in_=decoder_output.rearrange("b u k -> (b u) k"))
             wenc_sb = stage.tile([P, NCH, K1], BF16, name="wenc_sb")
             wdec_sb = stage.tile([P, NCH, K1], BF16, name="wdec_sb")
-            for c in range(0, NCH, 2):
-                g, j0 = c // 4, c % 4
+            for g in range(2):
                 for w_sb, w in ((wenc_sb, W_enc), (wdec_sb, W_dec)):
                     nc.sync.dma_start(
-                        out=w_sb[:, c : c + 2, :],
-                        in_=w[512 * g : 512 * g + 512, :].rearrange("(p j) k -> p j k", j=4)[
-                            :, j0 : j0 + 2, :
-                        ],
+                        out=w_sb[:, 4 * g : 4 * g + 4, :],
+                        in_=w[512 * g : 512 * g + 512, :].rearrange("(p j) k -> p j k", j=4),
                     )
             wfc_sb = stage.tile([P, 2, F], BF16, name="wfc_sb")
             nc.sync.dma_start(out=wfc_sb[:], in_=W_fc.rearrange("(h v) k -> v h k", h=2))
@@ -116,6 +116,14 @@ def tile_jointnet_t_kernel(
                     nc.scalar.copy(out=o, in_=i)
                 else:
                     nc.vector.tensor_copy(out=o, in_=i)
+
+            def transpose_weights(w_sb, grouped, g, on_scalar):
+                for c in (4 * g, 4 * g + 2):
+                    transpose_tiles(
+                        [halves(w_sb[:, c, :]), halves(w_sb[:, c + 1, :])],
+                        grouped[:, c * 512 : (c + 2) * 512],
+                        on_scalar,
+                    )
 
             def quantise(grouped, codes, scales, first, count):
                 nc.vector.quantize_mx(
@@ -164,17 +172,18 @@ def tile_jointnet_t_kernel(
             nc.vector.tensor_copy(out=bdec[:], in_=bdec_bf[:])
             quantise(xg, xc, xs, 0, 2)
             quantise(xg, xc, xs, 2, 1)
-            for c in range(0, NCH, 2):
-                for w_sb, grouped, on_scalar in ((wenc_sb, weg, c == 0), (wdec_sb, wdg, False)):
-                    transpose_tiles(
-                        [halves(w_sb[:, c, :]), halves(w_sb[:, c + 1, :])],
-                        grouped[:, c * 512 : (c + 2) * 512],
-                        on_scalar,
-                    )
-                quantise(weg, wec, wes, c, 2)
-                quantise(wdg, wdc, wds, c, 2)
-                input_matmuls(c, c == 0)
-                input_matmuls(c + 1, False)
+            transpose_weights(wenc_sb, weg, 0, True)
+            transpose_weights(wdec_sb, wdg, 0, False)
+            quantise(weg, wec, wes, 0, 4)
+            quantise(wdg, wdc, wds, 0, 4)
+            transpose_weights(wenc_sb, weg, 1, True)
+            for c in range(4):
+                input_matmuls(c, c % 2 == 1)
+            transpose_weights(wdec_sb, wdg, 1, False)
+            quantise(weg, wec, wes, 4, 4)
+            quantise(wdg, wdc, wds, 4, 4)
+            for c in range(4, 8):
+                input_matmuls(c, False)
             for g in range(2):
                 views = []
                 for h in range(2):
@@ -185,81 +194,116 @@ def tile_jointnet_t_kernel(
             nc.vector.tensor_copy(out=bfc[:], in_=bfc_bf[:])
 
         l_rest = ctx.enter_context(tc.tile_pool(name="l_rest", bufs=1))
+        tok_pool = ctx.enter_context(tc.tile_pool(name="tok", bufs=4))
 
         steps = [(r, 2) for r in range(0, ROWS - TAPER, 2)] + [
             (r, 1) for r in range(ROWS - TAPER, ROWS)
         ]
-        row0 = 0
+        NS = len(steps)
+        row0_of = [sum(BATCH_ROWS[:bi]) for bi in range(len(BATCH_ROWS))]
+        batch_of_row = []
         for bi, n in enumerate(BATCH_ROWS):
-            pool = l_first if bi == 0 else l_rest
-            L = pool.tile([P, n, V], F32, name="L%d" % bi)
-            negm = small.tile([P, n], F32, name="negm")
-            ssum = small.tile([P, n], F32, name="ssum")
-            for r, nu in steps:
-                if not row0 <= r < row0 + n:
-                    continue
-                b = r // U
-                k = r - row0
-                hP = hp_pool.tile([P, 4, 2 * nu * P], BF16, name="hP")
-                for g in range(2):
-                    for j in range(4):
-                        for q in range(nu):
-                            x = q * 2 + g
-                            nc.scalar.activation(
-                                out=hP[:, j, x * P : (x + 1) * P],
-                                in_=encB[:, 4 * g + j, b * T : (b + 1) * T],
-                                func=ACT.Tanh,
-                                bias=decB[:, 4 * g + j, r + q : r + q + 1],
-                                scale=1.0,
-                            )
-                grouped = gr_pool.tile([P, 8 * nu * P], BF16, name="grouped", align_bytes=64)
-                nc.vector.tensor_copy(
-                    out=grouped[:].rearrange("p (c i j) -> p c j i", i=4, j=4),
-                    in_=hP[:].rearrange("p j (c i) -> p c j i", i=4),
-                )
-                words = cd_pool.tile([P, 2 * nu * P], U32, name="words", align_bytes=64)
-                planes = cd_pool.tile([P, 2 * nu * P], U8, name="planes", align_bytes=64)
-                nc.vector.quantize_mx(
-                    out=words[:].bitcast(FP8X4), scales=planes[:], in_=grouped[:]
-                )
-                lg = ps_lg.tile([P, nu, V], F32, name="lg")
+            batch_of_row.extend([bi] * n)
+        last_step_of = [
+            max(s for s in range(NS) if batch_of_row[steps[s][0]] == bi)
+            for bi in range(len(BATCH_ROWS))
+        ]
+        n_batches = len(BATCH_ROWS)
+        hPs, groupeds, codes, lgs = {}, {}, {}, {}
+        Ls, negms, ssums, misc = {}, {}, {}, {}
+
+        def tanh_part(s, g):
+            r, nu = steps[s]
+            b = r // U
+            if g == 0:
+                hPs[s] = hp_pool.tile([P, 4, 2 * nu * P], BF16, name="hP")
+            for j in range(4):
                 for q in range(nu):
-                    for g in range(2):
-                        x = q * 2 + g
-                        nc.tensor.matmul_mx(
-                            out=lg[:, q, :],
-                            lhsT=words[:, x * P : (x + 1) * P].bitcast(FP8X4),
-                            lhsT_scale=planes[:, x * P : (x + 1) * P],
-                            rhs=wfc[:, g * V : (g + 1) * V].bitcast(FP8X4),
-                            rhs_scale=wfs[:, g * V : (g + 1) * V],
-                            start=(g == 0),
-                            stop=(g == 1),
-                        )
-                nc.vector.tensor_tensor(
-                    out=L[:, k : k + nu, :],
-                    in0=lg[:],
-                    in1=bfc[:].unsqueeze(1).to_broadcast([P, nu, V]),
-                    op=ALU.add,
-                )
-                nc.vector.tensor_reduce(
-                    out=negm[:, k : k + nu],
-                    in_=L[:, k : k + nu, 1:V],
-                    axis=AX.X,
-                    op=ALU.max,
-                    negate=True,
-                )
-                for q in range(nu):
-                    junk = junk_pool.tile([P, V], BF16, name="junk")
+                    x = q * 2 + g
                     nc.scalar.activation(
-                        out=junk[:, 1:V],
-                        in_=L[:, k + q, 1:V],
-                        func=ACT.Exp,
-                        bias=negm[:, k + q : k + q + 1],
+                        out=hPs[s][:, j, x * P : (x + 1) * P],
+                        in_=encB[:, 4 * g + j, b * T : (b + 1) * T],
+                        func=ACT.Tanh,
+                        bias=decB[:, 4 * g + j, r + q : r + q + 1],
                         scale=1.0,
-                        accum_out=ssum[:, k + q : k + q + 1],
                     )
 
-            l0 = L[:, :, 0]
+        def regroup(s):
+            nu = steps[s][1]
+            groupeds[s] = gr_pool.tile([P, 8 * nu * P], BF16, name="grouped", align_bytes=64)
+            nc.vector.tensor_copy(
+                out=groupeds[s][:].rearrange("p (c i j) -> p c j i", i=4, j=4),
+                in_=hPs[s][:].rearrange("p j (c i) -> p c j i", i=4),
+            )
+
+        def quantise_h(s):
+            nu = steps[s][1]
+            words = cd_pool.tile([P, 2 * nu * P], U32, name="words", align_bytes=64)
+            planes = cd_pool.tile([P, 2 * nu * P], U8, name="planes", align_bytes=64)
+            codes[s] = (words, planes)
+            nc.vector.quantize_mx(
+                out=words[:].bitcast(FP8X4), scales=planes[:], in_=groupeds[s][:]
+            )
+
+        def logits(s):
+            nu = steps[s][1]
+            words, planes = codes[s]
+            lgs[s] = ps_lg.tile([P, nu, V], F32, name="lg")
+            for q in range(nu):
+                for g in range(2):
+                    x = q * 2 + g
+                    nc.tensor.matmul_mx(
+                        out=lgs[s][:, q, :],
+                        lhsT=words[:, x * P : (x + 1) * P].bitcast(FP8X4),
+                        lhsT_scale=planes[:, x * P : (x + 1) * P],
+                        rhs=wfc[:, g * V : (g + 1) * V].bitcast(FP8X4),
+                        rhs_scale=wfs[:, g * V : (g + 1) * V],
+                        start=(g == 0),
+                        stop=(g == 1),
+                    )
+
+        def bias_and_max(s):
+            r, nu = steps[s]
+            bi = batch_of_row[r]
+            n = BATCH_ROWS[bi]
+            if r == row0_of[bi]:
+                pool = l_first if bi == 0 else l_rest
+                Ls[bi] = pool.tile([P, n, V], F32, name="L%d" % bi)
+                negms[bi] = small.tile([P, n], F32, name="negm")
+                ssums[bi] = small.tile([P, n], F32, name="ssum")
+            k = r - row0_of[bi]
+            nc.vector.tensor_tensor(
+                out=Ls[bi][:, k : k + nu, :],
+                in0=lgs[s][:],
+                in1=bfc[:].unsqueeze(1).to_broadcast([P, nu, V]),
+                op=ALU.add,
+            )
+            nc.vector.tensor_reduce(
+                out=negms[bi][:, k : k + nu],
+                in_=Ls[bi][:, k : k + nu, 1:V],
+                axis=AX.X,
+                op=ALU.max,
+                negate=True,
+            )
+
+        def exps(s):
+            r, nu = steps[s]
+            bi = batch_of_row[r]
+            k = r - row0_of[bi]
+            for q in range(nu):
+                junk = junk_pool.tile([P, V], BF16, name="junk")
+                nc.scalar.activation(
+                    out=junk[:, 1:V],
+                    in_=Ls[bi][:, k + q, 1:V],
+                    func=ACT.Exp,
+                    bias=negms[bi][:, k + q : k + q + 1],
+                    scale=1.0,
+                    accum_out=ssums[bi][:, k + q : k + q + 1],
+                )
+
+        def row_a(bi):
+            n = BATCH_ROWS[bi]
+            l0 = Ls[bi][:, :, 0]
             nab = small.tile([P, n], F32, name="nab")
             t1 = small.tile([P, n], F32, name="t1")
             mn = small.tile([P, n], F32, name="mn")
@@ -267,45 +311,136 @@ def tile_jointnet_t_kernel(
                 out=nab[:], in0=l0, scalar=-1.0, in1=l0, op0=ALU.mult, op1=ALU.min
             )
             nc.vector.scalar_tensor_tensor(
-                out=t1[:], in0=l0, scalar=0.0, in1=negm[:], op0=ALU.max, op1=ALU.subtract
+                out=t1[:], in0=l0, scalar=0.0, in1=negms[bi][:], op0=ALU.max, op1=ALU.subtract
             )
             nc.vector.tensor_scalar_min(out=mn[:], in0=l0, scalar1=0.0)
-            ex = small.tile([P, n], F32, name="ex")
-            nc.scalar.activation(out=ex[:], in_=nab[:], func=ACT.Exp)
-            sq = small.tile([P, 2, n], F32, name="sq")
-            nc.vector.tensor_scalar_add(out=sq[:, 0, :], in0=ex[:], scalar1=1.0)
-            nc.vector.tensor_tensor(out=sq[:, 1, :], in0=sq[:, 0, :], in1=ssum[:], op=ALU.mult)
-            lns = small.tile([P, 2, n], F32, name="lns")
-            nc.scalar.activation(out=lns[:], in_=sq[:], func=ACT.Ln)
+            misc[bi] = {"nab": nab, "t1": t1, "mn": mn}
+
+        def row_b(bi):
+            ex = small.tile([P, BATCH_ROWS[bi]], F32, name="ex")
+            nc.scalar.activation(out=ex[:], in_=misc[bi]["nab"][:], func=ACT.Exp)
+            misc[bi]["ex"] = ex
+
+        def row_c(bi):
+            sq = small.tile([P, 2, BATCH_ROWS[bi]], F32, name="sq")
+            nc.vector.tensor_scalar_add(out=sq[:, 0, :], in0=misc[bi]["ex"][:], scalar1=1.0)
+            nc.vector.tensor_tensor(
+                out=sq[:, 1, :], in0=sq[:, 0, :], in1=ssums[bi][:], op=ALU.mult
+            )
+            misc[bi]["sq"] = sq
+
+        def row_d(bi):
+            lns = small.tile([P, 2, BATCH_ROWS[bi]], F32, name="lns")
+            nc.scalar.activation(out=lns[:], in_=misc[bi]["sq"][:], func=ACT.Ln)
+            misc[bi]["lns"] = lns
+
+        def row_e(bi):
+            n = BATCH_ROWS[bi]
+            lns = misc[bi]["lns"]
             negc = small.tile([P, n], F32, name="negc")
             o0 = small.tile([P, n], F32, name="o0")
             nc.vector.scalar_tensor_tensor(
-                out=negc[:], in0=t1[:], scalar=-1.0, in1=lns[:, 1, :],
+                out=negc[:], in0=misc[bi]["t1"][:], scalar=-1.0, in1=lns[:, 1, :],
                 op0=ALU.mult, op1=ALU.subtract,
             )
-            nc.vector.tensor_tensor(out=o0[:], in0=mn[:], in1=lns[:, 0, :], op=ALU.subtract)
-            nc.vector.tensor_tensor(out=l0, in0=o0[:], in1=negc[:], op=ALU.subtract)
-            engines = V3_ENGINES[bi]
-            for k0 in range(0, n, 4):
-                r = row0 + k0
-                for q in range(4):
-                    k = k0 + q
-                    row = L[:, k, :]
-                    e = engines[k % len(engines)]
-                    if e == "G":
-                        nc.gpsimd.tensor_scalar(
-                            out=row, in0=row, scalar1=1.0, scalar2=negc[:, k : k + 1],
-                            op0=ALU.mult, op1=ALU.add,
-                        )
-                    elif e == "A":
-                        nc.scalar.activation(
-                            out=row, in_=row, func=ACT.Identity, bias=negc[:, k : k + 1], scale=1.0
-                        )
-                    else:
-                        nc.vector.tensor_scalar(
-                            out=row, in0=row, scalar1=negc[:, k : k + 1], scalar2=None, op0=ALU.add
-                        )
-                nc.sync.dma_start(
-                    out=out[r // U, :, r % U : r % U + 4, :], in_=L[:, k0 : k0 + 4, :]
+            nc.vector.tensor_tensor(
+                out=o0[:], in0=misc[bi]["mn"][:], in1=lns[:, 0, :], op=ALU.subtract
+            )
+            nc.vector.tensor_tensor(
+                out=Ls[bi][:, :, 0], in0=o0[:], in1=negc[:], op=ALU.subtract
+            )
+            misc[bi]["negc"] = negc
+
+        ready = []
+        taken = [0]
+        done_rows = {}
+        stored = {}
+
+        def take(count):
+            got = []
+            while taken[0] < len(ready) and len(got) < count:
+                r = ready[taken[0]]
+                if got and batch_of_row[r] != batch_of_row[got[0]]:
+                    break
+                got.append(r)
+                taken[0] += 1
+            return got
+
+        def subtract_rows(rows, engine):
+            if not rows:
+                return
+            bi = batch_of_row[rows[0]]
+            k0 = rows[0] - row0_of[bi]
+            negc = misc[bi]["negc"]
+            if engine == "G":
+                tok = tok_pool.tile([P, 2], F32, name="tok")
+                nc.vector.tensor_copy(
+                    out=tok[:, 0 : len(rows)], in_=negc[:, k0 : k0 + len(rows)]
                 )
-            row0 += n
+            for i, r in enumerate(rows):
+                k = r - row0_of[bi]
+                row = Ls[bi][:, k, :]
+                if engine == "G":
+                    nc.gpsimd.tensor_scalar(
+                        out=row, in0=row, scalar1=1.0, scalar2=tok[:, i : i + 1],
+                        op0=ALU.mult, op1=ALU.add,
+                    )
+                elif engine == "A":
+                    nc.scalar.activation(
+                        out=row, in_=row, func=ACT.Identity, bias=negc[:, k : k + 1], scale=1.0
+                    )
+                else:
+                    nc.vector.tensor_scalar(
+                        out=row, in0=row, scalar1=negc[:, k : k + 1], scalar2=None, op0=ALU.add
+                    )
+                done_rows[r] = True
+
+        def stores():
+            for r in range(0, ROWS, 4):
+                if r not in stored and all((r + i) in done_rows for i in range(4)):
+                    bi = batch_of_row[r]
+                    k = r - row0_of[bi]
+                    nc.sync.dma_start(
+                        out=out[r // U, :, r % U : r % U + 4, :], in_=Ls[bi][:, k : k + 4, :]
+                    )
+                    stored[r] = True
+
+        for s in range(LEAD):
+            tanh_part(s, 0)
+        for s in range(LEAD):
+            tanh_part(s, 1)
+        for w in range(NS + 9):
+            late = w >= LATE_FROM
+            rows_a = take(QUOTA_LATE[2] if late else QUOTA[2])
+            if LEAD <= w < NS:
+                tanh_part(w, 0)
+            if 0 <= w - 4 < NS:
+                exps(w - 4)
+            for bi in range(n_batches):
+                if w - 4 == last_step_of[bi]:
+                    row_b(bi)
+                if w - 5 == last_step_of[bi]:
+                    row_d(bi)
+            subtract_rows(rows_a, "A")
+            if LEAD <= w < NS:
+                tanh_part(w, 1)
+            if 0 <= w - 1 < NS:
+                regroup(w - 1)
+            if 0 <= w - 2 < NS:
+                quantise_h(w - 2)
+                logits(w - 2)
+            for bi in range(n_batches):
+                if w - 6 == last_step_of[bi]:
+                    row_e(bi)
+                    ready.extend(range(row0_of[bi], row0_of[bi] + BATCH_ROWS[bi]))
+            subtract_rows(take(QUOTA_LATE[0] if late else QUOTA[0]), "G")
+            if 0 <= w - 3 < NS:
+                bias_and_max(w - 3)
+            for bi in range(n_batches):
+                if w - 3 == last_step_of[bi]:
+                    row_a(bi)
+                if w - 4 == last_step_of[bi]:
+                    row_c(bi)
+            subtract_rows(take(QUOTA_LATE[1] if late else QUOTA[1]), "V")
+            stores()
+        assert taken[0] == ROWS and len(stored) == ROWS // 4

@@ -1,3 +1,4 @@
+import math
 from contextlib import ExitStack
 
 import concourse.mybir as mybir
@@ -6,6 +7,7 @@ from concourse.masks import make_identity
 F32 = mybir.dt.float32
 BF16 = mybir.dt.bfloat16
 U32 = mybir.dt.uint32
+I32 = mybir.dt.int32
 U8 = mybir.dt.uint8
 FP8X4 = mybir.dt.float8_e4m3fn_x4
 ACT = mybir.ActivationFunctionType
@@ -16,13 +18,12 @@ P = 128
 B, T, U, K1, F, V = 2, 128, 64, 512, 1024, 256
 NCH = 8
 ROWS = B * U
-BATCH_ROWS = [72, 44, 12]
+BATCH_ROWS = [24, 24, 24, 24, 16, 8, 8]
 TAPER = 4
 LEAD = 3
 PIN = True
-QUOTA = (2, 1, 0)
-QUOTA_LATE = (1, 3, 2)
-LATE_FROM = 63
+LOG2E_STEP = math.log(2.0) / 2**23
+LOG_SHIFT = -127.0 * math.log(2.0) + 0.0298
 
 FLOPS = 2 * (B * T * K1 * F + B * U * K1 * F + B * T * U * F * V)
 
@@ -43,7 +44,8 @@ def tile_jointnet_t_kernel(
         cd_pool = ctx.enter_context(tc.tile_pool(name="cd", bufs=3))
         small = ctx.enter_context(tc.tile_pool(name="small", bufs=2))
         junk_pool = ctx.enter_context(tc.tile_pool(name="junk", bufs=2))
-        l_first = ctx.enter_context(tc.tile_pool(name="l_first", bufs=1))
+        l_pool = ctx.enter_context(tc.tile_pool(name="l_pool", bufs=3))
+        tok_pool = ctx.enter_context(tc.tile_pool(name="tok", bufs=4))
 
         xc = const.tile([P, 3 * P], U32, name="xc", align_bytes=64)
         xs = const.tile([P, 3 * P], U8, name="xs", align_bytes=64)
@@ -193,9 +195,6 @@ def tile_jointnet_t_kernel(
             quantise(wfg, wfc, wfs, 0, 4)
             nc.vector.tensor_copy(out=bfc[:], in_=bfc_bf[:])
 
-        l_rest = ctx.enter_context(tc.tile_pool(name="l_rest", bufs=1))
-        tok_pool = ctx.enter_context(tc.tile_pool(name="tok", bufs=4))
-
         steps = [(r, 2) for r in range(0, ROWS - TAPER, 2)] + [
             (r, 1) for r in range(ROWS - TAPER, ROWS)
         ]
@@ -267,10 +266,10 @@ def tile_jointnet_t_kernel(
             bi = batch_of_row[r]
             n = BATCH_ROWS[bi]
             if r == row0_of[bi]:
-                pool = l_first if bi == 0 else l_rest
-                Ls[bi] = pool.tile([P, n, V], F32, name="L%d" % bi)
+                Ls[bi] = l_pool.tile([P, max(BATCH_ROWS), V], F32, name="L")
                 negms[bi] = small.tile([P, n], F32, name="negm")
                 ssums[bi] = small.tile([P, n], F32, name="ssum")
+                misc[bi] = {}
             k = r - row0_of[bi]
             nc.vector.tensor_tensor(
                 out=Ls[bi][:, k : k + nu, :],
@@ -301,55 +300,104 @@ def tile_jointnet_t_kernel(
                     accum_out=ssums[bi][:, k + q : k + q + 1],
                 )
 
-        def row_a(bi):
+        def row_tile(bi, name, pair=False):
             n = BATCH_ROWS[bi]
-            l0 = Ls[bi][:, :, 0]
-            nab = small.tile([P, n], F32, name="nab")
-            t1 = small.tile([P, n], F32, name="t1")
-            mn = small.tile([P, n], F32, name="mn")
+            shape = [P, 2, n] if pair else [P, n]
+            misc[bi][name] = small.tile(shape, F32, name=name)
+            return misc[bi][name]
+
+        def blank(bi):
+            return Ls[bi][:, 0 : BATCH_ROWS[bi], 0]
+
+        def row_mn(bi):
+            nc.vector.tensor_scalar_min(out=row_tile(bi, "mn")[:], in0=blank(bi), scalar1=0.0)
+
+        def row_nab(bi):
             nc.vector.scalar_tensor_tensor(
-                out=nab[:], in0=l0, scalar=-1.0, in1=l0, op0=ALU.mult, op1=ALU.min
+                out=row_tile(bi, "nab")[:], in0=blank(bi), scalar=-1.0, in1=blank(bi),
+                op0=ALU.mult, op1=ALU.min,
             )
+
+        def row_t1(bi):
             nc.vector.scalar_tensor_tensor(
-                out=t1[:], in0=l0, scalar=0.0, in1=negms[bi][:], op0=ALU.max, op1=ALU.subtract
+                out=row_tile(bi, "t1")[:], in0=blank(bi), scalar=0.0, in1=negms[bi][:],
+                op0=ALU.max, op1=ALU.subtract,
             )
-            nc.vector.tensor_scalar_min(out=mn[:], in0=l0, scalar1=0.0)
-            misc[bi] = {"nab": nab, "t1": t1, "mn": mn}
 
-        def row_b(bi):
-            ex = small.tile([P, BATCH_ROWS[bi]], F32, name="ex")
-            nc.scalar.activation(out=ex[:], in_=misc[bi]["nab"][:], func=ACT.Exp)
-            misc[bi]["ex"] = ex
+        def row_ex(bi):
+            nc.scalar.activation(out=row_tile(bi, "ex")[:], in_=misc[bi]["nab"][:], func=ACT.Exp)
 
-        def row_c(bi):
-            sq = small.tile([P, 2, BATCH_ROWS[bi]], F32, name="sq")
-            nc.vector.tensor_scalar_add(out=sq[:, 0, :], in0=misc[bi]["ex"][:], scalar1=1.0)
-            nc.vector.tensor_tensor(
-                out=sq[:, 1, :], in0=sq[:, 0, :], in1=ssums[bi][:], op=ALU.mult
-            )
-            misc[bi]["sq"] = sq
-
-        def row_d(bi):
-            lns = small.tile([P, 2, BATCH_ROWS[bi]], F32, name="lns")
-            nc.scalar.activation(out=lns[:], in_=misc[bi]["sq"][:], func=ACT.Ln)
-            misc[bi]["lns"] = lns
-
-        def row_e(bi):
-            n = BATCH_ROWS[bi]
-            lns = misc[bi]["lns"]
-            negc = small.tile([P, n], F32, name="negc")
-            o0 = small.tile([P, n], F32, name="o0")
+        def row_sq(bi):
+            x = row_tile(bi, "x", True)
+            nc.vector.tensor_scalar_add(out=x[:, 0, :], in0=misc[bi]["ex"][:], scalar1=1.0)
             nc.vector.scalar_tensor_tensor(
-                out=negc[:], in0=misc[bi]["t1"][:], scalar=-1.0, in1=lns[:, 1, :],
-                op0=ALU.mult, op1=ALU.subtract,
+                out=x[:, 1, :], in0=misc[bi]["ex"][:], scalar=1.0, in1=ssums[bi][:],
+                op0=ALU.add, op1=ALU.mult,
             )
+
+        def row_v0(bi):
+            nc.vector.tensor_scalar(
+                out=row_tile(bi, "v0", True)[:],
+                in0=misc[bi]["x"][:].bitcast(I32),
+                scalar1=3.0 * LOG2E_STEP, scalar2=3.0 * LOG_SHIFT, op0=ALU.mult, op1=ALU.add,
+            )
+
+        def row_exp(bi, i):
+            nc.scalar.activation(
+                out=row_tile(bi, "e%d" % i, True)[:], in_=misc[bi]["v%d" % i][:],
+                func=ACT.Exp, scale=-1.0 / 3.0,
+            )
+
+        def row_w(bi, i):
             nc.vector.tensor_tensor(
-                out=o0[:], in0=misc[bi]["mn"][:], in1=lns[:, 0, :], op=ALU.subtract
+                out=row_tile(bi, "w%d" % i, True)[:], in0=misc[bi]["x"][:],
+                in1=misc[bi]["e%d" % i][:], op=ALU.mult,
             )
+
+        def row_u(bi, i):
+            w = misc[bi]["w%d" % i]
+            nc.vector.scalar_tensor_tensor(
+                out=row_tile(bi, "u%d" % i, True)[:], in0=w[:], scalar=-4.5, in1=w[:],
+                op0=ALU.add, op1=ALU.mult,
+            )
+
+        def row_t(bi, i):
+            nc.vector.scalar_tensor_tensor(
+                out=row_tile(bi, "t%d" % (i + 2), True)[:], in0=misc[bi]["u%d" % i][:],
+                scalar=9.0, in1=misc[bi]["w%d" % i][:], op0=ALU.add, op1=ALU.mult,
+            )
+
+        def row_v(bi, i):
+            nc.vector.scalar_tensor_tensor(
+                out=row_tile(bi, "v%d" % (i + 1), True)[:], in0=misc[bi]["t%d" % (i + 2)][:],
+                scalar=-5.5, in1=misc[bi]["v%d" % i][:], op0=ALU.add, op1=ALU.add,
+            )
+            misc[bi]["y"] = misc[bi]["v%d" % (i + 1)]
+            misc[bi]["factor"] = -1.0 / 3.0
+
+        def row_ln(bi):
+            nc.scalar.activation(
+                out=row_tile(bi, "y", True)[:], in_=misc[bi]["x"][:], func=ACT.Ln
+            )
+            misc[bi]["factor"] = -1.0
+
+        def row_negc(bi):
+            nc.vector.scalar_tensor_tensor(
+                out=row_tile(bi, "negc")[:], in0=misc[bi]["y"][:, 1, :], scalar=misc[bi]["factor"],
+                in1=misc[bi]["t1"][:], op0=ALU.mult, op1=ALU.subtract,
+            )
+
+        def row_o0(bi):
+            nc.vector.scalar_tensor_tensor(
+                out=row_tile(bi, "o0")[:], in0=misc[bi]["y"][:, 0, :], scalar=misc[bi]["factor"],
+                in1=misc[bi]["mn"][:], op0=ALU.mult, op1=ALU.add,
+            )
+
+        def row_blank(bi):
             nc.vector.tensor_tensor(
-                out=Ls[bi][:, :, 0], in0=o0[:], in1=negc[:], op=ALU.subtract
+                out=blank(bi), in0=misc[bi]["o0"][:], in1=misc[bi]["negc"][:], op=ALU.subtract
             )
-            misc[bi]["negc"] = negc
+            ready.extend(range(row0_of[bi], row0_of[bi] + BATCH_ROWS[bi]))
 
         ready = []
         taken = [0]
@@ -405,42 +453,75 @@ def tile_jointnet_t_kernel(
                     )
                     stored[r] = True
 
+        def first(work):
+            return lambda bi: work(bi, 0)
+
+        def second(work):
+            return lambda bi: work(bi, 1)
+
+        fillers = {}
+        for bi in range(n_batches):
+            e = last_step_of[bi]
+            plan = [(3, 4, row_mn), (3, 4, row_nab), (3, 4, row_t1), (4, 4, row_sq)]
+            if bi < n_batches - 1:
+                plan += [(5, 1, row_v0), (5, 3, first(row_w)), (5, 4, first(row_u))]
+                plan += [(6, 0, first(row_t)), (6, 1, first(row_v)), (6, 3, second(row_w))]
+                plan += [(6, 4, second(row_u)), (7, 0, second(row_t)), (7, 1, second(row_v))]
+                plan += [(7, 2, row_negc), (7, 3, row_o0), (7, 4, row_blank)]
+            else:
+                plan += [(6, 0, row_negc), (6, 1, row_o0), (6, 2, row_blank)]
+            for delay, place, work in plan:
+                fillers.setdefault((e + delay, place), []).append((work, bi))
+
+        def fill(w, place):
+            for work, bi in fillers.get((w, place), []):
+                work(bi)
+
+        def quota(w):
+            if w < 44:
+                return 2, 0, 0
+            if w < NS:
+                return 2, 1, 0
+            return 2, 3, 2
+
         for s in range(LEAD):
             tanh_part(s, 0)
         for s in range(LEAD):
             tanh_part(s, 1)
-        for w in range(NS + 9):
-            late = w >= LATE_FROM
-            rows_a = take(QUOTA_LATE[2] if late else QUOTA[2])
+        for w in range(NS + 10):
+            on_gpsimd, on_vector, on_scalar = quota(w)
+            rows_a = take(on_scalar)
             if LEAD <= w < NS:
                 tanh_part(w, 0)
             if 0 <= w - 4 < NS:
                 exps(w - 4)
             for bi in range(n_batches):
                 if w - 4 == last_step_of[bi]:
-                    row_b(bi)
+                    row_ex(bi)
                 if w - 5 == last_step_of[bi]:
-                    row_d(bi)
+                    if bi == n_batches - 1:
+                        row_ln(bi)
             subtract_rows(rows_a, "A")
-            if LEAD <= w < NS:
-                tanh_part(w, 1)
+            fill(w, 0)
             if 0 <= w - 1 < NS:
                 regroup(w - 1)
+            fill(w, 1)
+            for bi in range(n_batches - 1):
+                if w - 5 == last_step_of[bi]:
+                    row_exp(bi, 0)
+                if w - 6 == last_step_of[bi]:
+                    row_exp(bi, 1)
+            if LEAD <= w < NS:
+                tanh_part(w, 1)
             if 0 <= w - 2 < NS:
                 quantise_h(w - 2)
                 logits(w - 2)
-            for bi in range(n_batches):
-                if w - 6 == last_step_of[bi]:
-                    row_e(bi)
-                    ready.extend(range(row0_of[bi], row0_of[bi] + BATCH_ROWS[bi]))
-            subtract_rows(take(QUOTA_LATE[0] if late else QUOTA[0]), "G")
+            fill(w, 2)
+            subtract_rows(take(on_gpsimd), "G")
             if 0 <= w - 3 < NS:
                 bias_and_max(w - 3)
-            for bi in range(n_batches):
-                if w - 3 == last_step_of[bi]:
-                    row_a(bi)
-                if w - 4 == last_step_of[bi]:
-                    row_c(bi)
-            subtract_rows(take(QUOTA_LATE[1] if late else QUOTA[1]), "V")
+            fill(w, 3)
+            fill(w, 4)
+            subtract_rows(take(on_vector), "V")
             stores()
         assert taken[0] == ROWS and len(stored) == ROWS // 4

@@ -44,7 +44,7 @@ def tile_jointnet_t_kernel(
         cd_pool = ctx.enter_context(tc.tile_pool(name="cd", bufs=3))
         small = ctx.enter_context(tc.tile_pool(name="small", bufs=2))
         junk_pool = ctx.enter_context(tc.tile_pool(name="junk", bufs=2))
-        l_pool = ctx.enter_context(tc.tile_pool(name="l_pool", bufs=3))
+        l_pool = ctx.enter_context(tc.tile_pool(name="l_pool", bufs=4))
         tok_pool = ctx.enter_context(tc.tile_pool(name="tok", bufs=4))
 
         xc = const.tile([P, 3 * P], U32, name="xc", align_bytes=64)
@@ -261,7 +261,7 @@ def tile_jointnet_t_kernel(
                         stop=(g == 1),
                     )
 
-        def bias_and_max(s):
+        def bias_add(s):
             r, nu = steps[s]
             bi = batch_of_row[r]
             n = BATCH_ROWS[bi]
@@ -277,6 +277,11 @@ def tile_jointnet_t_kernel(
                 in1=bfc[:].unsqueeze(1).to_broadcast([P, nu, V]),
                 op=ALU.add,
             )
+
+        def row_max(s):
+            r, nu = steps[s]
+            bi = batch_of_row[r]
+            k = r - row0_of[bi]
             nc.vector.tensor_reduce(
                 out=negms[bi][:, k : k + nu],
                 in_=Ls[bi][:, k : k + nu, 1:V],
@@ -421,7 +426,7 @@ def tile_jointnet_t_kernel(
             k0 = rows[0] - row0_of[bi]
             negc = misc[bi]["negc"]
             if engine == "G":
-                tok = tok_pool.tile([P, 2], F32, name="tok")
+                tok = tok_pool.tile([P, 4], F32, name="tok")
                 nc.vector.tensor_copy(
                     out=tok[:, 0 : len(rows)], in_=negc[:, k0 : k0 + len(rows)]
                 )
@@ -462,14 +467,14 @@ def tile_jointnet_t_kernel(
         fillers = {}
         for bi in range(n_batches):
             e = last_step_of[bi]
-            plan = [(3, 4, row_mn), (3, 4, row_nab), (3, 4, row_t1), (4, 4, row_sq)]
+            plan = [(4, 0, row_mn), (4, 1, row_nab), (5, 1, row_t1), (6, 0, row_sq)]
             if bi < n_batches - 1:
-                plan += [(5, 1, row_v0), (5, 3, first(row_w)), (5, 4, first(row_u))]
-                plan += [(6, 0, first(row_t)), (6, 1, first(row_v)), (6, 3, second(row_w))]
-                plan += [(6, 4, second(row_u)), (7, 0, second(row_t)), (7, 1, second(row_v))]
-                plan += [(7, 2, row_negc), (7, 3, row_o0), (7, 4, row_blank)]
+                plan += [(6, 1, row_v0), (7, 0, first(row_w)), (7, 1, first(row_u))]
+                plan += [(7, 2, first(row_t)), (7, 3, first(row_v)), (9, 0, second(row_w))]
+                plan += [(9, 1, second(row_u)), (9, 2, second(row_t)), (9, 3, second(row_v))]
+                plan += [(10, 0, row_negc), (10, 1, row_o0), (10, 2, row_blank)]
             else:
-                plan += [(6, 0, row_negc), (6, 1, row_o0), (6, 2, row_blank)]
+                plan += [(7, 0, row_negc), (7, 1, row_o0), (7, 2, row_blank)]
             for delay, place, work in plan:
                 fillers.setdefault((e + delay, place), []).append((work, bi))
 
@@ -481,35 +486,35 @@ def tile_jointnet_t_kernel(
             if w < 44:
                 return 2, 0, 0
             if w < NS:
-                return 2, 1, 0
+                return 3, 0, 0
             return 2, 3, 2
 
         for s in range(LEAD):
             tanh_part(s, 0)
         for s in range(LEAD):
             tanh_part(s, 1)
-        for w in range(NS + 10):
+        for w in range(NS + 11):
             on_gpsimd, on_vector, on_scalar = quota(w)
             rows_a = take(on_scalar)
             if LEAD <= w < NS:
                 tanh_part(w, 0)
-            if 0 <= w - 4 < NS:
-                exps(w - 4)
+            if 0 <= w - 5 < NS:
+                exps(w - 5)
             for bi in range(n_batches):
-                if w - 4 == last_step_of[bi]:
-                    row_ex(bi)
                 if w - 5 == last_step_of[bi]:
-                    if bi == n_batches - 1:
-                        row_ln(bi)
+                    row_ex(bi)
             subtract_rows(rows_a, "A")
             fill(w, 0)
             if 0 <= w - 1 < NS:
                 regroup(w - 1)
             fill(w, 1)
-            for bi in range(n_batches - 1):
-                if w - 5 == last_step_of[bi]:
-                    row_exp(bi, 0)
+            for bi in range(n_batches):
                 if w - 6 == last_step_of[bi]:
+                    if bi == n_batches - 1:
+                        row_ln(bi)
+                    else:
+                        row_exp(bi, 0)
+                if w - 8 == last_step_of[bi] and bi < n_batches - 1:
                     row_exp(bi, 1)
             if LEAD <= w < NS:
                 tanh_part(w, 1)
@@ -519,9 +524,10 @@ def tile_jointnet_t_kernel(
             fill(w, 2)
             subtract_rows(take(on_gpsimd), "G")
             if 0 <= w - 3 < NS:
-                bias_and_max(w - 3)
+                bias_add(w - 3)
             fill(w, 3)
-            fill(w, 4)
+            if 0 <= w - 4 < NS:
+                row_max(w - 4)
             subtract_rows(take(on_vector), "V")
             stores()
         assert taken[0] == ROWS and len(stored) == ROWS // 4

@@ -17,11 +17,10 @@ AX = mybir.AxisListType
 P = 128
 B, T, U, K1, F, V = 2, 128, 64, 512, 1024, 256
 NCH = 8
-ROWS = B * U
+TB, UG = T // 32, U // 16
+NB = B * TB * UG
+ROWS = 4 * NB
 BATCH_ROWS = [24, 24, 24, 24, 16, 8, 8]
-TAPER = 4
-LEAD = 3
-PIN = True
 LOG2E_STEP = math.log(2.0) / 2**23
 LOG_SHIFT = -127.0 * math.log(2.0) + 0.0298
 
@@ -33,38 +32,88 @@ def tile_jointnet_t_kernel(
 ):
     nc = tc.nc
     with ExitStack() as ctx:
-        if PIN:
-            ctx.enter_context(tc.manual_schedule())
+        ctx.enter_context(tc.manual_schedule())
         const = ctx.enter_context(tc.tile_pool(name="const", bufs=1))
-        ps_tr = ctx.enter_context(tc.psum_pool(name="ps_tr", bufs=3))
-        ps_s1 = ctx.enter_context(tc.psum_pool(name="ps_s1", bufs=2))
-        ps_lg = ctx.enter_context(tc.psum_pool(name="ps_lg", bufs=3))
-        hp_pool = ctx.enter_context(tc.tile_pool(name="hp", bufs=LEAD + 2))
+        ps_cb = ctx.enter_context(tc.psum_pool(name="ps_cb", bufs=4))
+        hp_pool = ctx.enter_context(tc.tile_pool(name="hp", bufs=4))
         gr_pool = ctx.enter_context(tc.tile_pool(name="gr", bufs=3))
-        cd_pool = ctx.enter_context(tc.tile_pool(name="cd", bufs=3))
-        small = ctx.enter_context(tc.tile_pool(name="small", bufs=2))
+        cd_pool = ctx.enter_context(tc.tile_pool(name="cd", bufs=6))
+        small = ctx.enter_context(tc.tile_pool(name="small", bufs=3))
         junk_pool = ctx.enter_context(tc.tile_pool(name="junk", bufs=2))
-        l_pool = ctx.enter_context(tc.tile_pool(name="l_pool", bufs=4))
+        l_early = ctx.enter_context(tc.tile_pool(name="l_early", bufs=2))
         tok_pool = ctx.enter_context(tc.tile_pool(name="tok", bufs=4))
 
-        xc = const.tile([P, 3 * P], U32, name="xc", align_bytes=64)
-        xs = const.tile([P, 3 * P], U8, name="xs", align_bytes=64)
+        enc_c = const.tile([P, B * T], U32, name="enc_c", align_bytes=64)
+        enc_s = const.tile([P, B * T], U8, name="enc_s", align_bytes=64)
+        dec_c = const.tile([P, 4 * B * U], U32, name="dec_c", align_bytes=64)
+        dec_s = const.tile([P, 4 * B * U], U8, name="dec_s", align_bytes=64)
+        enc_xc = const.tile([P, B * TB, 512], U32, name="enc_xc", align_bytes=64)
+        enc_xs = const.tile([P, B * TB, 512], U8, name="enc_xs", align_bytes=64)
+        dec_xc = const.tile([P, B * UG, 512], U32, name="dec_xc", align_bytes=64)
+        dec_xs = const.tile([P, B * UG, 512], U8, name="dec_xs", align_bytes=64)
         wec = const.tile([P, NCH * P], U32, name="wec", align_bytes=64)
         wes = const.tile([P, NCH * P], U8, name="wes", align_bytes=64)
         wdc = const.tile([P, NCH * P], U32, name="wdc", align_bytes=64)
         wds = const.tile([P, NCH * P], U8, name="wds", align_bytes=64)
         wfc = const.tile([P, 4 * P], U32, name="wfc", align_bytes=64)
         wfs = const.tile([P, 4 * P], U8, name="wfs", align_bytes=64)
-        encB = const.tile([P, NCH, B * T], F32, name="encB")
-        decB = const.tile([P, NCH, B * U], F32, name="decB")
-        benc = const.tile([P, NCH], F32, name="benc")
-        bdec = const.tile([P, NCH], F32, name="bdec")
+        bsum = const.tile([P, NCH], F32, name="bsum")
         bfc = const.tile([P, V], F32, name="bfc")
         ident = const.tile([P, P], F32, name="ident")
         warm_in = const.tile([P, 1], F32, name="warm_in")
         warm_out = const.tile([P, 1], F32, name="warm_out")
 
-        with tc.tile_pool(name="stage", bufs=1) as stage:
+        def repeat_enc(i):
+            nc.vector.tensor_copy(
+                out=enc_xc[:, i, :].bitcast(I32).rearrange("p (r t) -> p r t", t=32),
+                in_=enc_c[:, 32 * i : 32 * i + 32].bitcast(I32).unsqueeze(1).to_broadcast([P, 16, 32]),
+            )
+            nc.vector.tensor_copy(
+                out=enc_xs[:, i, :].bitcast(I32).rearrange("p (r t) -> p r t", t=8),
+                in_=enc_s[:, 32 * i : 32 * i + 32].bitcast(I32).unsqueeze(1).to_broadcast([P, 16, 8]),
+            )
+
+        def repeat_dec(i):
+            codes = dec_c[:, 64 * i : 64 * i + 64].bitcast(I32)
+            codes = codes.rearrange("p (uq m r) -> p m uq r", m=4, r=4)[:, :, :, 0:1]
+            scales = dec_s[:, 64 * i : 64 * i + 64].bitcast(I32)
+            scales = scales.rearrange("p (uq m) -> p m uq", m=4).unsqueeze(3)
+            nc.vector.tensor_copy(
+                out=dec_xc[:, i, :].bitcast(I32).rearrange("p (m uq t) -> p m uq t", m=4, t=32),
+                in_=codes.to_broadcast([P, 4, 4, 32]),
+            )
+            nc.vector.tensor_copy(
+                out=dec_xs[:, i, :].bitcast(I32).rearrange("p (m uq t) -> p m uq t", m=4, t=8),
+                in_=scales.to_broadcast([P, 4, 4, 8]),
+            )
+
+        HALVES = [(0, 0), (1, 0), (0, 1), (1, 1)] + [(n, g) for n in range(2, NB) for g in range(2)]
+        NS = len(HALVES)
+        sums = {}
+
+        def sum_matmuls(s):
+            n, g = HALVES[s]
+            e = n // UG
+            d = (n // (TB * UG)) * UG + n % UG
+            for j in range(4):
+                c = 4 * g + j
+                cols = slice(c * P, (c + 1) * P)
+                sums[s, j] = ps_cb.tile([P, 512], F32, name="sum")
+                for wc, ws, xc, xs, first in (
+                    (wec, wes, enc_xc[:, e, :], enc_xs[:, e, :], True),
+                    (wdc, wds, dec_xc[:, d, :], dec_xs[:, d, :], False),
+                ):
+                    nc.tensor.matmul_mx(
+                        out=sums[s, j][:],
+                        lhsT=wc[:, cols].bitcast(FP8X4),
+                        lhsT_scale=ws[:, cols],
+                        rhs=xc.bitcast(FP8X4),
+                        rhs_scale=xs,
+                        start=first,
+                        stop=not first,
+                    )
+
+        with tc.tile_pool(name="stage", bufs=1) as stage, tc.psum_pool(name="ps_tr", bufs=4) as ps_tr:
             benc_bf = stage.tile([P, NCH], BF16, name="benc_bf")
             bdec_bf = stage.tile([P, NCH], BF16, name="bdec_bf")
             bfc_bf = stage.tile([P, V], BF16, name="bfc_bf")
@@ -94,10 +143,13 @@ def tile_jointnet_t_kernel(
             nc.sync.dma_start(out=bfc_bf[:], in_=b_fc.partition_broadcast(P))
 
             make_identity(nc, ident[:])
+            nc.gpsimd.memset(enc_s[:].bitcast(U32), 0)
+            nc.gpsimd.memset(dec_s[:].bitcast(U32), 0)
             nc.vector.memset(warm_in[:], 0.0)
             nc.scalar.activation(out=warm_out[:], in_=warm_in[:], func=ACT.Tanh)
 
-            xg = stage.tile([P, 3 * 512], BF16, name="xg", align_bytes=64)
+            eg = stage.tile([P, 2 * 512], BF16, name="eg", align_bytes=64)
+            dg = stage.tile([P, 4 * 512], BF16, name="dg", align_bytes=64)
             weg = stage.tile([P, NCH * 512], BF16, name="weg", align_bytes=64)
             wdg = stage.tile([P, NCH * 512], BF16, name="wdg", align_bytes=64)
             wfg = stage.tile([P, 4 * 512], BF16, name="wfg", align_bytes=64)
@@ -106,26 +158,36 @@ def tile_jointnet_t_kernel(
                 w32 = rows.bitcast(F32)
                 return [w32[:, 0:P], w32[:, P : 2 * P]]
 
-            def transpose_tiles(views, dst, on_scalar):
-                n = len(views)
+            def transpose_in(views):
                 tr = ps_tr.tile([P, 2, 2, P], F32, name="tr")
-                for s in range(n):
+                for i in range(len(views)):
                     for u in range(2):
-                        nc.tensor.transpose(tr[:, s, u, :], views[s][u], ident[:])
-                o = dst.bitcast(F32).rearrange("p (s r u) -> p s r u", s=n, u=2)
-                i = tr[:, 0:n, :, :].rearrange("p s u r -> p s r u")
-                if on_scalar:
-                    nc.scalar.copy(out=o, in_=i)
-                else:
-                    nc.vector.tensor_copy(out=o, in_=i)
+                        nc.tensor.transpose(tr[:, i, u, :], views[i][u], ident[:])
+                return tr
 
-            def transpose_weights(w_sb, grouped, g, on_scalar):
-                for c in (4 * g, 4 * g + 2):
-                    transpose_tiles(
-                        [halves(w_sb[:, c, :]), halves(w_sb[:, c + 1, :])],
-                        grouped[:, c * 512 : (c + 2) * 512],
-                        on_scalar,
-                    )
+            def copy_out(dst, src, on_scalar):
+                if on_scalar:
+                    nc.scalar.copy(out=dst, in_=src)
+                else:
+                    nc.vector.tensor_copy(out=dst, in_=src)
+
+            def regrouped(tr, dst, on_scalar):
+                n = dst.shape[1] // 512
+                copy_out(
+                    dst.bitcast(F32).rearrange("p (s r u) -> p s r u", s=n, u=2),
+                    tr[:, 0:n, :, :].rearrange("p s u r -> p s r u"),
+                    on_scalar,
+                )
+
+            def transpose_weights(w_sb, g):
+                return [
+                    (c, transpose_in([halves(w_sb[:, c, :]), halves(w_sb[:, c + 1, :])]))
+                    for c in (4 * g, 4 * g + 2)
+                ]
+
+            def regroup_weights(trs, grouped, on_scalar):
+                for c, tr in trs:
+                    regrouped(tr, grouped[:, c * 512 : (c + 2) * 512], on_scalar)
 
             def quantise(grouped, codes, scales, first, count):
                 nc.vector.quantize_mx(
@@ -134,127 +196,91 @@ def tile_jointnet_t_kernel(
                     in_=grouped[:, first * 512 : (first + count) * 512],
                 )
 
-            def input_matmuls(c, on_scalar):
-                cols = slice(c * P, (c + 1) * P)
-                s1 = ps_s1.tile([P, 384], F32, name="s1")
-                nc.tensor.matmul_mx(
-                    out=s1[:, 0:256],
-                    lhsT=wec[:, cols].bitcast(FP8X4),
-                    lhsT_scale=wes[:, cols],
-                    rhs=xc[:, 0:256].bitcast(FP8X4),
-                    rhs_scale=xs[:, 0:256],
-                    start=True,
-                    stop=True,
-                )
-                nc.tensor.matmul_mx(
-                    out=s1[:, 256:384],
-                    lhsT=wdc[:, cols].bitcast(FP8X4),
-                    lhsT_scale=wds[:, cols],
-                    rhs=xc[:, 256:384].bitcast(FP8X4),
-                    rhs_scale=xs[:, 256:384],
-                    start=True,
-                    stop=True,
-                )
-                for dst, src, bias in (
-                    (decB[:, c, :], s1[:, 256:384], bdec[:, c : c + 1]),
-                    (encB[:, c, :], s1[:, 0:256], benc[:, c : c + 1]),
-                ):
-                    if on_scalar:
-                        nc.scalar.activation(out=dst, in_=src, func=ACT.Identity, bias=bias, scale=1.0)
-                    else:
-                        nc.vector.tensor_scalar(
-                            out=dst, in0=src, scalar1=bias, scalar2=None, op0=ALU.add
-                        )
-
-            transpose_tiles(
-                [halves(enc_sb[:, 0, :]), halves(enc_sb[:, 1, :])], xg[:, 0:1024], True
+            enc_tr = transpose_in([halves(enc_sb[:, 0, :]), halves(enc_sb[:, 1, :])])
+            dec_tr = transpose_in([halves(dec_sb[:, :])])
+            we_tr = transpose_weights(wenc_sb, 0)
+            regrouped(enc_tr, eg[:], True)
+            nc.scalar.copy(
+                out=dg[:].bitcast(F32).rearrange("p (c r u) -> p c r u", r=4, u=2),
+                in_=dec_tr[:, 0, :, :].rearrange("p u c -> p c u").unsqueeze(2).to_broadcast([P, P, 4, 2]),
             )
-            transpose_tiles([halves(dec_sb[:, :])], xg[:, 1024:1536], False)
-            nc.vector.tensor_copy(out=benc[:], in_=benc_bf[:])
-            nc.vector.tensor_copy(out=bdec[:], in_=bdec_bf[:])
-            quantise(xg, xc, xs, 0, 2)
-            quantise(xg, xc, xs, 2, 1)
-            transpose_weights(wenc_sb, weg, 0, True)
-            transpose_weights(wdec_sb, wdg, 0, False)
+            wd_tr = transpose_weights(wdec_sb, 0)
+            regroup_weights(we_tr, weg, True)
+            nc.vector.tensor_tensor(out=bsum[:], in0=benc_bf[:], in1=bdec_bf[:], op=ALU.add)
+            quantise(eg, enc_c, enc_s, 0, 2)
+            quantise(dg, dec_c, dec_s, 0, 4)
+            repeat_enc(0)
+            repeat_dec(0)
+            regroup_weights(wd_tr, wdg, False)
             quantise(weg, wec, wes, 0, 4)
             quantise(wdg, wdc, wds, 0, 4)
-            transpose_weights(wenc_sb, weg, 1, True)
-            for c in range(4):
-                input_matmuls(c, c % 2 == 1)
-            transpose_weights(wdec_sb, wdg, 1, False)
+            repeat_dec(1)
+            we_tr = transpose_weights(wenc_sb, 1)
+            wd_tr = transpose_weights(wdec_sb, 1)
+            sum_matmuls(0)
+            regroup_weights(we_tr, weg, False)
+            regroup_weights(wd_tr, wdg, False)
             quantise(weg, wec, wes, 4, 4)
             quantise(wdg, wdc, wds, 4, 4)
-            for c in range(4, 8):
-                input_matmuls(c, False)
             for g in range(2):
                 views = []
                 for h in range(2):
                     w32 = wfc_sb[:, h, :].bitcast(F32).rearrange("p (g w u) -> p g w u", g=2, u=2)
                     views.append([w32[:, g, :, 0], w32[:, g, :, 1]])
-                transpose_tiles(views, wfg[:, g * 1024 : (g + 1) * 1024], False)
+                fc_tr = transpose_in(views)
+                regrouped(fc_tr, wfg[:, g * 1024 : (g + 1) * 1024], False)
             quantise(wfg, wfc, wfs, 0, 4)
             nc.vector.tensor_copy(out=bfc[:], in_=bfc_bf[:])
 
-        steps = [(r, 2) for r in range(0, ROWS - TAPER, 2)] + [
-            (r, 1) for r in range(ROWS - TAPER, ROWS)
-        ]
-        NS = len(steps)
+        l_late = ctx.enter_context(tc.tile_pool(name="l_late", bufs=2))
+        ps_lg = ctx.enter_context(tc.psum_pool(name="ps_lg", bufs=4))
+
         row0_of = [sum(BATCH_ROWS[:bi]) for bi in range(len(BATCH_ROWS))]
         batch_of_row = []
         for bi, n in enumerate(BATCH_ROWS):
             batch_of_row.extend([bi] * n)
-        last_step_of = [
-            max(s for s in range(NS) if batch_of_row[steps[s][0]] == bi)
-            for bi in range(len(BATCH_ROWS))
-        ]
         n_batches = len(BATCH_ROWS)
+        last_step_of = [(row0_of[bi] + BATCH_ROWS[bi]) // 2 - 1 for bi in range(n_batches)]
         hPs, groupeds, codes, lgs = {}, {}, {}, {}
         Ls, negms, ssums, misc = {}, {}, {}, {}
 
-        def tanh_part(s, g):
-            r, nu = steps[s]
-            b = r // U
-            if g == 0:
-                hPs[s] = hp_pool.tile([P, 4, 2 * nu * P], BF16, name="hP")
+        def tanh_half(s):
+            g = HALVES[s][1]
+            hPs[s] = hp_pool.tile([P, 4, 512], BF16, name="hP")
             for j in range(4):
-                for q in range(nu):
-                    x = q * 2 + g
-                    nc.scalar.activation(
-                        out=hPs[s][:, j, x * P : (x + 1) * P],
-                        in_=encB[:, 4 * g + j, b * T : (b + 1) * T],
-                        func=ACT.Tanh,
-                        bias=decB[:, 4 * g + j, r + q : r + q + 1],
-                        scale=1.0,
-                    )
+                nc.scalar.activation(
+                    out=hPs[s][:, j, :],
+                    in_=sums[s, j][:],
+                    func=ACT.Tanh,
+                    bias=bsum[:, 4 * g + j : 4 * g + j + 1],
+                    scale=1.0,
+                )
 
         def regroup(s):
-            nu = steps[s][1]
-            groupeds[s] = gr_pool.tile([P, 8 * nu * P], BF16, name="grouped", align_bytes=64)
+            groupeds[s] = gr_pool.tile([P, 4 * 512], BF16, name="grouped", align_bytes=64)
             nc.vector.tensor_copy(
                 out=groupeds[s][:].rearrange("p (c i j) -> p c j i", i=4, j=4),
                 in_=hPs[s][:].rearrange("p j (c i) -> p c j i", i=4),
             )
 
         def quantise_h(s):
-            nu = steps[s][1]
-            words = cd_pool.tile([P, 2 * nu * P], U32, name="words", align_bytes=64)
-            planes = cd_pool.tile([P, 2 * nu * P], U8, name="planes", align_bytes=64)
-            codes[s] = (words, planes)
+            words = cd_pool.tile([P, 512], U32, name="words", align_bytes=64)
+            planes = cd_pool.tile([P, 512], U8, name="planes", align_bytes=64)
+            codes[HALVES[s]] = (words, planes)
             nc.vector.quantize_mx(
                 out=words[:].bitcast(FP8X4), scales=planes[:], in_=groupeds[s][:]
             )
 
         def logits(s):
-            nu = steps[s][1]
-            words, planes = codes[s]
-            lgs[s] = ps_lg.tile([P, nu, V], F32, name="lg")
-            for q in range(nu):
+            lgs[s] = ps_lg.tile([P, 2, V], F32, name="lg")
+            for q in range(2):
+                m = 2 * (s % 2) + q
                 for g in range(2):
-                    x = q * 2 + g
+                    words, planes = codes[s // 2, g]
                     nc.tensor.matmul_mx(
                         out=lgs[s][:, q, :],
-                        lhsT=words[:, x * P : (x + 1) * P].bitcast(FP8X4),
-                        lhsT_scale=planes[:, x * P : (x + 1) * P],
+                        lhsT=words[:, m * P : (m + 1) * P].bitcast(FP8X4),
+                        lhsT_scale=planes[:, m * P : (m + 1) * P],
                         rhs=wfc[:, g * V : (g + 1) * V].bitcast(FP8X4),
                         rhs_scale=wfs[:, g * V : (g + 1) * V],
                         start=(g == 0),
@@ -262,39 +288,40 @@ def tile_jointnet_t_kernel(
                     )
 
         def bias_add(s):
-            r, nu = steps[s]
+            r = 2 * s
             bi = batch_of_row[r]
             n = BATCH_ROWS[bi]
             if r == row0_of[bi]:
-                Ls[bi] = l_pool.tile([P, max(BATCH_ROWS), V], F32, name="L")
+                pool = l_early if bi % 4 < 2 else l_late
+                Ls[bi] = pool.tile([P, max(BATCH_ROWS), V], F32, name="L")
                 negms[bi] = small.tile([P, n], F32, name="negm")
                 ssums[bi] = small.tile([P, n], F32, name="ssum")
                 misc[bi] = {}
             k = r - row0_of[bi]
             nc.vector.tensor_tensor(
-                out=Ls[bi][:, k : k + nu, :],
+                out=Ls[bi][:, k : k + 2, :],
                 in0=lgs[s][:],
-                in1=bfc[:].unsqueeze(1).to_broadcast([P, nu, V]),
+                in1=bfc[:].unsqueeze(1).to_broadcast([P, 2, V]),
                 op=ALU.add,
             )
 
         def row_max(s):
-            r, nu = steps[s]
+            r = 2 * s
             bi = batch_of_row[r]
             k = r - row0_of[bi]
             nc.vector.tensor_reduce(
-                out=negms[bi][:, k : k + nu],
-                in_=Ls[bi][:, k : k + nu, 1:V],
+                out=negms[bi][:, k : k + 2],
+                in_=Ls[bi][:, k : k + 2, 1:V],
                 axis=AX.X,
                 op=ALU.max,
                 negate=True,
             )
 
         def exps(s):
-            r, nu = steps[s]
+            r = 2 * s
             bi = batch_of_row[r]
             k = r - row0_of[bi]
-            for q in range(nu):
+            for q in range(2):
                 junk = junk_pool.tile([P, V], BF16, name="junk")
                 nc.scalar.activation(
                     out=junk[:, 1:V],
@@ -449,13 +476,17 @@ def tile_jointnet_t_kernel(
                 done_rows[r] = True
 
         def stores():
-            for r in range(0, ROWS, 4):
+            for n in range(NB):
+                r = 4 * n
                 if r not in stored and all((r + i) in done_rows for i in range(4)):
                     bi = batch_of_row[r]
                     k = r - row0_of[bi]
-                    nc.sync.dma_start(
-                        out=out[r // U, :, r % U : r % U + 4, :], in_=Ls[bi][:, k : k + 4, :]
-                    )
+                    b, t0, u0 = n // (TB * UG), 32 * (n // UG % TB), 16 * (n % UG)
+                    for uq in range(4):
+                        nc.sync.dma_start(
+                            out=out[b, t0 : t0 + 32, u0 + 4 * uq : u0 + 4 * uq + 4, :],
+                            in_=Ls[bi][32 * uq : 32 * uq + 32, k : k + 4, :],
+                        )
                     stored[r] = True
 
         def first(work):
@@ -467,14 +498,14 @@ def tile_jointnet_t_kernel(
         fillers = {}
         for bi in range(n_batches):
             e = last_step_of[bi]
-            plan = [(4, 0, row_mn), (4, 1, row_nab), (5, 1, row_t1), (6, 0, row_sq)]
+            plan = [(6, 0, row_mn), (6, 1, row_nab), (7, 1, row_t1), (8, 0, row_sq)]
             if bi < n_batches - 1:
-                plan += [(6, 1, row_v0), (7, 0, first(row_w)), (7, 1, first(row_u))]
-                plan += [(7, 2, first(row_t)), (7, 3, first(row_v)), (9, 0, second(row_w))]
-                plan += [(9, 1, second(row_u)), (9, 2, second(row_t)), (9, 3, second(row_v))]
-                plan += [(10, 0, row_negc), (10, 1, row_o0), (10, 2, row_blank)]
+                plan += [(8, 1, row_v0), (9, 0, first(row_w)), (9, 1, first(row_u))]
+                plan += [(9, 2, first(row_t)), (9, 3, first(row_v)), (11, 0, second(row_w))]
+                plan += [(11, 1, second(row_u)), (11, 2, second(row_t)), (11, 3, second(row_v))]
+                plan += [(12, 0, row_negc), (12, 1, row_o0), (12, 2, row_blank)]
             else:
-                plan += [(7, 0, row_negc), (7, 1, row_o0), (7, 2, row_blank)]
+                plan += [(9, 0, row_negc), (9, 1, row_o0), (9, 2, row_blank)]
             for delay, place, work in plan:
                 fillers.setdefault((e + delay, place), []).append((work, bi))
 
@@ -489,19 +520,17 @@ def tile_jointnet_t_kernel(
                 return 3, 0, 0
             return 2, 3, 2
 
-        for s in range(LEAD):
-            tanh_part(s, 0)
-        for s in range(LEAD):
-            tanh_part(s, 1)
-        for w in range(NS + 11):
+        for w in range(NS + 13):
             on_gpsimd, on_vector, on_scalar = quota(w)
             rows_a = take(on_scalar)
-            if LEAD <= w < NS:
-                tanh_part(w, 0)
-            if 0 <= w - 5 < NS:
-                exps(w - 5)
+            if w < NS:
+                tanh_half(w)
+            if w + 1 < NS:
+                sum_matmuls(w + 1)
+            if 0 <= w - 7 < NS:
+                exps(w - 7)
             for bi in range(n_batches):
-                if w - 5 == last_step_of[bi]:
+                if w - 7 == last_step_of[bi]:
                     row_ex(bi)
             subtract_rows(rows_a, "A")
             fill(w, 0)
@@ -509,25 +538,30 @@ def tile_jointnet_t_kernel(
                 regroup(w - 1)
             fill(w, 1)
             for bi in range(n_batches):
-                if w - 6 == last_step_of[bi]:
+                if w - 8 == last_step_of[bi]:
                     if bi == n_batches - 1:
                         row_ln(bi)
                     else:
                         row_exp(bi, 0)
-                if w - 8 == last_step_of[bi] and bi < n_batches - 1:
+                if w - 10 == last_step_of[bi] and bi < n_batches - 1:
                     row_exp(bi, 1)
-            if LEAD <= w < NS:
-                tanh_part(w, 1)
             if 0 <= w - 2 < NS:
                 quantise_h(w - 2)
-                logits(w - 2)
+            if 0 <= w - 4 < NS:
+                logits(w - 4)
+            n = w // 2 + 1
+            if w % 2 == 0 and 2 <= n < NB:
+                if n % UG == 0:
+                    repeat_enc(n // UG)
+                if n % (TB * UG) < UG:
+                    repeat_dec(n // (TB * UG) * UG + n % UG)
             fill(w, 2)
             subtract_rows(take(on_gpsimd), "G")
-            if 0 <= w - 3 < NS:
-                bias_add(w - 3)
+            if 0 <= w - 5 < NS:
+                bias_add(w - 5)
             fill(w, 3)
-            if 0 <= w - 4 < NS:
-                row_max(w - 4)
+            if 0 <= w - 6 < NS:
+                row_max(w - 6)
             subtract_rows(take(on_vector), "V")
             stores()
-        assert taken[0] == ROWS and len(stored) == ROWS // 4
+        assert taken[0] == ROWS and len(stored) == NB

@@ -20,7 +20,8 @@ NCH = 8
 TB, UG = T // 32, U // 16
 NB = B * TB * UG
 ROWS = 4 * NB
-BATCH_ROWS = [24, 24, 24, 24, 16, 8, 8]
+BATCH_ROWS = [16, 16, 16, 16, 16, 16, 16, 8, 8]
+NC = 4
 LOG2E_STEP = math.log(2.0) / 2**23
 LOG_SHIFT = -127.0 * math.log(2.0) + 0.0298
 
@@ -35,28 +36,37 @@ def tile_jointnet_t_kernel(
         ctx.enter_context(tc.manual_schedule())
         const = ctx.enter_context(tc.tile_pool(name="const", bufs=1))
         ps_cb = ctx.enter_context(tc.psum_pool(name="ps_cb", bufs=4))
-        hp_pool = ctx.enter_context(tc.tile_pool(name="hp", bufs=4))
-        gr_pool = ctx.enter_context(tc.tile_pool(name="gr", bufs=3))
-        cd_pool = ctx.enter_context(tc.tile_pool(name="cd", bufs=6))
+        hp_pool = ctx.enter_context(tc.tile_pool(name="hp", bufs=3))
+        et_pool = ctx.enter_context(tc.tile_pool(name="et", bufs=4))
+        dt_pool = ctx.enter_context(tc.tile_pool(name="dt", bufs=8))
+        cb_pool = ctx.enter_context(tc.tile_pool(name="cb", bufs=3))
+        gr_pool = ctx.enter_context(tc.tile_pool(name="gr", bufs=4))
+        cd_pool = ctx.enter_context(tc.tile_pool(name="cd", bufs=5))
         small = ctx.enter_context(tc.tile_pool(name="small", bufs=3))
         junk_pool = ctx.enter_context(tc.tile_pool(name="junk", bufs=2))
-        l_early = ctx.enter_context(tc.tile_pool(name="l_early", bufs=2))
         tok_pool = ctx.enter_context(tc.tile_pool(name="tok", bufs=4))
 
         enc_c = const.tile([P, B * T], U32, name="enc_c", align_bytes=64)
         enc_s = const.tile([P, B * T], U8, name="enc_s", align_bytes=64)
-        dec_c = const.tile([P, 4 * B * U], U32, name="dec_c", align_bytes=64)
-        dec_s = const.tile([P, 4 * B * U], U8, name="dec_s", align_bytes=64)
-        enc_xc = const.tile([P, B * TB, 512], U32, name="enc_xc", align_bytes=64)
-        enc_xs = const.tile([P, B * TB, 512], U8, name="enc_xs", align_bytes=64)
-        dec_xc = const.tile([P, B * UG, 512], U32, name="dec_xc", align_bytes=64)
-        dec_xs = const.tile([P, B * UG, 512], U8, name="dec_xs", align_bytes=64)
+        dec_c = const.tile([P, 64], U32, name="dec_c", align_bytes=64)
+        dec_s = const.tile([P, 64], U8, name="dec_s", align_bytes=64)
+        dec_1 = const.tile([P, B * U], U32, name="dec_1", align_bytes=64)
+        dec_1s = const.tile([P, B * U], U8, name="dec_1s", align_bytes=64)
+        enc_xc = const.tile([P, NC, 512], U32, name="enc_xc", align_bytes=64)
+        enc_xs = const.tile([P, NC, 512], U8, name="enc_xs", align_bytes=64)
+        dec_xc = const.tile([P, 1, 512], U32, name="dec_xc", align_bytes=64)
+        dec_xs = const.tile([P, 1, 512], U8, name="dec_xs", align_bytes=64)
         wec = const.tile([P, NCH * P], U32, name="wec", align_bytes=64)
         wes = const.tile([P, NCH * P], U8, name="wes", align_bytes=64)
         wdc = const.tile([P, NCH * P], U32, name="wdc", align_bytes=64)
         wds = const.tile([P, NCH * P], U8, name="wds", align_bytes=64)
         wfc = const.tile([P, 4 * P], U32, name="wfc", align_bytes=64)
         wfs = const.tile([P, 4 * P], U8, name="wfs", align_bytes=64)
+        enc_rows = const.tile([P, F], F32, name="enc_rows")
+        dec_rows = const.tile([P, F], F32, name="dec_rows")
+        bias_rows = const.tile([P, F], F32, name="bias_rows")
+        enc_i = const.tile([P, B, 4 * T], F32, name="enc_i")
+        dec_i = const.tile([P, B * U, 4], F32, name="dec_i")
         bsum = const.tile([P, NCH], F32, name="bsum")
         bfc = const.tile([P, V], F32, name="bfc")
         ident = const.tile([P, P], F32, name="ident")
@@ -87,14 +97,16 @@ def tile_jointnet_t_kernel(
                 in_=scales.to_broadcast([P, 4, 4, 8]),
             )
 
-        HALVES = [(0, 0), (1, 0), (0, 1), (1, 1)] + [(n, g) for n in range(2, NB) for g in range(2)]
-        NS = len(HALVES)
+        def place_of(n):
+            return n // (UG * TB), n // TB % UG, n % TB
+
+        HALVES = [(0, 0), (1, 0), (0, 1), (1, 1)] + [(n, g) for n in range(2, NC) for g in range(2)]
+        NS = 2 * NB
         sums = {}
 
         def sum_matmuls(s):
             n, g = HALVES[s]
-            e = n // UG
-            d = (n // (TB * UG)) * UG + n % UG
+            b, d, e = place_of(n)
             for j in range(4):
                 c = 4 * g + j
                 cols = slice(c * P, (c + 1) * P)
@@ -126,6 +138,8 @@ def tile_jointnet_t_kernel(
                     out=bdec_bf[:].rearrange("p (g j) -> p g j", g=2),
                     in_=b_dec.rearrange("(g p j) -> p g j", g=2, j=4),
                 )
+            benc_all = stage.tile([P, F], BF16, name="benc_all")
+            bdec_all = stage.tile([P, F], BF16, name="bdec_all")
             enc_sb = stage.tile([P, B, K1], BF16, name="enc_sb")
             nc.sync.dma_start(out=enc_sb[:], in_=encoder_output.rearrange("b t k -> t b k"))
             dec_sb = stage.tile([P, K1], BF16, name="dec_sb")
@@ -141,6 +155,8 @@ def tile_jointnet_t_kernel(
             wfc_sb = stage.tile([P, 2, F], BF16, name="wfc_sb")
             nc.sync.dma_start(out=wfc_sb[:], in_=W_fc.rearrange("(h v) k -> v h k", h=2))
             nc.sync.dma_start(out=bfc_bf[:], in_=b_fc.partition_broadcast(P))
+            nc.sync.dma_start(out=benc_all[:], in_=b_enc.partition_broadcast(P))
+            nc.sync.dma_start(out=bdec_all[:], in_=b_dec.partition_broadcast(P))
 
             make_identity(nc, ident[:])
             nc.gpsimd.memset(enc_s[:].bitcast(U32), 0)
@@ -149,7 +165,8 @@ def tile_jointnet_t_kernel(
             nc.scalar.activation(out=warm_out[:], in_=warm_in[:], func=ACT.Tanh)
 
             eg = stage.tile([P, 2 * 512], BF16, name="eg", align_bytes=64)
-            dg = stage.tile([P, 4 * 512], BF16, name="dg", align_bytes=64)
+            dg = stage.tile([P, 256], BF16, name="dg", align_bytes=64)
+            d1 = stage.tile([P, 512], BF16, name="d1", align_bytes=64)
             weg = stage.tile([P, NCH * 512], BF16, name="weg", align_bytes=64)
             wdg = stage.tile([P, NCH * 512], BF16, name="wdg", align_bytes=64)
             wfg = stage.tile([P, 4 * 512], BF16, name="wfg", align_bytes=64)
@@ -202,19 +219,21 @@ def tile_jointnet_t_kernel(
             regrouped(enc_tr, eg[:], True)
             nc.scalar.copy(
                 out=dg[:].bitcast(F32).rearrange("p (c r u) -> p c r u", r=4, u=2),
-                in_=dec_tr[:, 0, :, :].rearrange("p u c -> p c u").unsqueeze(2).to_broadcast([P, P, 4, 2]),
+                in_=dec_tr[:, 0, :, 0:16].rearrange("p u c -> p c u").unsqueeze(2).to_broadcast([P, 16, 4, 2]),
             )
+            regrouped(dec_tr, d1[:], False)
             wd_tr = transpose_weights(wdec_sb, 0)
             regroup_weights(we_tr, weg, True)
             nc.vector.tensor_tensor(out=bsum[:], in0=benc_bf[:], in1=bdec_bf[:], op=ALU.add)
             quantise(eg, enc_c, enc_s, 0, 2)
-            quantise(dg, dec_c, dec_s, 0, 4)
+            nc.vector.quantize_mx(out=dec_c[:].bitcast(FP8X4), scales=dec_s[:], in_=dg[:])
+            quantise(d1, dec_1, dec_1s, 0, 1)
             repeat_enc(0)
             repeat_dec(0)
             regroup_weights(wd_tr, wdg, False)
             quantise(weg, wec, wes, 0, 4)
             quantise(wdg, wdc, wds, 0, 4)
-            repeat_dec(1)
+            repeat_enc(1)
             we_tr = transpose_weights(wenc_sb, 1)
             wd_tr = transpose_weights(wdec_sb, 1)
             sum_matmuls(0)
@@ -231,8 +250,15 @@ def tile_jointnet_t_kernel(
                 regrouped(fc_tr, wfg[:, g * 1024 : (g + 1) * 1024], False)
             quantise(wfg, wfc, wfs, 0, 4)
             nc.vector.tensor_copy(out=bfc[:], in_=bfc_bf[:])
+            for g in range(2):
+                nc.vector.tensor_tensor(
+                    out=bias_rows[:, 512 * g : 512 * g + 512].rearrange("p (j w) -> p j w", j=4),
+                    in0=benc_all[:, 512 * g : 512 * g + 512].rearrange("p (w j) -> p j w", j=4),
+                    in1=bdec_all[:, 512 * g : 512 * g + 512].rearrange("p (w j) -> p j w", j=4),
+                    op=ALU.add,
+                )
 
-        l_late = ctx.enter_context(tc.tile_pool(name="l_late", bufs=2))
+        l_pool = ctx.enter_context(tc.tile_pool(name="l_pool", bufs=4))
         ps_lg = ctx.enter_context(tc.psum_pool(name="ps_lg", bufs=4))
 
         row0_of = [sum(BATCH_ROWS[:bi]) for bi in range(len(BATCH_ROWS))]
@@ -241,7 +267,7 @@ def tile_jointnet_t_kernel(
             batch_of_row.extend([bi] * n)
         n_batches = len(BATCH_ROWS)
         last_step_of = [(row0_of[bi] + BATCH_ROWS[bi]) // 2 - 1 for bi in range(n_batches)]
-        hPs, groupeds, codes, lgs = {}, {}, {}, {}
+        hPs, groupeds, codes, lgs, combs, ets, dts = {}, {}, {}, {}, {}, {}, {}
         Ls, negms, ssums, misc = {}, {}, {}, {}
 
         def tanh_half(s):
@@ -266,25 +292,162 @@ def tile_jointnet_t_kernel(
         def quantise_h(s):
             words = cd_pool.tile([P, 512], U32, name="words", align_bytes=64)
             planes = cd_pool.tile([P, 512], U8, name="planes", align_bytes=64)
-            codes[HALVES[s]] = (words, planes)
             nc.vector.quantize_mx(
                 out=words[:].bitcast(FP8X4), scales=planes[:], in_=groupeds[s][:]
             )
+            if s < 2 * NC:
+                n, g = HALVES[s]
+                for m in range(4):
+                    codes[4 * n + m, g] = (words, planes, slice(m * P, (m + 1) * P))
+            else:
+                for x in range(4):
+                    codes[2 * s + x // 2, x % 2] = (words, planes, slice(x * P, (x + 1) * P))
 
         def logits(s):
             lgs[s] = ps_lg.tile([P, 2, V], F32, name="lg")
             for q in range(2):
-                m = 2 * (s % 2) + q
                 for g in range(2):
-                    words, planes = codes[s // 2, g]
+                    words, planes, cols = codes[2 * s + q, g]
                     nc.tensor.matmul_mx(
                         out=lgs[s][:, q, :],
-                        lhsT=words[:, m * P : (m + 1) * P].bitcast(FP8X4),
-                        lhsT_scale=planes[:, m * P : (m + 1) * P],
+                        lhsT=words[:, cols].bitcast(FP8X4),
+                        lhsT_scale=planes[:, cols],
                         rhs=wfc[:, g * V : (g + 1) * V].bitcast(FP8X4),
                         rhs_scale=wfs[:, g * V : (g + 1) * V],
                         start=(g == 0),
                         stop=(g == 1),
+                    )
+
+        def park(run0, slot):
+            rows = out[1, run0 : run0 + 32, 48 + 4 * slot : 52 + 4 * slot, :]
+            return rows.rearrange("t w v -> t (w v)")
+
+        def park_enc(i):
+            return park(32 + 32 * (i // 4), i % 4)
+
+        def bank_matmul(dst, lhs, lhs_s, lcols, rhs, rhs_s, rcols):
+            nc.tensor.matmul_mx(
+                out=dst,
+                lhsT=lhs[:, lcols].bitcast(FP8X4),
+                lhsT_scale=lhs_s[:, lcols],
+                rhs=rhs[:, rcols].bitcast(FP8X4),
+                rhs_scale=rhs_s[:, rcols],
+                start=True,
+                stop=True,
+            )
+
+        def enc_to_rows(b):
+            for g in range(2):
+                bank = ps_lg.tile([P, 2, V], F32, name="lg")
+                flat = bank[:].rearrange("p a v -> p (a v)")
+                cols = slice(512 * g, 512 * g + 512)
+                bank_matmul(flat, enc_c, enc_s, slice(b * T, (b + 1) * T), wec, wes, cols)
+                nc.vector.tensor_copy(out=enc_rows[:, cols], in_=flat)
+            for tb in range(TB):
+                nc.sync.dma_start(
+                    out=park_enc(TB * b + tb), in_=enc_rows[32 * tb : 32 * tb + 32, :]
+                )
+
+        def dec_to_rows():
+            for g in range(2):
+                bank = ps_lg.tile([P, 2, V], F32, name="lg")
+                flat = bank[:].rearrange("p a v -> p (a v)")
+                cols = slice(512 * g, 512 * g + 512)
+                bank_matmul(flat, dec_1, dec_1s, slice(0, P), wdc, wds, cols)
+                nc.vector.tensor_tensor(
+                    out=dec_rows[:, cols], in0=flat, in1=bias_rows[:, cols], op=ALU.add
+                )
+            for i in range(4):
+                nc.sync.dma_start(out=park(96, i), in_=dec_rows[32 * i : 32 * i + 32, :])
+
+        def enc_interleaved(b):
+            bank = ps_lg.tile([P, 2, V], F32, name="lg")
+            four = bank[:].rearrange("p a (c t) -> p (a c) t", c=2)
+            for j in range(4):
+                cols = slice((4 + j) * P, (5 + j) * P)
+                bank_matmul(four[:, j, :], wec, wes, cols, enc_c, enc_s, slice(b * T, (b + 1) * T))
+            nc.vector.tensor_copy(
+                out=enc_i[:, b, :].rearrange("p (t j) -> p t j", j=4),
+                in_=four.rearrange("p j t -> p t j"),
+            )
+
+        def dec_interleaved():
+            bank = ps_lg.tile([P, 2, V], F32, name="lg")
+            four = bank[:].rearrange("p a (c t) -> p (a c) t", c=2)
+            for j in range(4):
+                cols = slice((4 + j) * P, (5 + j) * P)
+                bank_matmul(four[:, j, :], wdc, wds, cols, dec_1, dec_1s, slice(0, P))
+            nc.vector.tensor_tensor(
+                out=dec_i[:],
+                in0=four.rearrange("p j c -> p c j"),
+                in1=bsum[:, 4:8].unsqueeze(1).to_broadcast([P, B * U, 4]),
+                op=ALU.add,
+            )
+
+        def load_enc(i):
+            ets[i] = et_pool.tile([P, F], F32, name="et")
+            for uq in range(4):
+                nc.sync.dma_start(out=ets[i][32 * uq : 32 * uq + 32, :], in_=park_enc(i))
+
+        def load_dec(i):
+            for m in range(4):
+                dts[i, m] = dt_pool.tile([P, F], F32, name="dt")
+                for uq in range(4):
+                    row = 16 * i + 4 * uq + m
+                    src = park(96, row // 32)[row % 32, :]
+                    nc.sync.dma_start(
+                        out=dts[i, m][32 * uq : 32 * uq + 32, :], in_=src.partition_broadcast(32)
+                    )
+
+        def sum_transposes(s):
+            b, ug, tb = place_of(s // 2)
+            for x in range(3):
+                m, g = 2 * (s % 2) + x // 2, x % 2
+                sums[s, x] = ps_cb.tile([P, 512], F32, name="sum")
+                for j in range(4):
+                    cols = slice((4 * g + j) * P, (4 * g + j + 1) * P)
+                    for src, begins in (
+                        (ets[TB * b + tb][:, cols], True),
+                        (dts[UG * b + ug, m][:, cols], False),
+                    ):
+                        nc.tensor.matmul(
+                            out=sums[s, x][:, j * P : (j + 1) * P],
+                            lhsT=src,
+                            rhs=ident[:],
+                            start=begins,
+                            stop=not begins,
+                            is_transpose=True,
+                        )
+
+        def sum_on_vector(s):
+            b, ug, tb = place_of(s // 2)
+            m = 2 * (s % 2) + 1
+            u0 = b * U + ug * 16
+            combs[s] = cb_pool.tile([P, 512], F32, name="comb")
+            nc.vector.tensor_tensor(
+                out=combs[s][:].rearrange("p (q t j) -> p q t j", q=4, j=4),
+                in0=enc_i[:, b, 128 * tb : 128 * tb + 128]
+                .rearrange("p (t j) -> p t j", j=4)
+                .unsqueeze(1)
+                .to_broadcast([P, 4, 32, 4]),
+                in1=dec_i[:, u0 : u0 + 16, :]
+                .rearrange("p (q m) j -> p m q j", m=4)[:, m, :, :]
+                .unsqueeze(2)
+                .to_broadcast([P, 4, 32, 4]),
+                op=ALU.add,
+            )
+
+        def tanh_pair(s):
+            groupeds[s] = gr_pool.tile([P, 4 * 512], BF16, name="grouped", align_bytes=64)
+            for x in range(4):
+                dst = groupeds[s][:, 512 * x : 512 * x + 512]
+                if x == 3:
+                    nc.scalar.activation(out=dst, in_=combs[s][:], func=ACT.Tanh)
+                else:
+                    nc.scalar.activation(
+                        out=dst.rearrange("p (t j) -> p t j", j=4),
+                        in_=sums[s, x][:].rearrange("p (j t) -> p t j", j=4),
+                        func=ACT.Tanh,
                     )
 
         def bias_add(s):
@@ -292,8 +455,7 @@ def tile_jointnet_t_kernel(
             bi = batch_of_row[r]
             n = BATCH_ROWS[bi]
             if r == row0_of[bi]:
-                pool = l_early if bi % 4 < 2 else l_late
-                Ls[bi] = pool.tile([P, max(BATCH_ROWS), V], F32, name="L")
+                Ls[bi] = l_pool.tile([P, max(BATCH_ROWS), V], F32, name="L")
                 negms[bi] = small.tile([P, n], F32, name="negm")
                 ssums[bi] = small.tile([P, n], F32, name="ssum")
                 misc[bi] = {}
@@ -481,7 +643,8 @@ def tile_jointnet_t_kernel(
                 if r not in stored and all((r + i) in done_rows for i in range(4)):
                     bi = batch_of_row[r]
                     k = r - row0_of[bi]
-                    b, t0, u0 = n // (TB * UG), 32 * (n // UG % TB), 16 * (n % UG)
+                    b, ug, tb = place_of(n)
+                    t0, u0 = 32 * tb, 16 * ug
                     for uq in range(4):
                         nc.sync.dma_start(
                             out=out[b, t0 : t0 + 32, u0 + 4 * uq : u0 + 4 * uq + 4, :],
@@ -495,73 +658,103 @@ def tile_jointnet_t_kernel(
         def second(work):
             return lambda bi: work(bi, 1)
 
+        def lag(p):
+            return 3 if p < 12 else 2 if p < 24 else 1 if p < 36 else 0
+
+        def lag_exp(p):
+            return lag(p) + (2 if p < 44 else 1 if p < 52 else 0)
+
+        def due(w, delay, extra):
+            return [p for p in range(NS) if p + delay + extra(p) == w]
+
         fillers = {}
+        ex_at, exp0_at, exp1_at, ln_at = {}, {}, {}, {}
         for bi in range(n_batches):
             e = last_step_of[bi]
-            plan = [(6, 0, row_mn), (6, 1, row_nab), (7, 1, row_t1), (8, 0, row_sq)]
+            a, x = e + 2 + lag(e), e + 4 + lag_exp(e)
+            ex_at[x] = bi
+            plan = [(a + 1, 0, row_mn), (a + 1, 1, row_nab), (a + 2, 1, row_t1), (x + 1, 0, row_sq)]
             if bi < n_batches - 1:
-                plan += [(8, 1, row_v0), (9, 0, first(row_w)), (9, 1, first(row_u))]
-                plan += [(9, 2, first(row_t)), (9, 3, first(row_v)), (11, 0, second(row_w))]
-                plan += [(11, 1, second(row_u)), (11, 2, second(row_t)), (11, 3, second(row_v))]
-                plan += [(12, 0, row_negc), (12, 1, row_o0), (12, 2, row_blank)]
+                exp0_at[x + 1], exp1_at[x + 3] = bi, bi
+                plan += [(x + 1, 1, row_v0), (x + 2, 0, first(row_w)), (x + 2, 1, first(row_u))]
+                plan += [(x + 2, 2, first(row_t)), (x + 2, 3, first(row_v)), (x + 4, 0, second(row_w))]
+                plan += [(x + 4, 1, second(row_u)), (x + 4, 2, second(row_t)), (x + 4, 3, second(row_v))]
+                plan += [(x + 5, 0, row_negc), (x + 5, 1, row_o0), (x + 5, 2, row_blank)]
             else:
-                plan += [(9, 0, row_negc), (9, 1, row_o0), (9, 2, row_blank)]
-            for delay, place, work in plan:
-                fillers.setdefault((e + delay, place), []).append((work, bi))
+                ln_at[x + 1] = bi
+                plan += [(x + 2, 0, row_negc), (x + 2, 1, row_o0), (x + 2, 2, row_blank)]
+            for step, place, work in plan:
+                fillers.setdefault((step, place), []).append((work, bi))
 
         def fill(w, place):
             for work, bi in fillers.get((w, place), []):
                 work(bi)
 
         def quota(w):
-            if w < 44:
-                return 2, 0, 0
-            if w < NS:
-                return 3, 0, 0
-            return 2, 3, 2
+            return (0, 3, 0) if w < NS else (2, 3, 2)
 
-        for w in range(NS + 13):
+        for w in range(NS + 12):
             on_gpsimd, on_vector, on_scalar = quota(w)
             rows_a = take(on_scalar)
-            if w < NS:
+            if w < 2 * NC:
                 tanh_half(w)
-            if w + 1 < NS:
+            elif w < NS:
+                tanh_pair(w)
+            if w + 1 < 2 * NC:
                 sum_matmuls(w + 1)
-            if 0 <= w - 7 < NS:
-                exps(w - 7)
-            for bi in range(n_batches):
-                if w - 7 == last_step_of[bi]:
-                    row_ex(bi)
+            elif w + 1 < NS:
+                sum_transposes(w + 1)
+            for p in due(w, 4, lag_exp):
+                exps(p)
+            if w in ex_at:
+                row_ex(ex_at[w])
             subtract_rows(rows_a, "A")
             fill(w, 0)
-            if 0 <= w - 1 < NS:
+            if 0 <= w - 1 < 2 * NC:
                 regroup(w - 1)
+            if 2 * NC <= w + 1 < NS:
+                sum_on_vector(w + 1)
             fill(w, 1)
-            for bi in range(n_batches):
-                if w - 8 == last_step_of[bi]:
-                    if bi == n_batches - 1:
-                        row_ln(bi)
-                    else:
-                        row_exp(bi, 0)
-                if w - 10 == last_step_of[bi] and bi < n_batches - 1:
-                    row_exp(bi, 1)
-            if 0 <= w - 2 < NS:
+            if w in exp0_at:
+                row_exp(exp0_at[w], 0)
+            if w in exp1_at:
+                row_exp(exp1_at[w], 1)
+            if w in ln_at:
+                row_ln(ln_at[w])
+            if 0 <= w - 2 < 2 * NC:
                 quantise_h(w - 2)
-            if 0 <= w - 4 < NS:
-                logits(w - 4)
-            n = w // 2 + 1
-            if w % 2 == 0 and 2 <= n < NB:
-                if n % UG == 0:
-                    repeat_enc(n // UG)
-                if n % (TB * UG) < UG:
-                    repeat_dec(n // (TB * UG) * UG + n % UG)
+            if 2 * NC <= w - 1 < NS:
+                quantise_h(w - 1)
+            for p in due(w, 1, lag):
+                logits(p)
+            if w == 0:
+                repeat_enc(2)
+                repeat_enc(3)
+            if w == 1:
+                dec_to_rows()
+                enc_to_rows(0)
+            if w == 2:
+                for i in range(TB):
+                    load_enc(i)
+                load_dec(1)
+            if w == 3:
+                dec_interleaved()
+                enc_interleaved(0)
+            if w == 12:
+                enc_to_rows(1)
+            if w == 13:
+                enc_interleaved(1)
+            if 26 <= w < 34 and w % 2 == 0:
+                load_enc(TB + w // 2 - 13)
+            if w % 8 == 1 and 16 <= w + 7 < NS:
+                load_dec((w + 7) // 8)
             fill(w, 2)
             subtract_rows(take(on_gpsimd), "G")
-            if 0 <= w - 5 < NS:
-                bias_add(w - 5)
+            for p in due(w, 2, lag):
+                bias_add(p)
             fill(w, 3)
-            if 0 <= w - 6 < NS:
-                row_max(w - 6)
+            for p in due(w, 3, lag):
+                row_max(p)
             subtract_rows(take(on_vector), "V")
             stores()
         assert taken[0] == ROWS and len(stored) == NB

@@ -15,15 +15,16 @@ ALU = mybir.AluOpType
 AX = mybir.AxisListType
 
 P = 128
+LOG2E_STEP = math.log(2.0) / 2**23
+LOG_SHIFT = -127.0 * math.log(2.0) + 0.0298
 B, T, U, K1, F, V = 2, 128, 64, 512, 1024, 256
 NCH = 8
 TB, UG = T // 32, U // 16
 NB = B * TB * UG
 ROWS = 4 * NB
-BATCH_ROWS = [16, 16, 16, 16, 16, 16, 16, 8, 8]
+BATCH_ROWS = [20, 20, 20, 20, 16, 8, 16, 8]
+ON_VECTOR = ({3}, {3}, {3}, {3})
 NC = 4
-LOG2E_STEP = math.log(2.0) / 2**23
-LOG_SHIFT = -127.0 * math.log(2.0) + 0.0298
 
 FLOPS = 2 * (B * T * K1 * F + B * U * K1 * F + B * T * U * F * V)
 
@@ -39,7 +40,7 @@ def tile_jointnet_t_kernel(
         hp_pool = ctx.enter_context(tc.tile_pool(name="hp", bufs=3))
         et_pool = ctx.enter_context(tc.tile_pool(name="et", bufs=4))
         dt_pool = ctx.enter_context(tc.tile_pool(name="dt", bufs=8))
-        cb_pool = ctx.enter_context(tc.tile_pool(name="cb", bufs=3))
+        cb_pool = ctx.enter_context(tc.tile_pool(name="cb", bufs=4))
         gr_pool = ctx.enter_context(tc.tile_pool(name="gr", bufs=4))
         cd_pool = ctx.enter_context(tc.tile_pool(name="cd", bufs=5))
         small = ctx.enter_context(tc.tile_pool(name="small", bufs=3))
@@ -71,6 +72,7 @@ def tile_jointnet_t_kernel(
         bfc = const.tile([P, V], F32, name="bfc")
         ident = const.tile([P, P], F32, name="ident")
         warm_in = const.tile([P, 1], F32, name="warm_in")
+        one = const.tile([P, 1], F32, name="one")
         warm_out = const.tile([P, 1], F32, name="warm_out")
 
         def repeat_enc(i):
@@ -162,6 +164,7 @@ def tile_jointnet_t_kernel(
             nc.gpsimd.memset(enc_s[:].bitcast(U32), 0)
             nc.gpsimd.memset(dec_s[:].bitcast(U32), 0)
             nc.vector.memset(warm_in[:], 0.0)
+            nc.vector.memset(one[:], 1.0)
             nc.scalar.activation(out=warm_out[:], in_=warm_in[:], func=ACT.Tanh)
 
             eg = stage.tile([P, 2 * 512], BF16, name="eg", align_bytes=64)
@@ -231,8 +234,9 @@ def tile_jointnet_t_kernel(
             repeat_enc(0)
             repeat_dec(0)
             regroup_weights(wd_tr, wdg, False)
-            quantise(weg, wec, wes, 0, 4)
-            quantise(wdg, wdc, wds, 0, 4)
+            for first in (0, 2):
+                quantise(weg, wec, wes, first, 2)
+                quantise(wdg, wdc, wds, first, 2)
             repeat_enc(1)
             we_tr = transpose_weights(wenc_sb, 1)
             wd_tr = transpose_weights(wdec_sb, 1)
@@ -269,6 +273,7 @@ def tile_jointnet_t_kernel(
         last_step_of = [(row0_of[bi] + BATCH_ROWS[bi]) // 2 - 1 for bi in range(n_batches)]
         hPs, groupeds, codes, lgs, combs, ets, dts = {}, {}, {}, {}, {}, {}, {}
         Ls, negms, ssums, misc = {}, {}, {}, {}
+        row_banks, feature_banks = {}, {}
 
         def tanh_half(s):
             g = HALVES[s][1]
@@ -336,13 +341,19 @@ def tile_jointnet_t_kernel(
                 stop=True,
             )
 
-        def enc_to_rows(b):
+        def enc_row_matmuls(b):
             for g in range(2):
                 bank = ps_lg.tile([P, 2, V], F32, name="lg")
                 flat = bank[:].rearrange("p a v -> p (a v)")
                 cols = slice(512 * g, 512 * g + 512)
                 bank_matmul(flat, enc_c, enc_s, slice(b * T, (b + 1) * T), wec, wes, cols)
-                nc.vector.tensor_copy(out=enc_rows[:, cols], in_=flat)
+                row_banks[b, g] = flat
+
+        def enc_to_rows(b):
+            for g in range(2):
+                nc.vector.tensor_copy(
+                    out=enc_rows[:, 512 * g : 512 * g + 512], in_=row_banks[b, g]
+                )
             for tb in range(TB):
                 nc.sync.dma_start(
                     out=park_enc(TB * b + tb), in_=enc_rows[32 * tb : 32 * tb + 32, :]
@@ -360,15 +371,18 @@ def tile_jointnet_t_kernel(
             for i in range(4):
                 nc.sync.dma_start(out=park(96, i), in_=dec_rows[32 * i : 32 * i + 32, :])
 
-        def enc_interleaved(b):
+        def enc_feature_matmuls(b):
             bank = ps_lg.tile([P, 2, V], F32, name="lg")
             four = bank[:].rearrange("p a (c t) -> p (a c) t", c=2)
             for j in range(4):
                 cols = slice((4 + j) * P, (5 + j) * P)
                 bank_matmul(four[:, j, :], wec, wes, cols, enc_c, enc_s, slice(b * T, (b + 1) * T))
+            feature_banks[b] = four
+
+        def enc_interleaved(b):
             nc.vector.tensor_copy(
                 out=enc_i[:, b, :].rearrange("p (t j) -> p t j", j=4),
-                in_=four.rearrange("p j t -> p t j"),
+                in_=feature_banks[b].rearrange("p j t -> p t j"),
             )
 
         def dec_interleaved():
@@ -401,7 +415,9 @@ def tile_jointnet_t_kernel(
 
         def sum_transposes(s):
             b, ug, tb = place_of(s // 2)
-            for x in range(3):
+            for x in range(4):
+                if x in ON_VECTOR[s % 4]:
+                    continue
                 m, g = 2 * (s % 2) + x // 2, x % 2
                 sums[s, x] = ps_cb.tile([P, 512], F32, name="sum")
                 for j in range(4):
@@ -421,28 +437,30 @@ def tile_jointnet_t_kernel(
 
         def sum_on_vector(s):
             b, ug, tb = place_of(s // 2)
-            m = 2 * (s % 2) + 1
             u0 = b * U + ug * 16
-            combs[s] = cb_pool.tile([P, 512], F32, name="comb")
-            nc.vector.tensor_tensor(
-                out=combs[s][:].rearrange("p (q t j) -> p q t j", q=4, j=4),
-                in0=enc_i[:, b, 128 * tb : 128 * tb + 128]
-                .rearrange("p (t j) -> p t j", j=4)
-                .unsqueeze(1)
-                .to_broadcast([P, 4, 32, 4]),
-                in1=dec_i[:, u0 : u0 + 16, :]
-                .rearrange("p (q m) j -> p m q j", m=4)[:, m, :, :]
-                .unsqueeze(2)
-                .to_broadcast([P, 4, 32, 4]),
-                op=ALU.add,
-            )
+            for x in sorted(ON_VECTOR[s % 4]):
+                m = 2 * (s % 2) + x // 2
+                combs[s, x] = cb_pool.tile([P, 512], F32, name="comb")
+                nc.vector.tensor_tensor(
+                    out=combs[s, x][:].rearrange("p (q t j) -> p q t j", q=4, j=4),
+                    in0=enc_i[:, b, 128 * tb : 128 * tb + 128]
+                    .rearrange("p (t j) -> p t j", j=4)
+                    .unsqueeze(1)
+                    .to_broadcast([P, 4, 32, 4]),
+                    in1=dec_i[:, u0 : u0 + 16, :]
+                    .rearrange("p (q m) j -> p m q j", m=4)[:, m, :, :]
+                    .unsqueeze(2)
+                    .to_broadcast([P, 4, 32, 4]),
+                    op=ALU.add,
+                )
 
-        def tanh_pair(s):
-            groupeds[s] = gr_pool.tile([P, 4 * 512], BF16, name="grouped", align_bytes=64)
-            for x in range(4):
+        def tanh_units(s, units):
+            if 0 in units:
+                groupeds[s] = gr_pool.tile([P, 4 * 512], BF16, name="grouped", align_bytes=64)
+            for x in units:
                 dst = groupeds[s][:, 512 * x : 512 * x + 512]
-                if x == 3:
-                    nc.scalar.activation(out=dst, in_=combs[s][:], func=ACT.Tanh)
+                if x in ON_VECTOR[s % 4]:
+                    nc.scalar.activation(out=dst, in_=combs[s, x][:], func=ACT.Tanh)
                 else:
                     nc.scalar.activation(
                         out=dst.rearrange("p (t j) -> p t j", j=4),
@@ -569,6 +587,9 @@ def tile_jointnet_t_kernel(
             misc[bi]["y"] = misc[bi]["v%d" % (i + 1)]
             misc[bi]["factor"] = -1.0 / 3.0
 
+        def rows_ready(bi):
+            ready.extend(range(row0_of[bi], row0_of[bi] + BATCH_ROWS[bi]))
+
         def row_ln(bi):
             nc.scalar.activation(
                 out=row_tile(bi, "y", True)[:], in_=misc[bi]["x"][:], func=ACT.Ln
@@ -591,7 +612,7 @@ def tile_jointnet_t_kernel(
             nc.vector.tensor_tensor(
                 out=blank(bi), in0=misc[bi]["o0"][:], in1=misc[bi]["negc"][:], op=ALU.subtract
             )
-            ready.extend(range(row0_of[bi], row0_of[bi] + BATCH_ROWS[bi]))
+            rows_ready(bi)
 
         ready = []
         taken = [0]
@@ -652,37 +673,49 @@ def tile_jointnet_t_kernel(
                         )
                     stored[r] = True
 
+        def lag(p):
+            return 3 if p < 12 else 2 if p < 24 else 1 if p < 36 else 0
+
+        def logits_at(p):
+            return p + 1 + lag(p)
+
+        def add_at(p):
+            return min(p + 2 + lag(p), NS)
+
+        def max_at(p):
+            return min(p + 3 + lag(p), NS)
+
+        def exp_at(p):
+            return min(p + 4 + lag(p) + (2 if p < 44 else 1 if p < 52 else 0), NS)
+
+        def due(w, at):
+            return [p for p in range(NS) if at(p) == w]
+
         def first(work):
             return lambda bi: work(bi, 0)
 
         def second(work):
             return lambda bi: work(bi, 1)
 
-        def lag(p):
-            return 3 if p < 12 else 2 if p < 24 else 1 if p < 36 else 0
-
-        def lag_exp(p):
-            return lag(p) + (2 if p < 44 else 1 if p < 52 else 0)
-
-        def due(w, delay, extra):
-            return [p for p in range(NS) if p + delay + extra(p) == w]
-
         fillers = {}
-        ex_at, exp0_at, exp1_at, ln_at = {}, {}, {}, {}
+        ex_at, exp0_at, exp1_at = {}, {}, {}
         for bi in range(n_batches):
             e = last_step_of[bi]
-            a, x = e + 2 + lag(e), e + 4 + lag_exp(e)
+            a, x = add_at(e), exp_at(e)
             ex_at[x] = bi
-            plan = [(a + 1, 0, row_mn), (a + 1, 1, row_nab), (a + 2, 1, row_t1), (x + 1, 0, row_sq)]
-            if bi < n_batches - 1:
+            if bi < n_batches - 2:
                 exp0_at[x + 1], exp1_at[x + 3] = bi, bi
+                plan = [(a + 1, 0, row_mn), (a + 1, 1, row_nab), (a + 2, 1, row_t1), (x + 1, 0, row_sq)]
                 plan += [(x + 1, 1, row_v0), (x + 2, 0, first(row_w)), (x + 2, 1, first(row_u))]
                 plan += [(x + 2, 2, first(row_t)), (x + 2, 3, first(row_v)), (x + 4, 0, second(row_w))]
                 plan += [(x + 4, 1, second(row_u)), (x + 4, 2, second(row_t)), (x + 4, 3, second(row_v))]
                 plan += [(x + 5, 0, row_negc), (x + 5, 1, row_o0), (x + 5, 2, row_blank)]
+            elif bi < n_batches - 1:
+                plan = [(a + 1, 0, row_nab), (a + 1, 1, row_mn), (a + 2, 2, row_t1), (x, 3, row_sq)]
+                plan += [(NS, 0, row_negc), (NS, 1, row_o0), (NS, 2, row_blank)]
             else:
-                ln_at[x + 1] = bi
-                plan += [(x + 2, 0, row_negc), (x + 2, 1, row_o0), (x + 2, 2, row_blank)]
+                plan = [(NS, 0, row_nab), (NS, 1, row_mn), (NS, 2, row_t1), (NS + 1, 0, row_sq)]
+                plan += [(NS + 2, 0, row_negc), (NS + 2, 1, row_o0), (NS + 2, 2, row_blank)]
             for step, place, work in plan:
                 fillers.setdefault((step, place), []).append((work, bi))
 
@@ -690,25 +723,23 @@ def tile_jointnet_t_kernel(
             for work, bi in fillers.get((w, place), []):
                 work(bi)
 
-        def quota(w):
-            return (0, 3, 0) if w < NS else (2, 3, 2)
-
-        for w in range(NS + 12):
-            on_gpsimd, on_vector, on_scalar = quota(w)
-            rows_a = take(on_scalar)
+        for w in range(NS):
             if w < 2 * NC:
                 tanh_half(w)
-            elif w < NS:
-                tanh_pair(w)
+            else:
+                tanh_units(w, (0, 1))
+            for p in due(w, exp_at):
+                exps(p)
+            if w in ex_at:
+                row_ex(ex_at[w])
+            if w >= 2 * NC:
+                tanh_units(w, (2, 3))
+            if w == NS - 1:
+                nc.scalar.activation(out=warm_out[:], in_=one[:], func=ACT.Ln)
             if w + 1 < 2 * NC:
                 sum_matmuls(w + 1)
             elif w + 1 < NS:
                 sum_transposes(w + 1)
-            for p in due(w, 4, lag_exp):
-                exps(p)
-            if w in ex_at:
-                row_ex(ex_at[w])
-            subtract_rows(rows_a, "A")
             fill(w, 0)
             if 0 <= w - 1 < 2 * NC:
                 regroup(w - 1)
@@ -719,19 +750,18 @@ def tile_jointnet_t_kernel(
                 row_exp(exp0_at[w], 0)
             if w in exp1_at:
                 row_exp(exp1_at[w], 1)
-            if w in ln_at:
-                row_ln(ln_at[w])
             if 0 <= w - 2 < 2 * NC:
                 quantise_h(w - 2)
-            if 2 * NC <= w - 1 < NS:
+            if 2 * NC <= w - 1:
                 quantise_h(w - 1)
-            for p in due(w, 1, lag):
+            for p in due(w, logits_at):
                 logits(p)
             if w == 0:
                 repeat_enc(2)
                 repeat_enc(3)
             if w == 1:
                 dec_to_rows()
+                enc_row_matmuls(0)
                 enc_to_rows(0)
             if w == 2:
                 for i in range(TB):
@@ -739,22 +769,50 @@ def tile_jointnet_t_kernel(
                 load_dec(1)
             if w == 3:
                 dec_interleaved()
+                enc_feature_matmuls(0)
                 enc_interleaved(0)
             if w == 12:
-                enc_to_rows(1)
+                enc_row_matmuls(1)
             if w == 13:
+                enc_to_rows(1)
+                enc_feature_matmuls(1)
+            if w == 14:
                 enc_interleaved(1)
             if 26 <= w < 34 and w % 2 == 0:
                 load_enc(TB + w // 2 - 13)
             if w % 8 == 1 and 16 <= w + 7 < NS:
                 load_dec((w + 7) // 8)
             fill(w, 2)
-            subtract_rows(take(on_gpsimd), "G")
-            for p in due(w, 2, lag):
+            subtract_rows(take(3), "G")
+            for p in due(w, add_at):
                 bias_add(p)
-            fill(w, 3)
-            for p in due(w, 3, lag):
+            for p in due(w, max_at):
                 row_max(p)
-            subtract_rows(take(on_vector), "V")
+            fill(w, 3)
             stores()
+
+        row_ln(n_batches - 2)
+        quantise_h(NS - 1)
+        for p in due(NS, logits_at):
+            logits(p)
+        for p in due(NS, add_at):
+            bias_add(p)
+        for p in due(NS, max_at):
+            row_max(p)
+        for p in due(NS, exp_at):
+            exps(p)
+        for place in range(3):
+            fill(NS, place)
+        row_ex(n_batches - 1)
+        while len(ready) > taken[0]:
+            subtract_rows(take(4), "V")
+            stores()
+        fill(NS + 1, 0)
+        row_ln(n_batches - 1)
+        for place in range(3):
+            fill(NS + 2, place)
+        while len(ready) > taken[0]:
+            subtract_rows(take(1), "A")
+            subtract_rows(take(2), "V")
+        stores()
         assert taken[0] == ROWS and len(stored) == NB

@@ -22,8 +22,9 @@ NCH = 8
 TB, UG = T // 32, U // 16
 NB = B * TB * UG
 ROWS = 4 * NB
-BATCH_ROWS = [20, 20, 20, 20, 16, 8, 16, 8]
-ON_VECTOR = ({3}, {3}, {3}, {3})
+BATCH_ROWS = [24, 24, 24, 20, 8, 8, 12, 8]
+EXTRA = 5
+ON_VECTOR = ({1, 3},) + ({3},) * 7
 NC = 4
 
 FLOPS = 2 * (B * T * K1 * F + B * U * K1 * F + B * T * U * F * V)
@@ -45,7 +46,6 @@ def tile_jointnet_t_kernel(
         cd_pool = ctx.enter_context(tc.tile_pool(name="cd", bufs=5))
         small = ctx.enter_context(tc.tile_pool(name="small", bufs=3))
         junk_pool = ctx.enter_context(tc.tile_pool(name="junk", bufs=2))
-        tok_pool = ctx.enter_context(tc.tile_pool(name="tok", bufs=4))
 
         enc_c = const.tile([P, B * T], U32, name="enc_c", align_bytes=64)
         enc_s = const.tile([P, B * T], U8, name="enc_s", align_bytes=64)
@@ -262,7 +262,8 @@ def tile_jointnet_t_kernel(
                     op=ALU.add,
                 )
 
-        l_pool = ctx.enter_context(tc.tile_pool(name="l_pool", bufs=4))
+        l_pool = ctx.enter_context(tc.tile_pool(name="l_pool", bufs=3))
+        l_extra = ctx.enter_context(tc.tile_pool(name="l_extra", bufs=1))
         ps_lg = ctx.enter_context(tc.psum_pool(name="ps_lg", bufs=4))
 
         row0_of = [sum(BATCH_ROWS[:bi]) for bi in range(len(BATCH_ROWS))]
@@ -416,7 +417,7 @@ def tile_jointnet_t_kernel(
         def sum_transposes(s):
             b, ug, tb = place_of(s // 2)
             for x in range(4):
-                if x in ON_VECTOR[s % 4]:
+                if x in ON_VECTOR[s % 8]:
                     continue
                 m, g = 2 * (s % 2) + x // 2, x % 2
                 sums[s, x] = ps_cb.tile([P, 512], F32, name="sum")
@@ -438,7 +439,7 @@ def tile_jointnet_t_kernel(
         def sum_on_vector(s):
             b, ug, tb = place_of(s // 2)
             u0 = b * U + ug * 16
-            for x in sorted(ON_VECTOR[s % 4]):
+            for x in sorted(ON_VECTOR[s % 8]):
                 m = 2 * (s % 2) + x // 2
                 combs[s, x] = cb_pool.tile([P, 512], F32, name="comb")
                 nc.vector.tensor_tensor(
@@ -459,7 +460,7 @@ def tile_jointnet_t_kernel(
                 groupeds[s] = gr_pool.tile([P, 4 * 512], BF16, name="grouped", align_bytes=64)
             for x in units:
                 dst = groupeds[s][:, 512 * x : 512 * x + 512]
-                if x in ON_VECTOR[s % 4]:
+                if x in ON_VECTOR[s % 8]:
                     nc.scalar.activation(out=dst, in_=combs[s, x][:], func=ACT.Tanh)
                 else:
                     nc.scalar.activation(
@@ -473,7 +474,10 @@ def tile_jointnet_t_kernel(
             bi = batch_of_row[r]
             n = BATCH_ROWS[bi]
             if r == row0_of[bi]:
-                Ls[bi] = l_pool.tile([P, max(BATCH_ROWS), V], F32, name="L")
+                if bi == EXTRA:
+                    Ls[bi] = l_extra.tile([P, n, V], F32, name="L_extra")
+                else:
+                    Ls[bi] = l_pool.tile([P, max(BATCH_ROWS), V], F32, name="L")
                 negms[bi] = small.tile([P, n], F32, name="negm")
                 ssums[bi] = small.tile([P, n], F32, name="ssum")
                 misc[bi] = {}
@@ -485,13 +489,13 @@ def tile_jointnet_t_kernel(
                 op=ALU.add,
             )
 
-        def row_max(s):
-            r = 2 * s
+        def row_max(s, count=2):
+            r = 2 * s + 2 - count
             bi = batch_of_row[r]
             k = r - row0_of[bi]
             nc.vector.tensor_reduce(
-                out=negms[bi][:, k : k + 2],
-                in_=Ls[bi][:, k : k + 2, 1:V],
+                out=negms[bi][:, k : k + count],
+                in_=Ls[bi][:, k : k + count, 1:V],
                 axis=AX.X,
                 op=ALU.max,
                 negate=True,
@@ -608,6 +612,23 @@ def tile_jointnet_t_kernel(
                 in1=misc[bi]["mn"][:], op0=ALU.mult, op1=ALU.add,
             )
 
+        def row_last_o0(bi):
+            nc.vector.scalar_tensor_tensor(
+                out=blank(bi), in0=misc[bi]["y"][:, 0, :], scalar=misc[bi]["factor"],
+                in1=misc[bi]["mn"][:], op0=ALU.mult, op1=ALU.add,
+            )
+            rows_ready(bi)
+
+        def row_q(bi):
+            nc.vector.tensor_scalar_add(
+                out=row_tile(bi, "x", True)[:, 0, :], in0=misc[bi]["ex"][:], scalar1=1.0
+            )
+
+        def row_qs(bi):
+            nc.vector.tensor_tensor(
+                out=misc[bi]["x"][:, 1, :], in0=misc[bi]["x"][:, 0, :], in1=ssums[bi][:], op=ALU.mult
+            )
+
         def row_blank(bi):
             nc.vector.tensor_tensor(
                 out=blank(bi), in0=misc[bi]["o0"][:], in1=misc[bi]["negc"][:], op=ALU.subtract
@@ -633,19 +654,13 @@ def tile_jointnet_t_kernel(
             if not rows:
                 return
             bi = batch_of_row[rows[0]]
-            k0 = rows[0] - row0_of[bi]
             negc = misc[bi]["negc"]
-            if engine == "G":
-                tok = tok_pool.tile([P, 4], F32, name="tok")
-                nc.vector.tensor_copy(
-                    out=tok[:, 0 : len(rows)], in_=negc[:, k0 : k0 + len(rows)]
-                )
-            for i, r in enumerate(rows):
+            for r in rows:
                 k = r - row0_of[bi]
-                row = Ls[bi][:, k, :]
+                row = Ls[bi][:, k, 1:V] if bi == n_batches - 1 else Ls[bi][:, k, :]
                 if engine == "G":
                     nc.gpsimd.tensor_scalar(
-                        out=row, in0=row, scalar1=1.0, scalar2=tok[:, i : i + 1],
+                        out=row, in0=row, scalar1=1.0, scalar2=negc[:, k : k + 1],
                         op0=ALU.mult, op1=ALU.add,
                     )
                 elif engine == "A":
@@ -673,6 +688,8 @@ def tile_jointnet_t_kernel(
                         )
                     stored[r] = True
 
+        PAIRED = 52
+
         def lag(p):
             return 3 if p < 12 else 2 if p < 24 else 1 if p < 36 else 0
 
@@ -686,7 +703,7 @@ def tile_jointnet_t_kernel(
             return min(p + 3 + lag(p), NS)
 
         def exp_at(p):
-            return min(p + 4 + lag(p) + (2 if p < 44 else 1 if p < 52 else 0), NS)
+            return min(p + 4 + lag(p) + (2 if p < 44 else 1 if p < PAIRED else 0), NS)
 
         def due(w, at):
             return [p for p in range(NS) if at(p) == w]
@@ -712,10 +729,8 @@ def tile_jointnet_t_kernel(
                 plan += [(x + 5, 0, row_negc), (x + 5, 1, row_o0), (x + 5, 2, row_blank)]
             elif bi < n_batches - 1:
                 plan = [(a + 1, 0, row_nab), (a + 1, 1, row_mn), (a + 2, 2, row_t1), (x, 3, row_sq)]
-                plan += [(NS, 0, row_negc), (NS, 1, row_o0), (NS, 2, row_blank)]
             else:
-                plan = [(NS, 0, row_nab), (NS, 1, row_mn), (NS, 2, row_t1), (NS + 1, 0, row_sq)]
-                plan += [(NS + 2, 0, row_negc), (NS + 2, 1, row_o0), (NS + 2, 2, row_blank)]
+                plan = []
             for step, place, work in plan:
                 fillers.setdefault((step, place), []).append((work, bi))
 
@@ -783,36 +798,59 @@ def tile_jointnet_t_kernel(
             if w % 8 == 1 and 16 <= w + 7 < NS:
                 load_dec((w + 7) // 8)
             fill(w, 2)
-            subtract_rows(take(3), "G")
-            for p in due(w, add_at):
-                bias_add(p)
-            for p in due(w, max_at):
-                row_max(p)
-            fill(w, 3)
+            if w < NS - 1:
+                for p in due(w, add_at):
+                    bias_add(p)
+                fill(w, 3)
+                for p in due(w, max_at):
+                    if p >= PAIRED:
+                        row_max(p)
+                    elif p % 2 == 1:
+                        row_max(p, 4)
+                subtract_rows(take(3 if w < 55 else 4), "V")
+            else:
+                subtract_rows(take(4), "G")
+                row_max(NS - 4)
+                bias_add(NS - 3)
+                fill(w, 3)
             stores()
 
-        row_ln(n_batches - 2)
+        late, last = n_batches - 2, n_batches - 1
+        row_ln(late)
+        exps(NS - 4)
         quantise_h(NS - 1)
-        for p in due(NS, logits_at):
-            logits(p)
-        for p in due(NS, add_at):
-            bias_add(p)
-        for p in due(NS, max_at):
-            row_max(p)
-        for p in due(NS, exp_at):
-            exps(p)
-        for place in range(3):
-            fill(NS, place)
-        row_ex(n_batches - 1)
+        logits(NS - 1)
+        row_max(NS - 3)
+        exps(NS - 3)
         while len(ready) > taken[0]:
-            subtract_rows(take(4), "V")
-            stores()
-        fill(NS + 1, 0)
-        row_ln(n_batches - 1)
-        for place in range(3):
-            fill(NS + 2, place)
-        while len(ready) > taken[0]:
-            subtract_rows(take(1), "A")
-            subtract_rows(take(2), "V")
+            subtract_rows(take(2), "A")
+        bias_add(NS - 2)
+        row_negc(late)
+        row_o0(late)
+        row_blank(late)
+        subtract_rows(take(4), "G")
+        row_max(NS - 2)
+        bias_add(NS - 1)
+        row_nab(last)
+        row_max(NS - 1)
+        row_ex(last)
+        exps(NS - 2)
+        exps(NS - 1)
+        subtract_rows(take(4), "V")
+        stores()
+        row_mn(last)
+        row_t1(last)
+        row_q(last)
+        row_qs(last)
+        row_ln(last)
+        subtract_rows(take(2), "G")
+        subtract_rows(take(2), "A")
+        row_negc(last)
+        row_last_o0(last)
+        stores()
+        subtract_rows(take(4), "V")
+        stores()
+        subtract_rows(take(2), "V")
+        subtract_rows(take(2), "A")
         stores()
         assert taken[0] == ROWS and len(stored) == NB

import math
from contextlib import ExitStack

import concourse.mybir as mybir
from concourse.masks import make_identity

F32 = mybir.dt.float32
BF16 = mybir.dt.bfloat16
U32 = mybir.dt.uint32
I32 = mybir.dt.int32
U8 = mybir.dt.uint8
FP8X4 = mybir.dt.float8_e4m3fn_x4
ACT = mybir.ActivationFunctionType
ALU = mybir.AluOpType
AX = mybir.AxisListType

P = 128
LOG2E_STEP = math.log(2.0) / 2**23
LOG_SHIFT = -127.0 * math.log(2.0) + 0.0298
B, T, U, K1, F, V = 2, 128, 64, 512, 1024, 256
NCH = 8
TB, UG = T // 32, U // 16
NB = B * TB * UG
ROWS = 4 * NB
BATCH_ROWS = [24, 24, 24, 20, 8, 8, 12, 8]
EXTRA = 5
ON_VECTOR = ({1, 3},) + ({3},) * 7
NC = 4

FLOPS = 2 * (B * T * K1 * F + B * U * K1 * F + B * T * U * F * V)


def tile_jointnet_t_kernel(
    tc, encoder_output, decoder_output, W_enc, b_enc, W_dec, b_dec, W_fc, b_fc, out
):
    nc = tc.nc
    with ExitStack() as ctx:
        ctx.enter_context(tc.manual_schedule())
        const = ctx.enter_context(tc.tile_pool(name="const", bufs=1))
        ps_cb = ctx.enter_context(tc.psum_pool(name="ps_cb", bufs=4))
        hp_pool = ctx.enter_context(tc.tile_pool(name="hp", bufs=3))
        et_pool = ctx.enter_context(tc.tile_pool(name="et", bufs=4))
        dt_pool = ctx.enter_context(tc.tile_pool(name="dt", bufs=8))
        cb_pool = ctx.enter_context(tc.tile_pool(name="cb", bufs=4))
        gr_pool = ctx.enter_context(tc.tile_pool(name="gr", bufs=4))
        cd_pool = ctx.enter_context(tc.tile_pool(name="cd", bufs=5))
        small = ctx.enter_context(tc.tile_pool(name="small", bufs=3))
        junk_pool = ctx.enter_context(tc.tile_pool(name="junk", bufs=2))

        enc_c = const.tile([P, B * T], U32, name="enc_c", align_bytes=64)
        enc_s = const.tile([P, B * T], U8, name="enc_s", align_bytes=64)
        dec_c = const.tile([P, 64], U32, name="dec_c", align_bytes=64)
        dec_s = const.tile([P, 64], U8, name="dec_s", align_bytes=64)
        dec_1 = const.tile([P, B * U], U32, name="dec_1", align_bytes=64)
        dec_1s = const.tile([P, B * U], U8, name="dec_1s", align_bytes=64)
        enc_xc = const.tile([P, NC, 512], U32, name="enc_xc", align_bytes=64)
        enc_xs = const.tile([P, NC, 512], U8, name="enc_xs", align_bytes=64)
        dec_xc = const.tile([P, 1, 512], U32, name="dec_xc", align_bytes=64)
        dec_xs = const.tile([P, 1, 512], U8, name="dec_xs", align_bytes=64)
        wec = const.tile([P, NCH * P], U32, name="wec", align_bytes=64)
        wes = const.tile([P, NCH * P], U8, name="wes", align_bytes=64)
        wdc = const.tile([P, NCH * P], U32, name="wdc", align_bytes=64)
        wds = const.tile([P, NCH * P], U8, name="wds", align_bytes=64)
        wfc = const.tile([P, 4 * P], U32, name="wfc", align_bytes=64)
        wfs = const.tile([P, 4 * P], U8, name="wfs", align_bytes=64)
        enc_rows = const.tile([P, F], F32, name="enc_rows")
        dec_rows = const.tile([P, F], F32, name="dec_rows")
        bias_rows = const.tile([P, F], F32, name="bias_rows")
        enc_i = const.tile([P, B, 4 * T], F32, name="enc_i")
        dec_i = const.tile([P, B * U, 4], F32, name="dec_i")
        bsum = const.tile([P, NCH], F32, name="bsum")
        bfc = const.tile([P, V], F32, name="bfc")
        ident = const.tile([P, P], F32, name="ident")
        warm_in = const.tile([P, 1], F32, name="warm_in")
        one = const.tile([P, 1], F32, name="one")
        warm_out = const.tile([P, 1], F32, name="warm_out")

        def repeat_enc(i):
            nc.vector.tensor_copy(
                out=enc_xc[:, i, :].bitcast(I32).rearrange("p (r t) -> p r t", t=32),
                in_=enc_c[:, 32 * i : 32 * i + 32].bitcast(I32).unsqueeze(1).to_broadcast([P, 16, 32]),
            )
            nc.vector.tensor_copy(
                out=enc_xs[:, i, :].bitcast(I32).rearrange("p (r t) -> p r t", t=8),
                in_=enc_s[:, 32 * i : 32 * i + 32].bitcast(I32).unsqueeze(1).to_broadcast([P, 16, 8]),
            )

        def repeat_dec(i):
            codes = dec_c[:, 64 * i : 64 * i + 64].bitcast(I32)
            codes = codes.rearrange("p (uq m r) -> p m uq r", m=4, r=4)[:, :, :, 0:1]
            scales = dec_s[:, 64 * i : 64 * i + 64].bitcast(I32)
            scales = scales.rearrange("p (uq m) -> p m uq", m=4).unsqueeze(3)
            nc.vector.tensor_copy(
                out=dec_xc[:, i, :].bitcast(I32).rearrange("p (m uq t) -> p m uq t", m=4, t=32),
                in_=codes.to_broadcast([P, 4, 4, 32]),
            )
            nc.vector.tensor_copy(
                out=dec_xs[:, i, :].bitcast(I32).rearrange("p (m uq t) -> p m uq t", m=4, t=8),
                in_=scales.to_broadcast([P, 4, 4, 8]),
            )

        def place_of(n):
            return n // (UG * TB), n // TB % UG, n % TB

        HALVES = [(0, 0), (1, 0), (0, 1), (1, 1)] + [(n, g) for n in range(2, NC) for g in range(2)]
        NS = 2 * NB
        sums = {}

        def sum_matmuls(s):
            n, g = HALVES[s]
            b, d, e = place_of(n)
            for j in range(4):
                c = 4 * g + j
                cols = slice(c * P, (c + 1) * P)
                sums[s, j] = ps_cb.tile([P, 512], F32, name="sum")
                for wc, ws, xc, xs, first in (
                    (wec, wes, enc_xc[:, e, :], enc_xs[:, e, :], True),
                    (wdc, wds, dec_xc[:, d, :], dec_xs[:, d, :], False),
                ):
                    nc.tensor.matmul_mx(
                        out=sums[s, j][:],
                        lhsT=wc[:, cols].bitcast(FP8X4),
                        lhsT_scale=ws[:, cols],
                        rhs=xc.bitcast(FP8X4),
                        rhs_scale=xs,
                        start=first,
                        stop=not first,
                    )

        with tc.tile_pool(name="stage", bufs=1) as stage, tc.psum_pool(name="ps_tr", bufs=4) as ps_tr:
            benc_bf = stage.tile([P, NCH], BF16, name="benc_bf")
            bdec_bf = stage.tile([P, NCH], BF16, name="bdec_bf")
            bfc_bf = stage.tile([P, V], BF16, name="bfc_bf")
            with nc.allow_non_contiguous_dma(reason="bias vectors, 8-byte runs"):
                nc.scalar.dma_start(
                    out=benc_bf[:].rearrange("p (g j) -> p g j", g=2),
                    in_=b_enc.rearrange("(g p j) -> p g j", g=2, j=4),
                )
                nc.scalar.dma_start(
                    out=bdec_bf[:].rearrange("p (g j) -> p g j", g=2),
                    in_=b_dec.rearrange("(g p j) -> p g j", g=2, j=4),
                )
            benc_all = stage.tile([P, F], BF16, name="benc_all")
            bdec_all = stage.tile([P, F], BF16, name="bdec_all")
            enc_sb = stage.tile([P, B, K1], BF16, name="enc_sb")
            nc.sync.dma_start(out=enc_sb[:], in_=encoder_output.rearrange("b t k -> t b k"))
            dec_sb = stage.tile([P, K1], BF16, name="dec_sb")
            nc.sync.dma_start(out=dec_sb[:], in_=decoder_output.rearrange("b u k -> (b u) k"))
            wenc_sb = stage.tile([P, NCH, K1], BF16, name="wenc_sb")
            wdec_sb = stage.tile([P, NCH, K1], BF16, name="wdec_sb")
            for g in range(2):
                for w_sb, w in ((wenc_sb, W_enc), (wdec_sb, W_dec)):
                    nc.sync.dma_start(
                        out=w_sb[:, 4 * g : 4 * g + 4, :],
                        in_=w[512 * g : 512 * g + 512, :].rearrange("(p j) k -> p j k", j=4),
                    )
            wfc_sb = stage.tile([P, 2, F], BF16, name="wfc_sb")
            nc.sync.dma_start(out=wfc_sb[:], in_=W_fc.rearrange("(h v) k -> v h k", h=2))
            nc.sync.dma_start(out=bfc_bf[:], in_=b_fc.partition_broadcast(P))
            nc.sync.dma_start(out=benc_all[:], in_=b_enc.partition_broadcast(P))
            nc.sync.dma_start(out=bdec_all[:], in_=b_dec.partition_broadcast(P))

            make_identity(nc, ident[:])
            nc.gpsimd.memset(enc_s[:].bitcast(U32), 0)
            nc.gpsimd.memset(dec_s[:].bitcast(U32), 0)
            nc.vector.memset(warm_in[:], 0.0)
            nc.vector.memset(one[:], 1.0)
            nc.scalar.activation(out=warm_out[:], in_=warm_in[:], func=ACT.Tanh)

            eg = stage.tile([P, 2 * 512], BF16, name="eg", align_bytes=64)
            dg = stage.tile([P, 256], BF16, name="dg", align_bytes=64)
            d1 = stage.tile([P, 512], BF16, name="d1", align_bytes=64)
            weg = stage.tile([P, NCH * 512], BF16, name="weg", align_bytes=64)
            wdg = stage.tile([P, NCH * 512], BF16, name="wdg", align_bytes=64)
            wfg = stage.tile([P, 4 * 512], BF16, name="wfg", align_bytes=64)

            def halves(rows):
                w32 = rows.bitcast(F32)
                return [w32[:, 0:P], w32[:, P : 2 * P]]

            def transpose_in(views):
                tr = ps_tr.tile([P, 2, 2, P], F32, name="tr")
                for i in range(len(views)):
                    for u in range(2):
                        nc.tensor.transpose(tr[:, i, u, :], views[i][u], ident[:])
                return tr

            def copy_out(dst, src, on_scalar):
                if on_scalar:
                    nc.scalar.copy(out=dst, in_=src)
                else:
                    nc.vector.tensor_copy(out=dst, in_=src)

            def regrouped(tr, dst, on_scalar):
                n = dst.shape[1] // 512
                copy_out(
                    dst.bitcast(F32).rearrange("p (s r u) -> p s r u", s=n, u=2),
                    tr[:, 0:n, :, :].rearrange("p s u r -> p s r u"),
                    on_scalar,
                )

            def transpose_weights(w_sb, g):
                return [
                    (c, transpose_in([halves(w_sb[:, c, :]), halves(w_sb[:, c + 1, :])]))
                    for c in (4 * g, 4 * g + 2)
                ]

            def regroup_weights(trs, grouped, on_scalar):
                for c, tr in trs:
                    regrouped(tr, grouped[:, c * 512 : (c + 2) * 512], on_scalar)

            def quantise(grouped, codes, scales, first, count):
                nc.vector.quantize_mx(
                    out=codes[:, first * P : (first + count) * P].bitcast(FP8X4),
                    scales=scales[:, first * P : (first + count) * P],
                    in_=grouped[:, first * 512 : (first + count) * 512],
                )

            enc_tr = transpose_in([halves(enc_sb[:, 0, :]), halves(enc_sb[:, 1, :])])
            dec_tr = transpose_in([halves(dec_sb[:, :])])
            we_tr = transpose_weights(wenc_sb, 0)
            regrouped(enc_tr, eg[:], True)
            nc.scalar.copy(
                out=dg[:].bitcast(F32).rearrange("p (c r u) -> p c r u", r=4, u=2),
                in_=dec_tr[:, 0, :, 0:16].rearrange("p u c -> p c u").unsqueeze(2).to_broadcast([P, 16, 4, 2]),
            )
            regrouped(dec_tr, d1[:], False)
            wd_tr = transpose_weights(wdec_sb, 0)
            regroup_weights(we_tr, weg, True)
            nc.vector.tensor_tensor(out=bsum[:], in0=benc_bf[:], in1=bdec_bf[:], op=ALU.add)
            quantise(eg, enc_c, enc_s, 0, 2)
            nc.vector.quantize_mx(out=dec_c[:].bitcast(FP8X4), scales=dec_s[:], in_=dg[:])
            quantise(d1, dec_1, dec_1s, 0, 1)
            repeat_enc(0)
            repeat_dec(0)
            regroup_weights(wd_tr, wdg, False)
            for first in (0, 2):
                quantise(weg, wec, wes, first, 2)
                quantise(wdg, wdc, wds, first, 2)
            repeat_enc(1)
            we_tr = transpose_weights(wenc_sb, 1)
            wd_tr = transpose_weights(wdec_sb, 1)
            sum_matmuls(0)
            regroup_weights(we_tr, weg, False)
            regroup_weights(wd_tr, wdg, False)
            quantise(weg, wec, wes, 4, 4)
            quantise(wdg, wdc, wds, 4, 4)
            for g in range(2):
                views = []
                for h in range(2):
                    w32 = wfc_sb[:, h, :].bitcast(F32).rearrange("p (g w u) -> p g w u", g=2, u=2)
                    views.append([w32[:, g, :, 0], w32[:, g, :, 1]])
                fc_tr = transpose_in(views)
                regrouped(fc_tr, wfg[:, g * 1024 : (g + 1) * 1024], False)
            quantise(wfg, wfc, wfs, 0, 4)
            nc.vector.tensor_copy(out=bfc[:], in_=bfc_bf[:])
            for g in range(2):
                nc.vector.tensor_tensor(
                    out=bias_rows[:, 512 * g : 512 * g + 512].rearrange("p (j w) -> p j w", j=4),
                    in0=benc_all[:, 512 * g : 512 * g + 512].rearrange("p (w j) -> p j w", j=4),
                    in1=bdec_all[:, 512 * g : 512 * g + 512].rearrange("p (w j) -> p j w", j=4),
                    op=ALU.add,
                )

        l_pool = ctx.enter_context(tc.tile_pool(name="l_pool", bufs=3))
        l_extra = ctx.enter_context(tc.tile_pool(name="l_extra", bufs=1))
        ps_lg = ctx.enter_context(tc.psum_pool(name="ps_lg", bufs=4))

        row0_of = [sum(BATCH_ROWS[:bi]) for bi in range(len(BATCH_ROWS))]
        batch_of_row = []
        for bi, n in enumerate(BATCH_ROWS):
            batch_of_row.extend([bi] * n)
        n_batches = len(BATCH_ROWS)
        last_step_of = [(row0_of[bi] + BATCH_ROWS[bi]) // 2 - 1 for bi in range(n_batches)]
        hPs, groupeds, codes, lgs, combs, ets, dts = {}, {}, {}, {}, {}, {}, {}
        Ls, negms, ssums, misc = {}, {}, {}, {}
        row_banks, feature_banks = {}, {}

        def tanh_half(s):
            g = HALVES[s][1]
            hPs[s] = hp_pool.tile([P, 4, 512], BF16, name="hP")
            for j in range(4):
                nc.scalar.activation(
                    out=hPs[s][:, j, :],
                    in_=sums[s, j][:],
                    func=ACT.Tanh,
                    bias=bsum[:, 4 * g + j : 4 * g + j + 1],
                    scale=1.0,
                )

        def regroup(s):
            groupeds[s] = gr_pool.tile([P, 4 * 512], BF16, name="grouped", align_bytes=64)
            nc.vector.tensor_copy(
                out=groupeds[s][:].rearrange("p (c i j) -> p c j i", i=4, j=4),
                in_=hPs[s][:].rearrange("p j (c i) -> p c j i", i=4),
            )

        def quantise_h(s):
            words = cd_pool.tile([P, 512], U32, name="words", align_bytes=64)
            planes = cd_pool.tile([P, 512], U8, name="planes", align_bytes=64)
            nc.vector.quantize_mx(
                out=words[:].bitcast(FP8X4), scales=planes[:], in_=groupeds[s][:]
            )
            if s < 2 * NC:
                n, g = HALVES[s]
                for m in range(4):
                    codes[4 * n + m, g] = (words, planes, slice(m * P, (m + 1) * P))
            else:
                for x in range(4):
                    codes[2 * s + x // 2, x % 2] = (words, planes, slice(x * P, (x + 1) * P))

        def logits(s):
            lgs[s] = ps_lg.tile([P, 2, V], F32, name="lg")
            for q in range(2):
                for g in range(2):
                    words, planes, cols = codes[2 * s + q, g]
                    nc.tensor.matmul_mx(
                        out=lgs[s][:, q, :],
                        lhsT=words[:, cols].bitcast(FP8X4),
                        lhsT_scale=planes[:, cols],
                        rhs=wfc[:, g * V : (g + 1) * V].bitcast(FP8X4),
                        rhs_scale=wfs[:, g * V : (g + 1) * V],
                        start=(g == 0),
                        stop=(g == 1),
                    )

        def park(run0, slot):
            rows = out[1, run0 : run0 + 32, 48 + 4 * slot : 52 + 4 * slot, :]
            return rows.rearrange("t w v -> t (w v)")

        def park_enc(i):
            return park(32 + 32 * (i // 4), i % 4)

        def bank_matmul(dst, lhs, lhs_s, lcols, rhs, rhs_s, rcols):
            nc.tensor.matmul_mx(
                out=dst,
                lhsT=lhs[:, lcols].bitcast(FP8X4),
                lhsT_scale=lhs_s[:, lcols],
                rhs=rhs[:, rcols].bitcast(FP8X4),
                rhs_scale=rhs_s[:, rcols],
                start=True,
                stop=True,
            )

        def enc_row_matmuls(b):
            for g in range(2):
                bank = ps_lg.tile([P, 2, V], F32, name="lg")
                flat = bank[:].rearrange("p a v -> p (a v)")
                cols = slice(512 * g, 512 * g + 512)
                bank_matmul(flat, enc_c, enc_s, slice(b * T, (b + 1) * T), wec, wes, cols)
                row_banks[b, g] = flat

        def enc_to_rows(b):
            for g in range(2):
                nc.vector.tensor_copy(
                    out=enc_rows[:, 512 * g : 512 * g + 512], in_=row_banks[b, g]
                )
            for tb in range(TB):
                nc.sync.dma_start(
                    out=park_enc(TB * b + tb), in_=enc_rows[32 * tb : 32 * tb + 32, :]
                )

        def dec_to_rows():
            for g in range(2):
                bank = ps_lg.tile([P, 2, V], F32, name="lg")
                flat = bank[:].rearrange("p a v -> p (a v)")
                cols = slice(512 * g, 512 * g + 512)
                bank_matmul(flat, dec_1, dec_1s, slice(0, P), wdc, wds, cols)
                nc.vector.tensor_tensor(
                    out=dec_rows[:, cols], in0=flat, in1=bias_rows[:, cols], op=ALU.add
                )
            for i in range(4):
                nc.sync.dma_start(out=park(96, i), in_=dec_rows[32 * i : 32 * i + 32, :])

        def enc_feature_matmuls(b):
            bank = ps_lg.tile([P, 2, V], F32, name="lg")
            four = bank[:].rearrange("p a (c t) -> p (a c) t", c=2)
            for j in range(4):
                cols = slice((4 + j) * P, (5 + j) * P)
                bank_matmul(four[:, j, :], wec, wes, cols, enc_c, enc_s, slice(b * T, (b + 1) * T))
            feature_banks[b] = four

        def enc_interleaved(b):
            nc.vector.tensor_copy(
                out=enc_i[:, b, :].rearrange("p (t j) -> p t j", j=4),
                in_=feature_banks[b].rearrange("p j t -> p t j"),
            )

        def dec_interleaved():
            bank = ps_lg.tile([P, 2, V], F32, name="lg")
            four = bank[:].rearrange("p a (c t) -> p (a c) t", c=2)
            for j in range(4):
                cols = slice((4 + j) * P, (5 + j) * P)
                bank_matmul(four[:, j, :], wdc, wds, cols, dec_1, dec_1s, slice(0, P))
            nc.vector.tensor_tensor(
                out=dec_i[:],
                in0=four.rearrange("p j c -> p c j"),
                in1=bsum[:, 4:8].unsqueeze(1).to_broadcast([P, B * U, 4]),
                op=ALU.add,
            )

        def load_enc(i):
            ets[i] = et_pool.tile([P, F], F32, name="et")
            for uq in range(4):
                nc.sync.dma_start(out=ets[i][32 * uq : 32 * uq + 32, :], in_=park_enc(i))

        def load_dec(i):
            for m in range(4):
                dts[i, m] = dt_pool.tile([P, F], F32, name="dt")
                for uq in range(4):
                    row = 16 * i + 4 * uq + m
                    src = park(96, row // 32)[row % 32, :]
                    nc.sync.dma_start(
                        out=dts[i, m][32 * uq : 32 * uq + 32, :], in_=src.partition_broadcast(32)
                    )

        def sum_transposes(s):
            b, ug, tb = place_of(s // 2)
            for x in range(4):
                if x in ON_VECTOR[s % 8]:
                    continue
                m, g = 2 * (s % 2) + x // 2, x % 2
                sums[s, x] = ps_cb.tile([P, 512], F32, name="sum")
                for j in range(4):
                    cols = slice((4 * g + j) * P, (4 * g + j + 1) * P)
                    for src, begins in (
                        (ets[TB * b + tb][:, cols], True),
                        (dts[UG * b + ug, m][:, cols], False),
                    ):
                        nc.tensor.matmul(
                            out=sums[s, x][:, j * P : (j + 1) * P],
                            lhsT=src,
                            rhs=ident[:],
                            start=begins,
                            stop=not begins,
                            is_transpose=True,
                        )

        def sum_on_vector(s):
            b, ug, tb = place_of(s // 2)
            u0 = b * U + ug * 16
            for x in sorted(ON_VECTOR[s % 8]):
                m = 2 * (s % 2) + x // 2
                combs[s, x] = cb_pool.tile([P, 512], F32, name="comb")
                nc.vector.tensor_tensor(
                    out=combs[s, x][:].rearrange("p (q t j) -> p q t j", q=4, j=4),
                    in0=enc_i[:, b, 128 * tb : 128 * tb + 128]
                    .rearrange("p (t j) -> p t j", j=4)
                    .unsqueeze(1)
                    .to_broadcast([P, 4, 32, 4]),
                    in1=dec_i[:, u0 : u0 + 16, :]
                    .rearrange("p (q m) j -> p m q j", m=4)[:, m, :, :]
                    .unsqueeze(2)
                    .to_broadcast([P, 4, 32, 4]),
                    op=ALU.add,
                )

        def tanh_units(s, units):
            if 0 in units:
                groupeds[s] = gr_pool.tile([P, 4 * 512], BF16, name="grouped", align_bytes=64)
            for x in units:
                dst = groupeds[s][:, 512 * x : 512 * x + 512]
                if x in ON_VECTOR[s % 8]:
                    nc.scalar.activation(out=dst, in_=combs[s, x][:], func=ACT.Tanh)
                else:
                    nc.scalar.activation(
                        out=dst.rearrange("p (t j) -> p t j", j=4),
                        in_=sums[s, x][:].rearrange("p (j t) -> p t j", j=4),
                        func=ACT.Tanh,
                    )

        def bias_add(s):
            r = 2 * s
            bi = batch_of_row[r]
            n = BATCH_ROWS[bi]
            if r == row0_of[bi]:
                if bi == EXTRA:
                    Ls[bi] = l_extra.tile([P, n, V], F32, name="L_extra")
                else:
                    Ls[bi] = l_pool.tile([P, max(BATCH_ROWS), V], F32, name="L")
                negms[bi] = small.tile([P, n], F32, name="negm")
                ssums[bi] = small.tile([P, n], F32, name="ssum")
                misc[bi] = {}
            k = r - row0_of[bi]
            nc.vector.tensor_tensor(
                out=Ls[bi][:, k : k + 2, :],
                in0=lgs[s][:],
                in1=bfc[:].unsqueeze(1).to_broadcast([P, 2, V]),
                op=ALU.add,
            )

        def row_max(s, count=2):
            r = 2 * s + 2 - count
            bi = batch_of_row[r]
            k = r - row0_of[bi]
            nc.vector.tensor_reduce(
                out=negms[bi][:, k : k + count],
                in_=Ls[bi][:, k : k + count, 1:V],
                axis=AX.X,
                op=ALU.max,
                negate=True,
            )

        def exps(s):
            r = 2 * s
            bi = batch_of_row[r]
            k = r - row0_of[bi]
            for q in range(2):
                junk = junk_pool.tile([P, V], BF16, name="junk")
                nc.scalar.activation(
                    out=junk[:, 1:V],
                    in_=Ls[bi][:, k + q, 1:V],
                    func=ACT.Exp,
                    bias=negms[bi][:, k + q : k + q + 1],
                    scale=1.0,
                    accum_out=ssums[bi][:, k + q : k + q + 1],
                )

        def row_tile(bi, name, pair=False):
            n = BATCH_ROWS[bi]
            shape = [P, 2, n] if pair else [P, n]
            misc[bi][name] = small.tile(shape, F32, name=name)
            return misc[bi][name]

        def blank(bi):
            return Ls[bi][:, 0 : BATCH_ROWS[bi], 0]

        def row_mn(bi):
            nc.vector.tensor_scalar_min(out=row_tile(bi, "mn")[:], in0=blank(bi), scalar1=0.0)

        def row_nab(bi):
            nc.vector.scalar_tensor_tensor(
                out=row_tile(bi, "nab")[:], in0=blank(bi), scalar=-1.0, in1=blank(bi),
                op0=ALU.mult, op1=ALU.min,
            )

        def row_t1(bi):
            nc.vector.scalar_tensor_tensor(
                out=row_tile(bi, "t1")[:], in0=blank(bi), scalar=0.0, in1=negms[bi][:],
                op0=ALU.max, op1=ALU.subtract,
            )

        def row_ex(bi):
            nc.scalar.activation(out=row_tile(bi, "ex")[:], in_=misc[bi]["nab"][:], func=ACT.Exp)

        def row_sq(bi):
            x = row_tile(bi, "x", True)
            nc.vector.tensor_scalar_add(out=x[:, 0, :], in0=misc[bi]["ex"][:], scalar1=1.0)
            nc.vector.scalar_tensor_tensor(
                out=x[:, 1, :], in0=misc[bi]["ex"][:], scalar=1.0, in1=ssums[bi][:],
                op0=ALU.add, op1=ALU.mult,
            )

        def row_v0(bi):
            nc.vector.tensor_scalar(
                out=row_tile(bi, "v0", True)[:],
                in0=misc[bi]["x"][:].bitcast(I32),
                scalar1=3.0 * LOG2E_STEP, scalar2=3.0 * LOG_SHIFT, op0=ALU.mult, op1=ALU.add,
            )

        def row_exp(bi, i):
            nc.scalar.activation(
                out=row_tile(bi, "e%d" % i, True)[:], in_=misc[bi]["v%d" % i][:],
                func=ACT.Exp, scale=-1.0 / 3.0,
            )

        def row_w(bi, i):
            nc.vector.tensor_tensor(
                out=row_tile(bi, "w%d" % i, True)[:], in0=misc[bi]["x"][:],
                in1=misc[bi]["e%d" % i][:], op=ALU.mult,
            )

        def row_u(bi, i):
            w = misc[bi]["w%d" % i]
            nc.vector.scalar_tensor_tensor(
                out=row_tile(bi, "u%d" % i, True)[:], in0=w[:], scalar=-4.5, in1=w[:],
                op0=ALU.add, op1=ALU.mult,
            )

        def row_t(bi, i):
            nc.vector.scalar_tensor_tensor(
                out=row_tile(bi, "t%d" % (i + 2), True)[:], in0=misc[bi]["u%d" % i][:],
                scalar=9.0, in1=misc[bi]["w%d" % i][:], op0=ALU.add, op1=ALU.mult,
            )

        def row_v(bi, i):
            nc.vector.scalar_tensor_tensor(
                out=row_tile(bi, "v%d" % (i + 1), True)[:], in0=misc[bi]["t%d" % (i + 2)][:],
                scalar=-5.5, in1=misc[bi]["v%d" % i][:], op0=ALU.add, op1=ALU.add,
            )
            misc[bi]["y"] = misc[bi]["v%d" % (i + 1)]
            misc[bi]["factor"] = -1.0 / 3.0

        def rows_ready(bi):
            ready.extend(range(row0_of[bi], row0_of[bi] + BATCH_ROWS[bi]))

        def row_ln(bi):
            nc.scalar.activation(
                out=row_tile(bi, "y", True)[:], in_=misc[bi]["x"][:], func=ACT.Ln
            )
            misc[bi]["factor"] = -1.0

        def row_negc(bi):
            nc.vector.scalar_tensor_tensor(
                out=row_tile(bi, "negc")[:], in0=misc[bi]["y"][:, 1, :], scalar=misc[bi]["factor"],
                in1=misc[bi]["t1"][:], op0=ALU.mult, op1=ALU.subtract,
            )

        def row_o0(bi):
            nc.vector.scalar_tensor_tensor(
                out=row_tile(bi, "o0")[:], in0=misc[bi]["y"][:, 0, :], scalar=misc[bi]["factor"],
                in1=misc[bi]["mn"][:], op0=ALU.mult, op1=ALU.add,
            )

        def row_last_o0(bi):
            nc.vector.scalar_tensor_tensor(
                out=blank(bi), in0=misc[bi]["y"][:, 0, :], scalar=misc[bi]["factor"],
                in1=misc[bi]["mn"][:], op0=ALU.mult, op1=ALU.add,
            )
            rows_ready(bi)

        def row_q(bi):
            nc.vector.tensor_scalar_add(
                out=row_tile(bi, "x", True)[:, 0, :], in0=misc[bi]["ex"][:], scalar1=1.0
            )

        def row_qs(bi):
            nc.vector.tensor_tensor(
                out=misc[bi]["x"][:, 1, :], in0=misc[bi]["x"][:, 0, :], in1=ssums[bi][:], op=ALU.mult
            )

        def row_blank(bi):
            nc.vector.tensor_tensor(
                out=blank(bi), in0=misc[bi]["o0"][:], in1=misc[bi]["negc"][:], op=ALU.subtract
            )
            rows_ready(bi)

        ready = []
        taken = [0]
        done_rows = {}
        stored = {}

        def take(count):
            got = []
            while taken[0] < len(ready) and len(got) < count:
                r = ready[taken[0]]
                if got and batch_of_row[r] != batch_of_row[got[0]]:
                    break
                got.append(r)
                taken[0] += 1
            return got

        def subtract_rows(rows, engine):
            if not rows:
                return
            bi = batch_of_row[rows[0]]
            negc = misc[bi]["negc"]
            for r in rows:
                k = r - row0_of[bi]
                row = Ls[bi][:, k, 1:V] if bi == n_batches - 1 else Ls[bi][:, k, :]
                if engine == "G":
                    nc.gpsimd.tensor_scalar(
                        out=row, in0=row, scalar1=1.0, scalar2=negc[:, k : k + 1],
                        op0=ALU.mult, op1=ALU.add,
                    )
                elif engine == "A":
                    nc.scalar.activation(
                        out=row, in_=row, func=ACT.Identity, bias=negc[:, k : k + 1], scale=1.0
                    )
                else:
                    nc.vector.tensor_scalar(
                        out=row, in0=row, scalar1=negc[:, k : k + 1], scalar2=None, op0=ALU.add
                    )
                done_rows[r] = True

        def stores():
            for n in range(NB):
                r = 4 * n
                if r not in stored and all((r + i) in done_rows for i in range(4)):
                    bi = batch_of_row[r]
                    k = r - row0_of[bi]
                    b, ug, tb = place_of(n)
                    t0, u0 = 32 * tb, 16 * ug
                    for uq in range(4):
                        nc.sync.dma_start(
                            out=out[b, t0 : t0 + 32, u0 + 4 * uq : u0 + 4 * uq + 4, :],
                            in_=Ls[bi][32 * uq : 32 * uq + 32, k : k + 4, :],
                        )
                    stored[r] = True

        PAIRED = 52

        def lag(p):
            return 3 if p < 12 else 2 if p < 24 else 1 if p < 36 else 0

        def logits_at(p):
            return p + 1 + lag(p)

        def add_at(p):
            return min(p + 2 + lag(p), NS)

        def max_at(p):
            return min(p + 3 + lag(p), NS)

        def exp_at(p):
            return min(p + 4 + lag(p) + (2 if p < 44 else 1 if p < PAIRED else 0), NS)

        def due(w, at):
            return [p for p in range(NS) if at(p) == w]

        def first(work):
            return lambda bi: work(bi, 0)

        def second(work):
            return lambda bi: work(bi, 1)

        fillers = {}
        ex_at, exp0_at, exp1_at = {}, {}, {}
        for bi in range(n_batches):
            e = last_step_of[bi]
            a, x = add_at(e), exp_at(e)
            ex_at[x] = bi
            if bi < n_batches - 2:
                exp0_at[x + 1], exp1_at[x + 3] = bi, bi
                plan = [(a + 1, 0, row_mn), (a + 1, 1, row_nab), (a + 2, 1, row_t1), (x + 1, 0, row_sq)]
                plan += [(x + 1, 1, row_v0), (x + 2, 0, first(row_w)), (x + 2, 1, first(row_u))]
                plan += [(x + 2, 2, first(row_t)), (x + 2, 3, first(row_v)), (x + 4, 0, second(row_w))]
                plan += [(x + 4, 1, second(row_u)), (x + 4, 2, second(row_t)), (x + 4, 3, second(row_v))]
                plan += [(x + 5, 0, row_negc), (x + 5, 1, row_o0), (x + 5, 2, row_blank)]
            elif bi < n_batches - 1:
                plan = [(a + 1, 0, row_nab), (a + 1, 1, row_mn), (a + 2, 2, row_t1), (x, 3, row_sq)]
            else:
                plan = []
            for step, place, work in plan:
                fillers.setdefault((step, place), []).append((work, bi))

        def fill(w, place):
            for work, bi in fillers.get((w, place), []):
                work(bi)

        for w in range(NS):
            if w < 2 * NC:
                tanh_half(w)
            else:
                tanh_units(w, (0, 1))
            for p in due(w, exp_at):
                exps(p)
            if w in ex_at:
                row_ex(ex_at[w])
            if w >= 2 * NC:
                tanh_units(w, (2, 3))
            if w == NS - 1:
                nc.scalar.activation(out=warm_out[:], in_=one[:], func=ACT.Ln)
            if w + 1 < 2 * NC:
                sum_matmuls(w + 1)
            elif w + 1 < NS:
                sum_transposes(w + 1)
            fill(w, 0)
            if 0 <= w - 1 < 2 * NC:
                regroup(w - 1)
            if 2 * NC <= w + 1 < NS:
                sum_on_vector(w + 1)
            fill(w, 1)
            if w in exp0_at:
                row_exp(exp0_at[w], 0)
            if w in exp1_at:
                row_exp(exp1_at[w], 1)
            if 0 <= w - 2 < 2 * NC:
                quantise_h(w - 2)
            if 2 * NC <= w - 1:
                quantise_h(w - 1)
            for p in due(w, logits_at):
                logits(p)
            if w == 0:
                repeat_enc(2)
                repeat_enc(3)
            if w == 1:
                dec_to_rows()
                enc_row_matmuls(0)
                enc_to_rows(0)
            if w == 2:
                for i in range(TB):
                    load_enc(i)
                load_dec(1)
            if w == 3:
                dec_interleaved()
                enc_feature_matmuls(0)
                enc_interleaved(0)
            if w == 12:
                enc_row_matmuls(1)
            if w == 13:
                enc_to_rows(1)
                enc_feature_matmuls(1)
            if w == 14:
                enc_interleaved(1)
            if 26 <= w < 34 and w % 2 == 0:
                load_enc(TB + w // 2 - 13)
            if w % 8 == 1 and 16 <= w + 7 < NS:
                load_dec((w + 7) // 8)
            fill(w, 2)
            if w < NS - 1:
                for p in due(w, add_at):
                    bias_add(p)
                fill(w, 3)
                for p in due(w, max_at):
                    if p >= PAIRED:
                        row_max(p)
                    elif p % 2 == 1:
                        row_max(p, 4)
                subtract_rows(take(3 if w < 55 else 4), "V")
            else:
                subtract_rows(take(4), "G")
                row_max(NS - 4)
                bias_add(NS - 3)
                fill(w, 3)
            stores()

        late, last = n_batches - 2, n_batches - 1
        row_ln(late)
        exps(NS - 4)
        quantise_h(NS - 1)
        logits(NS - 1)
        row_max(NS - 3)
        exps(NS - 3)
        while len(ready) > taken[0]:
            subtract_rows(take(2), "A")
        bias_add(NS - 2)
        row_negc(late)
        row_o0(late)
        row_blank(late)
        subtract_rows(take(4), "G")
        row_max(NS - 2)
        bias_add(NS - 1)
        row_nab(last)
        row_max(NS - 1)
        row_ex(last)
        exps(NS - 2)
        exps(NS - 1)
        subtract_rows(take(4), "V")
        stores()
        row_mn(last)
        row_t1(last)
        row_q(last)
        row_qs(last)
        row_ln(last)
        subtract_rows(take(2), "G")
        subtract_rows(take(2), "A")
        row_negc(last)
        row_last_o0(last)
        stores()
        subtract_rows(take(4), "V")
        stores()
        subtract_rows(take(2), "V")
        subtract_rows(take(2), "A")
        stores()
        assert taken[0] == ROWS and len(stored) == NB
